import numpy as np
import ml_dtypes


def mxq(x, axis, fmt="e4m3"):
    dtype, down = {"e4m3": (ml_dtypes.float8_e4m3fn, 7), "e5m2": (ml_dtypes.float8_e5m2, 14)}[fmt]
    v = np.moveaxis(np.asarray(x, np.float32).astype(ml_dtypes.bfloat16).astype(np.float64), axis, -1)
    blocks = v.reshape(v.shape[:-1] + (-1, 32))
    amax = np.abs(blocks).max(-1, keepdims=True)
    byte = np.maximum(np.where(amax > 0, np.frexp(amax)[1] - 1 + 127, 0) - down, 1)
    scale = np.exp2(byte - 127.0)
    codes = (blocks / scale).astype(np.float32).astype(dtype).astype(np.float64)
    return np.moveaxis((codes * scale).reshape(v.shape), -1, axis)


WIDE = False


def mx_kscale(k):
    if not WIDE:
        return np.ones(k)
    levels = np.array([10, -10, 5, -5, 0])
    a = np.random.permutation(np.resize(levels, k // 512 * 4)).reshape(k // 512, 4)
    idx = np.arange(k)
    return np.exp2(a[idx // 512, idx % 128 // 32])


BF16 = ml_dtypes.bfloat16


def bf(x):
    return np.asarray(x, np.float32).astype(BF16)


def f64(x):
    return np.asarray(x).astype(np.float64)


N, C, F, O, DEG = 2048, 512, 512, 40, 16


def draw_adj():
    hit = (np.random.random((N, N)) < 0.5 * DEG / N).astype(np.float64)
    wt = 0.5 + np.random.random((N, N))
    return np.clip(hit + hit.T + np.eye(N), 0.0, 1.0) * (wt + wt.T) * 0.5


def setup_inputs():
    t = mx_kscale(F)
    return {"h": bf(np.maximum(np.random.standard_normal((N, F)) * 3.4, 0.0) * t),
            "adj": bf(draw_adj()),
            "w": bf(np.random.standard_normal((F, F)) * 0.5 * DEG / np.sqrt(F) / t[:, None]),
            "rw": bf(np.random.standard_normal((F, F)) * 0.5 / np.sqrt(F) / t[:, None]),
            "b": bf(np.random.standard_normal(F) * 0.3)}


def reference(h, adj, w, rw, b):
    h, adj = f64(h), f64(adj)
    deg = np.sum(adj, axis=1)
    dis = deg ** -0.5
    norm_adj = dis[:, None] * adj * dis[None, :]
    nnz = np.maximum(np.sum(np.where(adj > 0.0, 1.0, 0.0), axis=1), 1.0)
    agg = (mxq(norm_adj, 1, "e4m3") @ mxq(h, 0, "e4m3")) / nnz[:, None]
    y = (mxq(agg, 1, "e4m3") @ mxq(f64(w), 0, "e4m3")) + (mxq(h, 1, "e4m3") @ mxq(f64(rw), 0, "e4m3")) + f64(b)
    return np.maximum(y, 0.0)

@@ -1,0 +1,320 @@
+from contextlib import ExitStack
+
+import concourse.mybir as mybir
+from concourse.masks import make_identity
+
+F32 = mybir.dt.float32
+BF16 = mybir.dt.bfloat16
+U32 = mybir.dt.uint32
+U8 = mybir.dt.uint8
+FP8X4 = mybir.dt.float8_e4m3fn_x4
+ALU = mybir.AluOpType
+ACT = mybir.ActivationFunctionType
+AXIS = mybir.AxisListType
+
+P = 128
+PACK = 4
+K_PASS = P * PACK
+NODES = 2048
+FEAT = 512
+ROW_TILES = NODES // P
+NODE_PASSES = NODES // K_PASS
+
+FLOPS = 2 * NODES * NODES * FEAT + 2 * 2 * NODES * FEAT * FEAT
+
+
+def quantise(nc, grouped, codes, scales):
+    nc.vector.quantize_mx(out=codes.bitcast(FP8X4), scales=scales, in_=grouped)
+
+
+def mx_pass(nc, acc, stat_codes, stat_scales, mov_codes, mov_scales, start, stop):
+    nc.tensor.matmul_mx(
+        out=acc,
+        lhsT=stat_codes.bitcast(FP8X4),
+        lhsT_scale=stat_scales,
+        rhs=mov_codes.bitcast(FP8X4),
+        rhs_scale=mov_scales,
+        start=start,
+        stop=stop,
+    )
+
+
+def tile_sage_re_pb_kernel(tc, h, adj, w, rw, b, out):
+    nc = tc.nc
+    with ExitStack() as stack:
+        keep = stack.enter_context(tc.tile_pool(name="keep", bufs=1))
+        stage = stack.enter_context(tc.tile_pool(name="stage", bufs=3))
+        work = stack.enter_context(tc.tile_pool(name="work", bufs=2))
+        psum_sums = stack.enter_context(tc.psum_pool(name="psum_sums", bufs=1))
+        psum_turn = stack.enter_context(tc.psum_pool(name="psum_turn", bufs=3))
+        psum_acc = stack.enter_context(tc.psum_pool(name="psum_acc", bufs=2))
+
+        ident = keep.tile([P, P], F32)
+        make_identity(nc, ident[:])
+        ones = keep.tile([P, 1], BF16)
+        nc.vector.memset(ones[:], 1.0)
+
+        h_rows = keep.tile([P, ROW_TILES, FEAT], BF16)
+        h_view = h.rearrange("(g q e) f -> q g e f", q=P, e=2)
+        for c in range(NODE_PASSES):
+            nc.sync.dma_start(
+                out=h_rows[:, PACK * c : PACK * (c + 1), :].rearrange("q (u e) f -> q u e f", e=2),
+                in_=h_view[:, 2 * c : 2 * (c + 1), :, :],
+            )
+        adj_rows = keep.tile([P, ROW_TILES, NODES], BF16)
+        for r in range(ROW_TILES):
+            nc.sync.dma_start(out=adj_rows[:, r, :], in_=adj[P * r : P * (r + 1), :])
+        weight_raw = {}
+        for name, weight in (("rw", rw), ("w", w)):
+            raw = keep.tile([P, PACK, FEAT], BF16, name="raw_" + name)
+            nc.sync.dma_start(
+                out=raw[:].rearrange("q (u e) o -> q u e o", e=2),
+                in_=weight.rearrange("(u q e) o -> q u e o", q=P, e=2),
+            )
+            weight_raw[name] = raw
+        bias = keep.tile([P, FEAT], BF16)
+        nc.sync.dma_start(out=bias[:], in_=b.partition_broadcast(P))
+
+        hn_codes = keep.tile([P, NODE_PASSES, FEAT], U32, align_bytes=64)
+        hn_scales = keep.tile([P, NODE_PASSES, FEAT], U8, align_bytes=64)
+        for c in range(NODE_PASSES):
+            grouped = stage.tile([P, FEAT * PACK], BF16, align_bytes=64, tag="grouped")
+            nc.scalar.copy(
+                out=grouped[:].rearrange("q (f t) -> q f t", t=PACK),
+                in_=h_rows[:, PACK * c : PACK * (c + 1), :].rearrange("q t f -> q f t"),
+            )
+            quantise(nc, grouped[:], hn_codes[:, c, :], hn_scales[:, c, :])
+
+        hf_codes = keep.tile([P, NODES], U32, align_bytes=64)
+        hf_scales = keep.tile([P, NODES], U8, align_bytes=64)
+        for c in range(NODE_PASSES):
+            grouped = stage.tile([P, K_PASS * PACK], BF16, align_bytes=64, tag="grouped")
+            grouped_words = grouped[:].bitcast(F32).rearrange(
+                "q (g p e u) -> q g p e u", g=2, e=2, u=2
+            )
+            for g in range(2):
+                turned = psum_turn.tile([P, PACK, P], F32, tag="turned")
+                for e in range(2):
+                    row_words = h_rows[:, PACK * c + 2 * g + e, :].bitcast(F32)
+                    for u in range(2):
+                        nc.tensor.transpose(
+                            out=turned[:, 2 * e + u, :],
+                            in_=row_words[:, P * u : P * (u + 1)],
+                            identity=ident[:],
+                        )
+                nc.scalar.copy(
+                    out=grouped_words[:, g, :, :, :],
+                    in_=turned[:].rearrange("q (e u) p -> q p e u", u=2),
+                )
+            cols = slice(K_PASS * c, K_PASS * (c + 1))
+            quantise(nc, grouped[:], hf_codes[:, cols], hf_scales[:, cols])
+
+        nnz = keep.tile([P, ROW_TILES], F32)
+        deg_parts = psum_sums.tile([P, ROW_TILES, ROW_TILES], F32)
+        for r in range(ROW_TILES):
+            positive = stage.tile([P, NODES], BF16, tag="positive")
+            nc.vector.tensor_scalar(
+                out=positive[:],
+                in0=adj_rows[:, r, :],
+                scalar1=0.0,
+                scalar2=None,
+                op0=ALU.is_gt,
+                op1=ALU.add,
+                accum_out=nnz[:, r : r + 1],
+            )
+            for s in range(ROW_TILES):
+                nc.tensor.matmul(
+                    out=deg_parts[:, s, r : r + 1],
+                    lhsT=adj_rows[:, r, P * s : P * (s + 1)],
+                    rhs=ones[:],
+                    start=True,
+                    stop=True,
+                )
+
+        deg = keep.tile([P, ROW_TILES], F32)
+        nc.vector.tensor_reduce(out=deg[:], in_=deg_parts[:], axis=AXIS.X, op=ALU.add)
+        root = keep.tile([P, ROW_TILES], F32)
+        nc.scalar.sqrt(out=root[:], in_=deg[:])
+        dis = keep.tile([P, ROW_TILES], F32)
+        nc.vector.reciprocal(out=dis[:], in_=root[:])
+
+        dis_row = keep.tile([P, NODES], F32)
+        for c in range(NODE_PASSES):
+            spread = psum_turn.tile([P, PACK, P], F32, tag="turned")
+            for k in range(PACK):
+                s = PACK * c + k
+                nc.tensor.matmul(
+                    out=spread[:, k, :],
+                    lhsT=dis[:, s : s + 1].to_broadcast([P, P]),
+                    rhs=ident[:],
+                    start=True,
+                    stop=True,
+                )
+            nc.scalar.copy(
+                out=dis_row[:, K_PASS * c : K_PASS * (c + 1)],
+                in_=spread[:].rearrange("p k n -> p (k n)"),
+            )
+
+        nnz_floor = keep.tile([P, ROW_TILES], F32)
+        nc.vector.tensor_scalar_max(out=nnz_floor[:], in0=nnz[:], scalar1=1.0)
+        inv_nnz = keep.tile([P, ROW_TILES], F32)
+        nc.vector.reciprocal(out=inv_nnz[:], in_=nnz_floor[:])
+
+        weight_codes = {}
+        weight_scales = {}
+        for name in ("rw", "w"):
+            grouped = stage.tile([P, FEAT * PACK], BF16, align_bytes=64, tag="grouped")
+            nc.vector.tensor_copy(
+                out=grouped[:].rearrange("q (o t) -> q o t", t=PACK),
+                in_=weight_raw[name][:].rearrange("q t o -> q o t"),
+            )
+            codes = keep.tile([P, FEAT], U32, align_bytes=64, name="codes_" + name)
+            scales = keep.tile([P, FEAT], U8, align_bytes=64, name="scales_" + name)
+            quantise(nc, grouped[:], codes[:], scales[:])
+            weight_codes[name] = codes
+            weight_scales[name] = scales
+
+        norm_of = {}
+        norm_grouped_of = {}
+        norm_mx_of = {}
+        agg_of = {}
+        agg_grouped_of = {}
+        agg_mx_of = {}
+        both_of = {}
+
+        def scale_rows(r):
+            norm = work.tile([P, NODES], BF16, tag="norm")
+            nc.vector.scalar_tensor_tensor(
+                out=norm[:],
+                in0=adj_rows[:, r, :],
+                scalar=dis[:, r : r + 1],
+                in1=dis_row[:],
+                op0=ALU.mult,
+                op1=ALU.mult,
+            )
+            norm_of[r] = norm
+
+        def turn_norm(r):
+            norm_words = norm_of[r][:].bitcast(F32)
+            grouped = work.tile([P, NODES], BF16, align_bytes=64, tag="norm_grouped")
+            grouped_words = grouped[:].bitcast(F32).rearrange(
+                "q (c i u) -> q c i u", c=NODE_PASSES, u=2
+            )
+            for half in range(2):
+                turned = psum_turn.tile([P, PACK, P], F32, tag="turned")
+                for k in range(PACK):
+                    first = P * (PACK * half + k)
+                    nc.tensor.transpose(
+                        out=turned[:, k, :],
+                        in_=norm_words[:, first : first + P],
+                        identity=ident[:],
+                    )
+                nc.scalar.copy(
+                    out=grouped_words[:, 2 * half : 2 * (half + 1), :, :],
+                    in_=turned[:].rearrange("q (c u) i -> q c i u", u=2),
+                )
+            norm_grouped_of[r] = grouped
+
+        def quantise_norm(r):
+            codes = work.tile([P, NODE_PASSES, P], U32, align_bytes=64, tag="norm_codes")
+            scales = work.tile([P, NODE_PASSES, P], U8, align_bytes=64, tag="norm_scales")
+            quantise(
+                nc,
+                norm_grouped_of[r][:],
+                codes[:].rearrange("q c i -> q (c i)"),
+                scales[:].rearrange("q c i -> q (c i)"),
+            )
+            norm_mx_of[r] = (codes, scales)
+
+        def aggregate(r):
+            codes, scales = norm_mx_of[r]
+            neighbours = psum_acc.tile([P, FEAT], F32, tag="neighbours", bufs=1)
+            for c in range(NODE_PASSES):
+                mx_pass(
+                    nc,
+                    neighbours[:],
+                    codes[:, c, :],
+                    scales[:, c, :],
+                    hn_codes[:, c, :],
+                    hn_scales[:, c, :],
+                    start=(c == 0),
+                    stop=(c == NODE_PASSES - 1),
+                )
+            agg = work.tile([P, FEAT], BF16, tag="agg")
+            nc.scalar.activation(
+                out=agg[:], in_=neighbours[:], func=ACT.Copy, scale=inv_nnz[:, r : r + 1]
+            )
+            agg_of[r] = agg
+
+        def turn_agg(r):
+            agg_words = agg_of[r][:].bitcast(F32)
+            turned = psum_turn.tile([P, 2, P], F32, tag="turned")
+            for u in range(2):
+                nc.tensor.transpose(
+                    out=turned[:, u, :], in_=agg_words[:, P * u : P * (u + 1)], identity=ident[:]
+                )
+            grouped = work.tile([P, P * PACK], BF16, align_bytes=64, tag="agg_grouped")
+            nc.scalar.copy(
+                out=grouped[:].bitcast(F32).rearrange("q (i u) -> q i u", u=2),
+                in_=turned[:].rearrange("q u i -> q i u"),
+            )
+            agg_grouped_of[r] = grouped
+
+        def quantise_agg(r):
+            codes = work.tile([P, P], U32, align_bytes=64, tag="agg_codes")
+            scales = work.tile([P, P], U8, align_bytes=64, tag="agg_scales")
+            quantise(nc, agg_grouped_of[r][:], codes[:], scales[:])
+            agg_mx_of[r] = (codes, scales)
+
+        def combine(r):
+            codes, scales = agg_mx_of[r]
+            nodes = slice(P * r, P * (r + 1))
+            both = psum_acc.tile([P, FEAT], F32, tag="both")
+            mx_pass(
+                nc,
+                both[:],
+                hf_codes[:, nodes],
+                hf_scales[:, nodes],
+                weight_codes["rw"][:],
+                weight_scales["rw"][:],
+                start=True,
+                stop=False,
+            )
+            mx_pass(
+                nc,
+                both[:],
+                codes[:],
+                scales[:],
+                weight_codes["w"][:],
+                weight_scales["w"][:],
+                start=False,
+                stop=True,
+            )
+            both_of[r] = both
+
+        def finish(r):
+            biased = work.tile([P, FEAT], F32, tag="biased")
+            nc.vector.tensor_tensor(out=biased[:], in0=both_of[r][:], in1=bias[:], op=ALU.add)
+            result = work.tile([P, FEAT], F32, tag="result")
+            nc.scalar.activation(out=result[:], in_=biased[:], func=ACT.Relu)
+            nc.sync.dma_start(out=out[P * r : P * (r + 1), :], in_=result[:])
+
+        def in_range(r):
+            return 0 <= r < ROW_TILES
+
+        with tc.manual_schedule():
+            for n in range(ROW_TILES + 3):
+                if in_range(n):
+                    scale_rows(n)
+                if in_range(n - 2):
+                    turn_agg(n - 2)
+                if in_range(n):
+                    turn_norm(n)
+                if in_range(n - 1):
+                    quantise_norm(n - 1)
+                    aggregate(n - 1)
+                if in_range(n - 2):
+                    quantise_agg(n - 2)
+                    combine(n - 2)
+                if in_range(n - 3):
+                    finish(n - 3)

@@ -53,6 +53,8 @@ def tile_sage_re_pb_kernel(tc, h, adj, w, rw, b, out):
         make_identity(nc, ident[:])
         ones = keep.tile([P, 1], BF16)
         nc.vector.memset(ones[:], 1.0)
+        warm = keep.tile([P, 1], F32)
+        nc.scalar.sqrt(out=warm[:], in_=ones[:])
 
         h_rows = keep.tile([P, ROW_TILES, FEAT], BF16)
         h_view = h.rearrange("(g q e) f -> q g e f", q=P, e=2)
@@ -77,18 +79,21 @@ def tile_sage_re_pb_kernel(tc, h, adj, w, rw, b, out):
 
         hn_codes = keep.tile([P, NODE_PASSES, FEAT], U32, align_bytes=64)
         hn_scales = keep.tile([P, NODE_PASSES, FEAT], U8, align_bytes=64)
-        for c in range(NODE_PASSES):
-            grouped = stage.tile([P, FEAT * PACK], BF16, align_bytes=64, tag="grouped")
+        hf_codes = keep.tile([P, NODES], U32, align_bytes=64)
+        hf_scales = keep.tile([P, NODES], U8, align_bytes=64)
+        hn_grouped_of = {}
+        hf_grouped_of = {}
+
+        def group_h_by_nodes(c):
+            grouped = stage.tile([P, FEAT * PACK], BF16, align_bytes=64, tag="grouped", bufs=4)
             nc.scalar.copy(
                 out=grouped[:].rearrange("q (f t) -> q f t", t=PACK),
                 in_=h_rows[:, PACK * c : PACK * (c + 1), :].rearrange("q t f -> q f t"),
             )
-            quantise(nc, grouped[:], hn_codes[:, c, :], hn_scales[:, c, :])
+            hn_grouped_of[c] = grouped
 
-        hf_codes = keep.tile([P, NODES], U32, align_bytes=64)
-        hf_scales = keep.tile([P, NODES], U8, align_bytes=64)
-        for c in range(NODE_PASSES):
-            grouped = stage.tile([P, K_PASS * PACK], BF16, align_bytes=64, tag="grouped")
+        def group_h_by_features(c):
+            grouped = stage.tile([P, K_PASS * PACK], BF16, align_bytes=64, tag="grouped", bufs=4)
             grouped_words = grouped[:].bitcast(F32).rearrange(
                 "q (g p e u) -> q g p e u", g=2, e=2, u=2
             )
@@ -106,12 +111,17 @@ def tile_sage_re_pb_kernel(tc, h, adj, w, rw, b, out):
                     out=grouped_words[:, g, :, :, :],
                     in_=turned[:].rearrange("q (e u) p -> q p e u", u=2),
                 )
+            hf_grouped_of[c] = grouped
+
+        def quantise_h(c):
+            quantise(nc, hn_grouped_of[c][:], hn_codes[:, c, :], hn_scales[:, c, :])
             cols = slice(K_PASS * c, K_PASS * (c + 1))
-            quantise(nc, grouped[:], hf_codes[:, cols], hf_scales[:, cols])
+            quantise(nc, hf_grouped_of[c][:], hf_codes[:, cols], hf_scales[:, cols])
 
         nnz = keep.tile([P, ROW_TILES], F32)
         deg_parts = psum_sums.tile([P, ROW_TILES, ROW_TILES], F32)
-        for r in range(ROW_TILES):
+
+        def count_and_sum(r):
             positive = stage.tile([P, NODES], BF16, tag="positive")
             nc.vector.tensor_scalar(
                 out=positive[:],
@@ -132,38 +142,39 @@ def tile_sage_re_pb_kernel(tc, h, adj, w, rw, b, out):
                 )
 
         deg = keep.tile([P, ROW_TILES], F32)
-        nc.vector.tensor_reduce(out=deg[:], in_=deg_parts[:], axis=AXIS.X, op=ALU.add)
         root = keep.tile([P, ROW_TILES], F32)
-        nc.scalar.sqrt(out=root[:], in_=deg[:])
         dis = keep.tile([P, ROW_TILES], F32)
-        nc.vector.reciprocal(out=dis[:], in_=root[:])
-
-        dis_row = keep.tile([P, NODES], F32)
-        for c in range(NODE_PASSES):
-            spread = psum_turn.tile([P, PACK, P], F32, tag="turned")
-            for k in range(PACK):
-                s = PACK * c + k
-                nc.tensor.matmul(
-                    out=spread[:, k, :],
-                    lhsT=dis[:, s : s + 1].to_broadcast([P, P]),
-                    rhs=ident[:],
-                    start=True,
-                    stop=True,
-                )
-            nc.scalar.copy(
-                out=dis_row[:, K_PASS * c : K_PASS * (c + 1)],
-                in_=spread[:].rearrange("p k n -> p (k n)"),
-            )
-
         nnz_floor = keep.tile([P, ROW_TILES], F32)
-        nc.vector.tensor_scalar_max(out=nnz_floor[:], in0=nnz[:], scalar1=1.0)
         inv_nnz = keep.tile([P, ROW_TILES], F32)
-        nc.vector.reciprocal(out=inv_nnz[:], in_=nnz_floor[:])
+        dis_row = keep.tile([P, NODES], F32)
+
+        def make_dis():
+            nc.vector.tensor_reduce(out=deg[:], in_=deg_parts[:], axis=AXIS.X, op=ALU.add)
+            nc.scalar.sqrt(out=root[:], in_=deg[:])
+            nc.vector.reciprocal(out=dis[:], in_=root[:])
+            for c in range(NODE_PASSES):
+                spread = psum_turn.tile([P, PACK, P], F32, tag="turned")
+                for k in range(PACK):
+                    s = PACK * c + k
+                    nc.tensor.transpose(
+                        out=spread[:, k, :],
+                        in_=dis[:, s : s + 1].to_broadcast([P, P]),
+                        identity=ident[:],
+                    )
+                nc.scalar.copy(
+                    out=dis_row[:, K_PASS * c : K_PASS * (c + 1)],
+                    in_=spread[:].rearrange("p k n -> p (k n)"),
+                )
+
+        def make_inv_nnz():
+            nc.vector.tensor_scalar_max(out=nnz_floor[:], in0=nnz[:], scalar1=1.0)
+            nc.vector.reciprocal(out=inv_nnz[:], in_=nnz_floor[:])
 
         weight_codes = {}
         weight_scales = {}
-        for name in ("rw", "w"):
-            grouped = stage.tile([P, FEAT * PACK], BF16, align_bytes=64, tag="grouped")
+
+        def quantise_weight(name):
+            grouped = stage.tile([P, FEAT * PACK], BF16, align_bytes=64, tag="grouped", bufs=4)
             nc.vector.tensor_copy(
                 out=grouped[:].rearrange("q (o t) -> q o t", t=PACK),
                 in_=weight_raw[name][:].rearrange("q t o -> q o t"),
@@ -303,6 +314,17 @@ def tile_sage_re_pb_kernel(tc, h, adj, w, rw, b, out):
             return 0 <= r < ROW_TILES
 
         with tc.manual_schedule():
+            for c in range(NODE_PASSES):
+                group_h_by_nodes(c)
+                group_h_by_features(c)
+                for r in range(PACK * c, PACK * (c + 1)):
+                    count_and_sum(r)
+                quantise_h(c)
+            make_dis()
+            quantise_weight("rw")
+            quantise_weight("w")
+            make_inv_nnz()
+
             for n in range(ROW_TILES + 3):
                 if in_range(n):
                     scale_rows(n)

@@ -18,7 +18,9 @@ K_PASS = P * PACK
 NODES = 2048
 FEAT = 512
 ROW_TILES = NODES // P
-NODE_PASSES = NODES // K_PASS
+CHUNKS = NODES // K_PASS
+GROUP = 2 * P
+GROUPS = NODES // GROUP
 
 FLOPS = 2 * NODES * NODES * FEAT + 2 * 2 * NODES * FEAT * FEAT
 
@@ -43,29 +45,36 @@ def tile_sage_re_pb_kernel(tc, h, adj, w, rw, b, out):
     nc = tc.nc
     with ExitStack() as stack:
         keep = stack.enter_context(tc.tile_pool(name="keep", bufs=1))
-        stage = stack.enter_context(tc.tile_pool(name="stage", bufs=3))
+        stage = stack.enter_context(tc.tile_pool(name="stage", bufs=2))
         work = stack.enter_context(tc.tile_pool(name="work", bufs=2))
-        psum_sums = stack.enter_context(tc.psum_pool(name="psum_sums", bufs=1))
-        psum_turn = stack.enter_context(tc.psum_pool(name="psum_turn", bufs=3))
+        psum_turn = stack.enter_context(tc.psum_pool(name="psum_turn", bufs=4))
         psum_acc = stack.enter_context(tc.psum_pool(name="psum_acc", bufs=2))
 
         ident = keep.tile([P, P], F32)
         make_identity(nc, ident[:])
         ones = keep.tile([P, 1], BF16)
         nc.vector.memset(ones[:], 1.0)
+        pick = keep.tile([P, 2, 2, P], F32)
+        nc.vector.memset(pick[:], 0.0)
+        for half in range(2):
+            for e in range(2):
+                nc.vector.tensor_copy(
+                    out=pick[:, half, e, e::2], in_=ident[:, P // 2 * half : P // 2 * (half + 1)]
+                )
         warm = keep.tile([P, 1], F32)
         nc.scalar.sqrt(out=warm[:], in_=ones[:])
 
         h_rows = keep.tile([P, ROW_TILES, FEAT], BF16)
         h_view = h.rearrange("(g q e) f -> q g e f", q=P, e=2)
-        for c in range(NODE_PASSES):
+        for c in range(CHUNKS):
             nc.sync.dma_start(
                 out=h_rows[:, PACK * c : PACK * (c + 1), :].rearrange("q (u e) f -> q u e f", e=2),
                 in_=h_view[:, 2 * c : 2 * (c + 1), :, :],
             )
         adj_rows = keep.tile([P, ROW_TILES, NODES], BF16)
-        for r in range(ROW_TILES):
-            nc.sync.dma_start(out=adj_rows[:, r, :], in_=adj[P * r : P * (r + 1), :])
+        adj_view = adj.rearrange("(g q e) n -> q g e n", q=P, e=2)
+        for slot in range(ROW_TILES):
+            nc.sync.dma_start(out=adj_rows[:, slot, :], in_=adj_view[:, slot // 2, slot % 2, :])
         weight_raw = {}
         for name, weight in (("rw", rw), ("w", w)):
             raw = keep.tile([P, PACK, FEAT], BF16, name="raw_" + name)
@@ -77,15 +86,18 @@ def tile_sage_re_pb_kernel(tc, h, adj, w, rw, b, out):
         bias = keep.tile([P, FEAT], BF16)
         nc.sync.dma_start(out=bias[:], in_=b.partition_broadcast(P))
 
-        hn_codes = keep.tile([P, NODE_PASSES, FEAT], U32, align_bytes=64)
-        hn_scales = keep.tile([P, NODE_PASSES, FEAT], U8, align_bytes=64)
+        hn_codes = keep.tile([P, CHUNKS, FEAT], U32, align_bytes=64)
+        hn_scales = keep.tile([P, CHUNKS, FEAT], U8, align_bytes=64)
         hf_codes = keep.tile([P, NODES], U32, align_bytes=64)
         hf_scales = keep.tile([P, NODES], U8, align_bytes=64)
         hn_grouped_of = {}
         hf_grouped_of = {}
 
+        def new_grouped(width):
+            return stage.tile([P, width], BF16, align_bytes=64, tag="grouped", bufs=GROUPS, name="grouped")
+
         def group_h_by_nodes(c):
-            grouped = stage.tile([P, FEAT * PACK], BF16, align_bytes=64, tag="grouped", bufs=4)
+            grouped = new_grouped(FEAT * PACK)
             nc.scalar.copy(
                 out=grouped[:].rearrange("q (f t) -> q f t", t=PACK),
                 in_=h_rows[:, PACK * c : PACK * (c + 1), :].rearrange("q t f -> q f t"),
@@ -93,7 +105,7 @@ def tile_sage_re_pb_kernel(tc, h, adj, w, rw, b, out):
             hn_grouped_of[c] = grouped
 
         def group_h_by_features(c):
-            grouped = stage.tile([P, K_PASS * PACK], BF16, align_bytes=64, tag="grouped", bufs=4)
+            grouped = new_grouped(K_PASS * PACK)
             grouped_words = grouped[:].bitcast(F32).rearrange(
                 "q (g p e u) -> q g p e u", g=2, e=2, u=2
             )
@@ -118,24 +130,36 @@ def tile_sage_re_pb_kernel(tc, h, adj, w, rw, b, out):
             cols = slice(K_PASS * c, K_PASS * (c + 1))
             quantise(nc, hf_grouped_of[c][:], hf_codes[:, cols], hf_scales[:, cols])
 
-        nnz = keep.tile([P, ROW_TILES], F32)
-        deg_parts = psum_sums.tile([P, ROW_TILES, ROW_TILES], F32)
+        row_count = keep.tile([P, ROW_TILES], F32)
+        deg_parts = psum_acc.tile([P, ROW_TILES, ROW_TILES], F32, tag="both", bufs=2)
+        mirror_parts = psum_acc.tile([P, ROW_TILES - PACK, ROW_TILES - PACK], F32, tag="neighbours", bufs=2)
 
-        def count_and_sum(r):
+        def count_and_sum(slot):
+            chunk = slot // PACK
+            first = K_PASS * chunk
             positive = stage.tile([P, NODES], BF16, tag="positive")
             nc.vector.tensor_scalar(
-                out=positive[:],
-                in0=adj_rows[:, r, :],
+                out=positive[:, first:],
+                in0=adj_rows[:, slot, first:],
                 scalar1=0.0,
                 scalar2=None,
                 op0=ALU.is_gt,
                 op1=ALU.add,
-                accum_out=nnz[:, r : r + 1],
+                accum_out=row_count[:, slot : slot + 1],
             )
             for s in range(ROW_TILES):
+                g, e = divmod(s, 2)
                 nc.tensor.matmul(
-                    out=deg_parts[:, s, r : r + 1],
-                    lhsT=adj_rows[:, r, P * s : P * (s + 1)],
+                    out=deg_parts[:, s, slot : slot + 1],
+                    lhsT=adj_rows[:, slot, GROUP * g + e : GROUP * (g + 1) : 2],
+                    rhs=ones[:],
+                    start=True,
+                    stop=True,
+                )
+            for s in range(PACK * (chunk + 1), ROW_TILES):
+                nc.tensor.matmul(
+                    out=mirror_parts[:, s - PACK, slot : slot + 1],
+                    lhsT=positive[:, P * s : P * (s + 1)],
                     rhs=ones[:],
                     start=True,
                     stop=True,
@@ -144,15 +168,13 @@ def tile_sage_re_pb_kernel(tc, h, adj, w, rw, b, out):
         deg = keep.tile([P, ROW_TILES], F32)
         root = keep.tile([P, ROW_TILES], F32)
         dis = keep.tile([P, ROW_TILES], F32)
-        nnz_floor = keep.tile([P, ROW_TILES], F32)
-        inv_nnz = keep.tile([P, ROW_TILES], F32)
         dis_row = keep.tile([P, NODES], F32)
 
         def make_dis():
             nc.vector.tensor_reduce(out=deg[:], in_=deg_parts[:], axis=AXIS.X, op=ALU.add)
             nc.scalar.sqrt(out=root[:], in_=deg[:])
             nc.vector.reciprocal(out=dis[:], in_=root[:])
-            for c in range(NODE_PASSES):
+            for c in range(CHUNKS):
                 spread = psum_turn.tile([P, PACK, P], F32, tag="turned")
                 for k in range(PACK):
                     s = PACK * c + k
@@ -162,181 +184,259 @@ def tile_sage_re_pb_kernel(tc, h, adj, w, rw, b, out):
                         identity=ident[:],
                     )
                 nc.scalar.copy(
-                    out=dis_row[:, K_PASS * c : K_PASS * (c + 1)],
-                    in_=spread[:].rearrange("p k n -> p (k n)"),
+                    out=dis_row[:, K_PASS * c : K_PASS * (c + 1)].rearrange(
+                        "p (u n e) -> p u n e", u=2, e=2
+                    ),
+                    in_=spread[:].rearrange("p (u e) n -> p u n e", e=2),
                 )
 
-        def make_inv_nnz():
-            nc.vector.tensor_scalar_max(out=nnz_floor[:], in0=nnz[:], scalar1=1.0)
-            nc.vector.reciprocal(out=inv_nnz[:], in_=nnz_floor[:])
+        nnz = keep.tile([P, ROW_TILES], F32)
+        mirror = keep.tile([P, ROW_TILES - PACK], F32)
+        inv_nnz = keep.tile([P, ROW_TILES], F32)
 
+        def make_inv_nnz():
+            moved = psum_turn.tile([P, 2, GROUPS], F32, tag="turned")
+            for half in range(2):
+                for e in range(2):
+                    nc.tensor.matmul(
+                        out=moved[:, half, :],
+                        lhsT=pick[:, half, e, :],
+                        rhs=row_count[:, e::2],
+                        start=(e == 0),
+                        stop=(e == 1),
+                    )
+            nc.vector.tensor_copy(
+                out=nnz[:].rearrange("p (g half) -> p g half", half=2),
+                in_=moved[:].rearrange("p half g -> p g half"),
+            )
+            for chunk in range(1, CHUNKS):
+                tiles = slice(PACK * (chunk - 1), PACK * chunk)
+                nc.vector.tensor_reduce(
+                    out=mirror[:, tiles],
+                    in_=mirror_parts[:, tiles, : PACK * chunk],
+                    axis=AXIS.X,
+                    op=ALU.add,
+                )
+            nc.vector.tensor_tensor(
+                out=nnz[:, PACK:], in0=nnz[:, PACK:], in1=mirror[:], op=ALU.add
+            )
+            nc.vector.tensor_scalar_max(out=nnz[:], in0=nnz[:], scalar1=1.0)
+            nc.vector.reciprocal(out=inv_nnz[:], in_=nnz[:])
+
+        weight_grouped = {}
         weight_codes = {}
         weight_scales = {}
 
-        def quantise_weight(name):
-            grouped = stage.tile([P, FEAT * PACK], BF16, align_bytes=64, tag="grouped", bufs=4)
-            nc.vector.tensor_copy(
+        def group_weight(name):
+            grouped = new_grouped(FEAT * PACK)
+            nc.scalar.copy(
                 out=grouped[:].rearrange("q (o t) -> q o t", t=PACK),
                 in_=weight_raw[name][:].rearrange("q t o -> q o t"),
             )
+            weight_grouped[name] = grouped
+
+        def quantise_weight(name):
+            grouped = weight_grouped[name]
             codes = keep.tile([P, FEAT], U32, align_bytes=64, name="codes_" + name)
             scales = keep.tile([P, FEAT], U8, align_bytes=64, name="scales_" + name)
             quantise(nc, grouped[:], codes[:], scales[:])
             weight_codes[name] = codes
             weight_scales[name] = scales
 
-        norm_of = {}
-        norm_grouped_of = {}
+        grouped_of = {}
         norm_mx_of = {}
         agg_of = {}
         agg_grouped_of = {}
         agg_mx_of = {}
         both_of = {}
 
-        def scale_rows(r):
-            norm = work.tile([P, NODES], BF16, tag="norm")
+        def grouped_norm(g):
+            if g not in grouped_of:
+                grouped_of[g] = new_grouped(CHUNKS * GROUP * PACK)
+            return grouped_of[g][:].rearrange("q (c i t) -> q c i t", c=CHUNKS, t=PACK)
+
+        def scale_row(slot, first_chunk=None, last_chunk=CHUNKS):
+            first = K_PASS * (slot // PACK if first_chunk is None else first_chunk)
+            last = K_PASS * last_chunk
             nc.vector.scalar_tensor_tensor(
-                out=norm[:],
-                in0=adj_rows[:, r, :],
-                scalar=dis[:, r : r + 1],
-                in1=dis_row[:],
+                out=adj_rows[:, slot, first:last],
+                in0=adj_rows[:, slot, first:last],
+                scalar=dis[:, slot : slot + 1],
+                in1=dis_row[:, first:last],
                 op0=ALU.mult,
                 op1=ALU.mult,
             )
-            norm_of[r] = norm
 
-        def turn_norm(r):
-            norm_words = norm_of[r][:].bitcast(F32)
-            grouped = work.tile([P, NODES], BF16, align_bytes=64, tag="norm_grouped")
-            grouped_words = grouped[:].bitcast(F32).rearrange(
-                "q (c i u) -> q c i u", c=NODE_PASSES, u=2
-            )
-            for half in range(2):
+        def turn_norm(g):
+            grouped_norm(g)
+            for c in range(g // 2, CHUNKS):
                 turned = psum_turn.tile([P, PACK, P], F32, tag="turned")
-                for k in range(PACK):
-                    first = P * (PACK * half + k)
-                    nc.tensor.transpose(
-                        out=turned[:, k, :],
-                        in_=norm_words[:, first : first + P],
-                        identity=ident[:],
-                    )
+                for e in range(2):
+                    words = adj_rows[:, 2 * g + e, K_PASS * c : K_PASS * (c + 1)].bitcast(F32)
+                    for u in range(2):
+                        nc.tensor.transpose(
+                            out=turned[:, 2 * e + u, :],
+                            in_=words[:, P * u : P * (u + 1)],
+                            identity=ident[:],
+                        )
+                span = GROUP * PACK // 2
                 nc.scalar.copy(
-                    out=grouped_words[:, 2 * half : 2 * (half + 1), :, :],
-                    in_=turned[:].rearrange("q (c u) i -> q c i u", u=2),
+                    out=grouped_of[g][:].bitcast(F32)[:, span * c : span * (c + 1)].rearrange(
+                        "q (p e u) -> q p e u", e=2, u=2
+                    ),
+                    in_=turned[:].rearrange("q (e u) p -> q p e u", u=2),
                 )
-            norm_grouped_of[r] = grouped
 
-        def quantise_norm(r):
-            codes = work.tile([P, NODE_PASSES, P], U32, align_bytes=64, tag="norm_codes")
-            scales = work.tile([P, NODE_PASSES, P], U8, align_bytes=64, tag="norm_scales")
+        def mirror_norm(engine_copy, c, g):
+            engine_copy(
+                out=grouped_norm(g)[:, c, :, :],
+                in_=adj_rows[:, PACK * c : PACK * (c + 1), GROUP * g : GROUP * (g + 1)].rearrange(
+                    "q t i -> q i t"
+                ),
+            )
+
+        def quantise_norm(g):
+            codes = work.tile([P, CHUNKS, GROUP], U32, align_bytes=64, tag="norm_codes")
+            scales = work.tile([P, CHUNKS, GROUP], U8, align_bytes=64, tag="norm_scales")
             quantise(
                 nc,
-                norm_grouped_of[r][:],
+                grouped_of[g][:],
                 codes[:].rearrange("q c i -> q (c i)"),
                 scales[:].rearrange("q c i -> q (c i)"),
             )
-            norm_mx_of[r] = (codes, scales)
+            norm_mx_of[g] = (codes, scales)
 
-        def aggregate(r):
-            codes, scales = norm_mx_of[r]
-            neighbours = psum_acc.tile([P, FEAT], F32, tag="neighbours", bufs=1)
-            for c in range(NODE_PASSES):
+        def aggregate(g):
+            codes, scales = norm_mx_of[g]
+            agg = work.tile([P, 2, FEAT], BF16, tag="agg")
+            for half in range(2):
+                cols = slice(P * half, P * (half + 1))
+                neighbours = psum_acc.tile([P, FEAT], F32, tag="neighbours", bufs=2)
+                for c in range(CHUNKS):
+                    mx_pass(
+                        nc,
+                        neighbours[:],
+                        codes[:, c, cols],
+                        scales[:, c, cols],
+                        hn_codes[:, c, :],
+                        hn_scales[:, c, :],
+                        start=(c == 0),
+                        stop=(c == CHUNKS - 1),
+                    )
+                tile = 2 * g + half
+                nc.scalar.activation(
+                    out=agg[:, half, :],
+                    in_=neighbours[:],
+                    func=ACT.Copy,
+                    scale=inv_nnz[:, tile : tile + 1],
+                )
+            agg_of[g] = agg
+
+        def turn_agg(g):
+            turned = psum_turn.tile([P, PACK, P], F32, tag="turned")
+            for half in range(2):
+                words = agg_of[g][:, half, :].bitcast(F32)
+                for u in range(2):
+                    nc.tensor.transpose(
+                        out=turned[:, 2 * half + u, :],
+                        in_=words[:, P * u : P * (u + 1)],
+                        identity=ident[:],
+                    )
+            grouped = work.tile([P, GROUP * PACK], BF16, align_bytes=64, tag="agg_grouped")
+            nc.scalar.copy(
+                out=grouped[:].bitcast(F32).rearrange("q (half i u) -> q half i u", half=2, u=2),
+                in_=turned[:].rearrange("q (half u) i -> q half i u", u=2),
+            )
+            agg_grouped_of[g] = grouped
+
+        def quantise_agg(g):
+            codes = work.tile([P, GROUP], U32, align_bytes=64, tag="agg_codes")
+            scales = work.tile([P, GROUP], U8, align_bytes=64, tag="agg_scales")
+            quantise(nc, agg_grouped_of[g][:], codes[:], scales[:])
+            agg_mx_of[g] = (codes, scales)
+
+        def combine(g):
+            codes, scales = agg_mx_of[g]
+            for half in range(2):
+                tile = 2 * g + half
+                nodes = slice(P * tile, P * (tile + 1))
+                cols = slice(P * half, P * (half + 1))
+                both = psum_acc.tile([P, FEAT], F32, tag="both", bufs=2)
                 mx_pass(
                     nc,
-                    neighbours[:],
-                    codes[:, c, :],
-                    scales[:, c, :],
-                    hn_codes[:, c, :],
-                    hn_scales[:, c, :],
-                    start=(c == 0),
-                    stop=(c == NODE_PASSES - 1),
+                    both[:],
+                    hf_codes[:, nodes],
+                    hf_scales[:, nodes],
+                    weight_codes["rw"][:],
+                    weight_scales["rw"][:],
+                    start=True,
+                    stop=False,
                 )
-            agg = work.tile([P, FEAT], BF16, tag="agg")
-            nc.scalar.activation(
-                out=agg[:], in_=neighbours[:], func=ACT.Copy, scale=inv_nnz[:, r : r + 1]
-            )
-            agg_of[r] = agg
-
-        def turn_agg(r):
-            agg_words = agg_of[r][:].bitcast(F32)
-            turned = psum_turn.tile([P, 2, P], F32, tag="turned")
-            for u in range(2):
-                nc.tensor.transpose(
-                    out=turned[:, u, :], in_=agg_words[:, P * u : P * (u + 1)], identity=ident[:]
+                mx_pass(
+                    nc,
+                    both[:],
+                    codes[:, cols],
+                    scales[:, cols],
+                    weight_codes["w"][:],
+                    weight_scales["w"][:],
+                    start=False,
+                    stop=True,
                 )
-            grouped = work.tile([P, P * PACK], BF16, align_bytes=64, tag="agg_grouped")
-            nc.scalar.copy(
-                out=grouped[:].bitcast(F32).rearrange("q (i u) -> q i u", u=2),
-                in_=turned[:].rearrange("q u i -> q i u"),
-            )
-            agg_grouped_of[r] = grouped
+                both_of[tile] = both
 
-        def quantise_agg(r):
-            codes = work.tile([P, P], U32, align_bytes=64, tag="agg_codes")
-            scales = work.tile([P, P], U8, align_bytes=64, tag="agg_scales")
-            quantise(nc, agg_grouped_of[r][:], codes[:], scales[:])
-            agg_mx_of[r] = (codes, scales)
-
-        def combine(r):
-            codes, scales = agg_mx_of[r]
-            nodes = slice(P * r, P * (r + 1))
-            both = psum_acc.tile([P, FEAT], F32, tag="both")
-            mx_pass(
-                nc,
-                both[:],
-                hf_codes[:, nodes],
-                hf_scales[:, nodes],
-                weight_codes["rw"][:],
-                weight_scales["rw"][:],
-                start=True,
-                stop=False,
-            )
-            mx_pass(
-                nc,
-                both[:],
-                codes[:],
-                scales[:],
-                weight_codes["w"][:],
-                weight_scales["w"][:],
-                start=False,
-                stop=True,
-            )
-            both_of[r] = both
-
-        def finish(r):
+        def finish(tile):
             biased = work.tile([P, FEAT], F32, tag="biased")
-            nc.vector.tensor_tensor(out=biased[:], in0=both_of[r][:], in1=bias[:], op=ALU.add)
+            nc.vector.tensor_tensor(out=biased[:], in0=both_of[tile][:], in1=bias[:], op=ALU.add)
             result = work.tile([P, FEAT], F32, tag="result")
             nc.scalar.activation(out=result[:], in_=biased[:], func=ACT.Relu)
-            nc.sync.dma_start(out=out[P * r : P * (r + 1), :], in_=result[:])
+            nc.sync.dma_start(out=out[P * tile : P * (tile + 1), :], in_=result[:])
 
-        def in_range(r):
-            return 0 <= r < ROW_TILES
+        def in_range(g):
+            return 0 <= g < GROUPS
 
         with tc.manual_schedule():
-            for c in range(NODE_PASSES):
+            for c in range(CHUNKS):
                 group_h_by_nodes(c)
                 group_h_by_features(c)
-                for r in range(PACK * c, PACK * (c + 1)):
-                    count_and_sum(r)
-                quantise_h(c)
+                for slot in range(PACK * c, PACK * (c + 1)):
+                    count_and_sum(slot)
+                if c < CHUNKS - 1:
+                    quantise_h(c)
+            quantise_h(CHUNKS - 1)
             make_dis()
-            quantise_weight("rw")
-            quantise_weight("w")
             make_inv_nnz()
+            group_weight("rw")
+            group_weight("w")
 
-            for n in range(ROW_TILES + 3):
-                if in_range(n):
-                    scale_rows(n)
-                if in_range(n - 2):
-                    turn_agg(n - 2)
-                if in_range(n):
-                    turn_norm(n)
-                if in_range(n - 1):
-                    quantise_norm(n - 1)
-                    aggregate(n - 1)
-                if in_range(n - 2):
-                    quantise_agg(n - 2)
-                    combine(n - 2)
-                if in_range(n - 3):
-                    finish(n - 3)
+        mirrors = [(c, g) for g in range(GROUPS) for c in range(g // 2)]
+        for n in range(GROUPS + 3):
+            if n == 0:
+                scale_row(0, 0, 2)
+                scale_row(1, 0, 2)
+                scale_row(0, 2, 4)
+                scale_row(1, 2, 4)
+            elif in_range(n):
+                scale_row(2 * n)
+            if in_range(n - 2):
+                turn_agg(n - 2)
+            if in_range(n - 3):
+                finish(2 * (n - 3))
+            if in_range(n) and n > 0:
+                scale_row(2 * n + 1)
+            ready = [(c, g) for c, g in mirrors if 2 * c + 1 < n][:2]
+            for engine_copy, (c, g) in zip((nc.scalar.copy, nc.vector.tensor_copy), ready):
+                mirror_norm(engine_copy, c, g)
+                mirrors.remove((c, g))
+            if in_range(n):
+                turn_norm(n)
+            if n == 1:
+                quantise_weight("rw")
+                quantise_weight("w")
+            if in_range(n - 1):
+                quantise_norm(n - 1)
+                aggregate(n - 1)
+            if in_range(n - 3):
+                finish(2 * (n - 3) + 1)
+            if in_range(n - 2):
+                quantise_agg(n - 2)
+                combine(n - 2)

@@ -22,6 +22,8 @@ CHUNKS = NODES // K_PASS
 GROUP = 2 * P
 GROUPS = NODES // GROUP
 
+RUN = 4
+
 FLOPS = 2 * NODES * NODES * FEAT + 2 * 2 * NODES * FEAT * FEAT
 
 
@@ -73,8 +75,10 @@ def tile_sage_re_pb_kernel(tc, h, adj, w, rw, b, out):
             )
         adj_rows = keep.tile([P, ROW_TILES, NODES], BF16)
         adj_view = adj.rearrange("(g q e) n -> q g e n", q=P, e=2)
-        for slot in range(ROW_TILES):
-            nc.sync.dma_start(out=adj_rows[:, slot, :], in_=adj_view[:, slot // 2, slot % 2, :])
+        for g in range(GROUPS):
+            nc.sync.dma_start(
+                out=adj_rows[:, 2 * g : 2 * (g + 1), :], in_=adj_view[:, g, :, :]
+            )
         weight_raw = {}
         for name, weight in (("rw", rw), ("w", w)):
             raw = keep.tile([P, PACK, FEAT], BF16, name="raw_" + name)
@@ -99,8 +103,8 @@ def tile_sage_re_pb_kernel(tc, h, adj, w, rw, b, out):
         def group_h_by_nodes(c):
             grouped = new_grouped(FEAT * PACK)
             nc.scalar.copy(
-                out=grouped[:].rearrange("q (f t) -> q f t", t=PACK),
-                in_=h_rows[:, PACK * c : PACK * (c + 1), :].rearrange("q t f -> q f t"),
+                out=grouped[:].rearrange("q (b f t) -> q b t f", f=RUN, t=PACK),
+                in_=h_rows[:, PACK * c : PACK * (c + 1), :].rearrange("q t (b f) -> q b t f", f=RUN),
             )
             hn_grouped_of[c] = grouped
 
@@ -229,7 +233,7 @@ def tile_sage_re_pb_kernel(tc, h, adj, w, rw, b, out):
 
         def group_weight(name):
             grouped = new_grouped(FEAT * PACK)
-            nc.scalar.copy(
+            nc.vector.tensor_copy(
                 out=grouped[:].rearrange("q (o t) -> q o t", t=PACK),
                 in_=weight_raw[name][:].rearrange("q t o -> q o t"),
             )
@@ -289,9 +293,9 @@ def tile_sage_re_pb_kernel(tc, h, adj, w, rw, b, out):
 
         def mirror_norm(engine_copy, c, g):
             engine_copy(
-                out=grouped_norm(g)[:, c, :, :],
+                out=grouped_norm(g)[:, c, :, :].rearrange("q (b i) t -> q b t i", i=RUN),
                 in_=adj_rows[:, PACK * c : PACK * (c + 1), GROUP * g : GROUP * (g + 1)].rearrange(
-                    "q t i -> q i t"
+                    "q t (b i) -> q b t i", i=RUN
                 ),
             )
 
@@ -404,9 +408,9 @@ def tile_sage_re_pb_kernel(tc, h, adj, w, rw, b, out):
                     quantise_h(c)
             quantise_h(CHUNKS - 1)
             make_dis()
-            make_inv_nnz()
             group_weight("rw")
             group_weight("w")
+            make_inv_nnz()
 
         mirrors = [(c, g) for g in range(GROUPS) for c in range(g // 2)]
         for n in range(GROUPS + 3):

@@ -21,6 +21,7 @@ ROW_TILES = NODES // P
 CHUNKS = NODES // K_PASS
 GROUP = 2 * P
 GROUPS = NODES // GROUP
+EARLY = PACK
 
 RUN = 4
 
@@ -48,7 +49,7 @@ def tile_sage_re_pb_kernel(tc, h, adj, w, rw, b, out):
     with ExitStack() as stack:
         keep = stack.enter_context(tc.tile_pool(name="keep", bufs=1))
         stage = stack.enter_context(tc.tile_pool(name="stage", bufs=2))
-        work = stack.enter_context(tc.tile_pool(name="work", bufs=2))
+        work = stack.enter_context(tc.tile_pool(name="work", bufs=3))
         psum_turn = stack.enter_context(tc.psum_pool(name="psum_turn", bufs=4))
         psum_acc = stack.enter_context(tc.psum_pool(name="psum_acc", bufs=2))
 
@@ -56,29 +57,29 @@ def tile_sage_re_pb_kernel(tc, h, adj, w, rw, b, out):
         make_identity(nc, ident[:])
         ones = keep.tile([P, 1], BF16)
         nc.vector.memset(ones[:], 1.0)
-        pick = keep.tile([P, 2, 2, P], F32)
-        nc.vector.memset(pick[:], 0.0)
-        for half in range(2):
-            for e in range(2):
-                nc.vector.tensor_copy(
-                    out=pick[:, half, e, e::2], in_=ident[:, P // 2 * half : P // 2 * (half + 1)]
-                )
         warm = keep.tile([P, 1], F32)
         nc.scalar.sqrt(out=warm[:], in_=ones[:])
 
         h_rows = keep.tile([P, ROW_TILES, FEAT], BF16)
         h_view = h.rearrange("(g q e) f -> q g e f", q=P, e=2)
-        for c in range(CHUNKS):
+        adj_rows = keep.tile([P, ROW_TILES, NODES], BF16)
+        adj_view = adj.rearrange("(g q e) n -> q g e n", q=P, e=2)
+
+        def load_h(c):
             nc.sync.dma_start(
                 out=h_rows[:, PACK * c : PACK * (c + 1), :].rearrange("q (u e) f -> q u e f", e=2),
                 in_=h_view[:, 2 * c : 2 * (c + 1), :, :],
             )
-        adj_rows = keep.tile([P, ROW_TILES, NODES], BF16)
-        adj_view = adj.rearrange("(g q e) n -> q g e n", q=P, e=2)
-        for g in range(GROUPS):
-            nc.sync.dma_start(
-                out=adj_rows[:, 2 * g : 2 * (g + 1), :], in_=adj_view[:, g, :, :]
-            )
+
+        for c in range(CHUNKS):
+            if c == CHUNKS - 1:
+                load_h(c)
+            for g in (2 * c, 2 * c + 1):
+                nc.sync.dma_start(
+                    out=adj_rows[:, 2 * g : 2 * (g + 1), :], in_=adj_view[:, g, :, :]
+                )
+            if c < CHUNKS - 1:
+                load_h(c)
         weight_raw = {}
         for name, weight in (("rw", rw), ("w", w)):
             raw = keep.tile([P, PACK, FEAT], BF16, name="raw_" + name)
@@ -129,101 +130,100 @@ def tile_sage_re_pb_kernel(tc, h, adj, w, rw, b, out):
                 )
             hf_grouped_of[c] = grouped
 
-        def quantise_h(c):
+        def quantise_h_by_nodes(c):
             quantise(nc, hn_grouped_of[c][:], hn_codes[:, c, :], hn_scales[:, c, :])
+
+        def quantise_h_by_features(c):
             cols = slice(K_PASS * c, K_PASS * (c + 1))
             quantise(nc, hf_grouped_of[c][:], hf_codes[:, cols], hf_scales[:, cols])
 
-        row_count = keep.tile([P, ROW_TILES], F32)
-        deg_parts = psum_acc.tile([P, ROW_TILES, ROW_TILES], F32, tag="both", bufs=2)
-        mirror_parts = psum_acc.tile([P, ROW_TILES - PACK, ROW_TILES - PACK], F32, tag="neighbours", bufs=2)
+        deg = keep.tile([P, ROW_TILES], F32)
+        deg_parts = psum_acc.tile([P, ROW_TILES - EARLY, ROW_TILES], F32, tag="both", bufs=2)
+        nnz_parts = psum_acc.tile([P, ROW_TILES, ROW_TILES], F32, tag="neighbours", bufs=2)
+        positive_of = {}
 
-        def count_and_sum(slot):
-            chunk = slot // PACK
-            first = K_PASS * chunk
-            positive = stage.tile([P, NODES], BF16, tag="positive")
+        def compare(g):
+            positive = new_grouped(2 * NODES)
             nc.vector.tensor_scalar(
-                out=positive[:, first:],
-                in0=adj_rows[:, slot, first:],
+                out=positive[:].rearrange("q (e n) -> q e n", e=2),
+                in0=adj_rows[:, 2 * g : 2 * (g + 1), :],
                 scalar1=0.0,
                 scalar2=None,
                 op0=ALU.is_gt,
-                op1=ALU.add,
-                accum_out=row_count[:, slot : slot + 1],
             )
-            for s in range(ROW_TILES):
-                g, e = divmod(s, 2)
-                nc.tensor.matmul(
-                    out=deg_parts[:, s, slot : slot + 1],
-                    lhsT=adj_rows[:, slot, GROUP * g + e : GROUP * (g + 1) : 2],
-                    rhs=ones[:],
-                    start=True,
-                    stop=True,
-                )
-            for s in range(PACK * (chunk + 1), ROW_TILES):
-                nc.tensor.matmul(
-                    out=mirror_parts[:, s - PACK, slot : slot + 1],
-                    lhsT=positive[:, P * s : P * (s + 1)],
-                    rhs=ones[:],
-                    start=True,
-                    stop=True,
-                )
+            positive_of[g] = positive
 
-        deg = keep.tile([P, ROW_TILES], F32)
+        def sum_columns(group):
+            for slot in (2 * group, 2 * group + 1):
+                for s in range(EARLY, ROW_TILES):
+                    g, e = divmod(s, 2)
+                    nc.tensor.matmul(
+                        out=deg_parts[:, s - EARLY, slot : slot + 1],
+                        lhsT=adj_rows[:, slot, GROUP * g + e : GROUP * (g + 1) : 2],
+                        rhs=ones[:],
+                        start=True,
+                        stop=True,
+                    )
+
+        def count_columns(g):
+            for e in range(2):
+                for s in range(ROW_TILES):
+                    first = NODES * e + P * s
+                    nc.tensor.matmul(
+                        out=nnz_parts[:, s, 2 * g + e : 2 * g + e + 1],
+                        lhsT=positive_of[g][:, first : first + P],
+                        rhs=ones[:],
+                        start=True,
+                        stop=True,
+                    )
+
+        spare = keep.tile([P, NODES], BF16)
+
+        def sum_row(slot):
+            nc.vector.tensor_scalar(
+                out=spare[:],
+                in0=adj_rows[:, slot, :],
+                scalar1=1.0,
+                scalar2=None,
+                op0=ALU.mult,
+                op1=ALU.add,
+                accum_out=deg[:, slot : slot + 1],
+            )
+
         root = keep.tile([P, ROW_TILES], F32)
         dis = keep.tile([P, ROW_TILES], F32)
         dis_row = keep.tile([P, NODES], F32)
 
-        def make_dis():
-            nc.vector.tensor_reduce(out=deg[:], in_=deg_parts[:], axis=AXIS.X, op=ALU.add)
-            nc.scalar.sqrt(out=root[:], in_=deg[:])
-            nc.vector.reciprocal(out=dis[:], in_=root[:])
-            for c in range(CHUNKS):
-                spread = psum_turn.tile([P, PACK, P], F32, tag="turned")
-                for k in range(PACK):
-                    s = PACK * c + k
-                    nc.tensor.transpose(
-                        out=spread[:, k, :],
-                        in_=dis[:, s : s + 1].to_broadcast([P, P]),
-                        identity=ident[:],
-                    )
-                nc.scalar.copy(
-                    out=dis_row[:, K_PASS * c : K_PASS * (c + 1)].rearrange(
-                        "p (u n e) -> p u n e", u=2, e=2
-                    ),
-                    in_=spread[:].rearrange("p (u e) n -> p u n e", e=2),
+        def make_dis(first_chunk, last_chunk):
+            slots = slice(PACK * first_chunk, PACK * last_chunk)
+            if first_chunk > 0:
+                nc.vector.tensor_reduce(
+                    out=deg[:, slots], in_=deg_parts[:], axis=AXIS.X, op=ALU.add
                 )
+            nc.scalar.sqrt(out=root[:, slots], in_=deg[:, slots])
+            nc.vector.reciprocal(out=dis[:, slots], in_=root[:, slots])
+
+        def spread_dis(c):
+            spread = psum_turn.tile([P, PACK, P], F32, tag="turned")
+            for k in range(PACK):
+                s = PACK * c + k
+                nc.tensor.transpose(
+                    out=spread[:, k, :],
+                    in_=dis[:, s : s + 1].to_broadcast([P, P]),
+                    identity=ident[:],
+                )
+            nc.scalar.copy(
+                out=dis_row[:, K_PASS * c : K_PASS * (c + 1)].rearrange(
+                    "p (u n e) -> p u n e", u=2, e=2
+                ),
+                in_=spread[:].rearrange("p (u e) n -> p u n e", e=2),
+            )
 
         nnz = keep.tile([P, ROW_TILES], F32)
-        mirror = keep.tile([P, ROW_TILES - PACK], F32)
         inv_nnz = keep.tile([P, ROW_TILES], F32)
 
         def make_inv_nnz():
-            moved = psum_turn.tile([P, 2, GROUPS], F32, tag="turned")
-            for half in range(2):
-                for e in range(2):
-                    nc.tensor.matmul(
-                        out=moved[:, half, :],
-                        lhsT=pick[:, half, e, :],
-                        rhs=row_count[:, e::2],
-                        start=(e == 0),
-                        stop=(e == 1),
-                    )
-            nc.vector.tensor_copy(
-                out=nnz[:].rearrange("p (g half) -> p g half", half=2),
-                in_=moved[:].rearrange("p half g -> p g half"),
-            )
-            for chunk in range(1, CHUNKS):
-                tiles = slice(PACK * (chunk - 1), PACK * chunk)
-                nc.vector.tensor_reduce(
-                    out=mirror[:, tiles],
-                    in_=mirror_parts[:, tiles, : PACK * chunk],
-                    axis=AXIS.X,
-                    op=ALU.add,
-                )
-            nc.vector.tensor_tensor(
-                out=nnz[:, PACK:], in0=nnz[:, PACK:], in1=mirror[:], op=ALU.add
-            )
+            nc.vector.tensor_reduce(out=nnz[:], in_=nnz_parts[:], axis=AXIS.X, op=ALU.add)
             nc.vector.tensor_scalar_max(out=nnz[:], in0=nnz[:], scalar1=1.0)
             nc.vector.reciprocal(out=inv_nnz[:], in_=nnz[:])
 
@@ -233,10 +233,12 @@ def tile_sage_re_pb_kernel(tc, h, adj, w, rw, b, out):
 
         def group_weight(name):
             grouped = new_grouped(FEAT * PACK)
-            nc.vector.tensor_copy(
-                out=grouped[:].rearrange("q (o t) -> q o t", t=PACK),
-                in_=weight_raw[name][:].rearrange("q t o -> q o t"),
-            )
+            for k in range(PACK):
+                cols = slice(P * k, P * (k + 1))
+                nc.scalar.copy(
+                    out=grouped[:].rearrange("q (o t) -> q o t", t=PACK)[:, cols, :],
+                    in_=weight_raw[name][:, :, cols].rearrange("q t o -> q o t"),
+                )
             weight_grouped[name] = grouped
 
         def quantise_weight(name):
@@ -259,8 +261,8 @@ def tile_sage_re_pb_kernel(tc, h, adj, w, rw, b, out):
                 grouped_of[g] = new_grouped(CHUNKS * GROUP * PACK)
             return grouped_of[g][:].rearrange("q (c i t) -> q c i t", c=CHUNKS, t=PACK)
 
-        def scale_row(slot, first_chunk=None, last_chunk=CHUNKS):
-            first = K_PASS * (slot // PACK if first_chunk is None else first_chunk)
+        def scale_row(slot, first_chunk, last_chunk):
+            first = K_PASS * first_chunk
             last = K_PASS * last_chunk
             nc.vector.scalar_tensor_tensor(
                 out=adj_rows[:, slot, first:last],
@@ -271,9 +273,9 @@ def tile_sage_re_pb_kernel(tc, h, adj, w, rw, b, out):
                 op1=ALU.mult,
             )
 
-        def turn_norm(g):
+        def turn_norm(g, first_chunk, last_chunk):
             grouped_norm(g)
-            for c in range(g // 2, CHUNKS):
+            for c in range(first_chunk, last_chunk):
                 turned = psum_turn.tile([P, PACK, P], F32, tag="turned")
                 for e in range(2):
                     words = adj_rows[:, 2 * g + e, K_PASS * c : K_PASS * (c + 1)].bitcast(F32)
@@ -399,40 +401,76 @@ def tile_sage_re_pb_kernel(tc, h, adj, w, rw, b, out):
             return 0 <= g < GROUPS
 
         with tc.manual_schedule():
-            for c in range(CHUNKS):
-                group_h_by_nodes(c)
-                group_h_by_features(c)
-                for slot in range(PACK * c, PACK * (c + 1)):
-                    count_and_sum(slot)
-                if c < CHUNKS - 1:
-                    quantise_h(c)
-            quantise_h(CHUNKS - 1)
-            make_dis()
+            for g in (0, 1):
+                compare(g)
+                sum_row(2 * g)
+                sum_row(2 * g + 1)
+                sum_columns(g)
+            group_h_by_nodes(0)
+            group_h_by_features(0)
+            make_dis(0, 1)
+            quantise_h_by_nodes(0)
+            spread_dis(0)
+            quantise_h_by_features(0)
+            for g in (2, 3):
+                compare(g)
+                sum_columns(g)
+            for slot in range(EARLY):
+                scale_row(slot, 0, 1)
+            group_h_by_nodes(1)
+            group_h_by_features(1)
+            count_columns(0)
+            count_columns(1)
+            for g in (0, 1):
+                turn_norm(g, 0, 1)
+            quantise_h_by_nodes(1)
+            quantise_h_by_features(1)
+            for g in (4, 5):
+                compare(g)
+                sum_columns(g)
+            group_h_by_nodes(2)
+            group_h_by_features(2)
+            count_columns(2)
+            count_columns(3)
+            quantise_h_by_nodes(2)
+            quantise_h_by_features(2)
+            group_h_by_nodes(3)
+            group_h_by_features(3)
+            for g in (6, 7):
+                compare(g)
+                sum_columns(g)
+            make_dis(1, CHUNKS)
+            quantise_h_by_nodes(3)
+            quantise_h_by_features(3)
+            for c in range(1, CHUNKS):
+                spread_dis(c)
+            for g in range(GROUPS - PACK, GROUPS):
+                count_columns(g)
+            make_inv_nnz()
             group_weight("rw")
             group_weight("w")
-            make_inv_nnz()
 
         mirrors = [(c, g) for g in range(GROUPS) for c in range(g // 2)]
         for n in range(GROUPS + 3):
+            first = max(n // 2, 1)
             if n == 0:
-                scale_row(0, 0, 2)
-                scale_row(1, 0, 2)
-                scale_row(0, 2, 4)
-                scale_row(1, 2, 4)
+                for c in (1, 2):
+                    for slot in (0, 1):
+                        scale_row(slot, c, 2 * c)
             elif in_range(n):
-                scale_row(2 * n)
+                scale_row(2 * n, first, CHUNKS)
             if in_range(n - 2):
                 turn_agg(n - 2)
             if in_range(n - 3):
                 finish(2 * (n - 3))
             if in_range(n) and n > 0:
-                scale_row(2 * n + 1)
+                scale_row(2 * n + 1, first, CHUNKS)
             ready = [(c, g) for c, g in mirrors if 2 * c + 1 < n][:2]
             for engine_copy, (c, g) in zip((nc.scalar.copy, nc.vector.tensor_copy), ready):
                 mirror_norm(engine_copy, c, g)
                 mirrors.remove((c, g))
             if in_range(n):
-                turn_norm(n)
+                turn_norm(n, first, CHUNKS)
             if n == 1:
                 quantise_weight("rw")
                 quantise_weight("w")

@@ -408,62 +408,69 @@ def tile_sage_re_pb_kernel(tc, h, adj, w, rw, b, out):
                 sum_columns(g)
             group_h_by_nodes(0)
             group_h_by_features(0)
+            count_columns(0)
+            compare(2)
             make_dis(0, 1)
-            quantise_h_by_nodes(0)
+            sum_columns(2)
+            count_columns(1)
+            compare(3)
+            sum_columns(3)
             spread_dis(0)
-            quantise_h_by_features(0)
-            for g in (2, 3):
-                compare(g)
-                sum_columns(g)
-            for slot in range(EARLY):
-                scale_row(slot, 0, 1)
             group_h_by_nodes(1)
             group_h_by_features(1)
-            count_columns(0)
-            count_columns(1)
-            for g in (0, 1):
-                turn_norm(g, 0, 1)
+            quantise_h_by_nodes(0)
+            quantise_h_by_features(0)
+            for slot in range(EARLY):
+                scale_row(slot, 0, 1)
+            count_columns(2)
+            compare(4)
+            sum_columns(4)
+            count_columns(3)
+            compare(5)
+            sum_columns(5)
             quantise_h_by_nodes(1)
             quantise_h_by_features(1)
-            for g in (4, 5):
-                compare(g)
-                sum_columns(g)
             group_h_by_nodes(2)
+            for g in (0, 1):
+                turn_norm(g, 0, 1)
             group_h_by_features(2)
-            count_columns(2)
-            count_columns(3)
-            quantise_h_by_nodes(2)
-            quantise_h_by_features(2)
             group_h_by_nodes(3)
-            group_h_by_features(3)
-            for g in (6, 7):
-                compare(g)
-                sum_columns(g)
+            count_columns(4)
+            compare(6)
+            sum_columns(6)
+            quantise_h_by_nodes(2)
+            count_columns(5)
+            compare(7)
+            sum_columns(7)
             make_dis(1, CHUNKS)
-            quantise_h_by_nodes(3)
-            quantise_h_by_features(3)
+            quantise_h_by_features(2)
             for c in range(1, CHUNKS):
                 spread_dis(c)
-            for g in range(GROUPS - PACK, GROUPS):
-                count_columns(g)
+            group_h_by_features(3)
+            quantise_h_by_nodes(3)
+            for c in (1, 2):
+                for slot in (0, 1):
+                    scale_row(slot, c, 2 * c)
+                turn_norm(0, c, 2 * c)
+                count_columns(5 + c)
+                group_weight(("rw", "w")[c - 1])
+            scale_row(2, 1, CHUNKS)
+            quantise_h_by_features(3)
             make_inv_nnz()
-            group_weight("rw")
-            group_weight("w")
 
         mirrors = [(c, g) for g in range(GROUPS) for c in range(g // 2)]
-        for n in range(GROUPS + 3):
+        for n in range(1, GROUPS + 3):
             first = max(n // 2, 1)
-            if n == 0:
-                for c in (1, 2):
-                    for slot in (0, 1):
-                        scale_row(slot, c, 2 * c)
-            elif in_range(n):
+            if in_range(n) and n > 1:
                 scale_row(2 * n, first, CHUNKS)
             if in_range(n - 2):
                 turn_agg(n - 2)
             if in_range(n - 3):
                 finish(2 * (n - 3))
-            if in_range(n) and n > 0:
+            if n == 1:
+                quantise_norm(0)
+                aggregate(0)
+            if in_range(n):
                 scale_row(2 * n + 1, first, CHUNKS)
             ready = [(c, g) for c, g in mirrors if 2 * c + 1 < n][:2]
             for engine_copy, (c, g) in zip((nc.scalar.copy, nc.vector.tensor_copy), ready):
@@ -474,7 +481,7 @@ def tile_sage_re_pb_kernel(tc, h, adj, w, rw, b, out):
             if n == 1:
                 quantise_weight("rw")
                 quantise_weight("w")
-            if in_range(n - 1):
+            if in_range(n - 1) and n > 1:
                 quantise_norm(n - 1)
                 aggregate(n - 1)
             if in_range(n - 3):

@@ -22,6 +22,7 @@ CHUNKS = NODES // K_PASS
 GROUP = 2 * P
 GROUPS = NODES // GROUP
 EARLY = PACK
+ROW_SUMS = EARLY + 2
 
 RUN = 4
 
@@ -99,7 +100,7 @@ def tile_sage_re_pb_kernel(tc, h, adj, w, rw, b, out):
         hf_grouped_of = {}
 
         def new_grouped(width):
-            return stage.tile([P, width], BF16, align_bytes=64, tag="grouped", bufs=GROUPS, name="grouped")
+            return stage.tile([P, width], BF16, align_bytes=64, tag="grouped", bufs=GROUPS + 1, name="grouped")
 
         def group_h_by_nodes(c):
             grouped = new_grouped(FEAT * PACK)
@@ -138,7 +139,7 @@ def tile_sage_re_pb_kernel(tc, h, adj, w, rw, b, out):
             quantise(nc, hf_grouped_of[c][:], hf_codes[:, cols], hf_scales[:, cols])
 
         deg = keep.tile([P, ROW_TILES], F32)
-        deg_parts = psum_acc.tile([P, ROW_TILES - EARLY, ROW_TILES], F32, tag="both", bufs=2)
+        deg_parts = psum_acc.tile([P, ROW_TILES - ROW_SUMS, ROW_TILES], F32, tag="both", bufs=2)
         nnz_parts = psum_acc.tile([P, ROW_TILES, ROW_TILES], F32, tag="neighbours", bufs=2)
         positive_of = {}
 
@@ -155,10 +156,10 @@ def tile_sage_re_pb_kernel(tc, h, adj, w, rw, b, out):
 
         def sum_columns(group):
             for slot in (2 * group, 2 * group + 1):
-                for s in range(EARLY, ROW_TILES):
+                for s in range(ROW_SUMS, ROW_TILES):
                     g, e = divmod(s, 2)
                     nc.tensor.matmul(
-                        out=deg_parts[:, s - EARLY, slot : slot + 1],
+                        out=deg_parts[:, s - ROW_SUMS, slot : slot + 1],
                         lhsT=adj_rows[:, slot, GROUP * g + e : GROUP * (g + 1) : 2],
                         rhs=ones[:],
                         start=True,
@@ -177,11 +178,20 @@ def tile_sage_re_pb_kernel(tc, h, adj, w, rw, b, out):
                         stop=True,
                     )
 
-        spare = keep.tile([P, NODES], BF16)
+        dis_row = keep.tile([P, NODES], F32)
+        spare = dis_row[:].bitcast(BF16)
 
-        def sum_row(slot):
+        def sum_row_on_scalar(slot):
+            nc.scalar.activation(
+                out=spare[:, :NODES],
+                in_=adj_rows[:, slot, :],
+                func=ACT.Copy,
+                accum_out=deg[:, slot : slot + 1],
+            )
+
+        def sum_row_on_vector(slot):
             nc.vector.tensor_scalar(
-                out=spare[:],
+                out=spare[:, NODES:],
                 in0=adj_rows[:, slot, :],
                 scalar1=1.0,
                 scalar2=None,
@@ -192,13 +202,11 @@ def tile_sage_re_pb_kernel(tc, h, adj, w, rw, b, out):
 
         root = keep.tile([P, ROW_TILES], F32)
         dis = keep.tile([P, ROW_TILES], F32)
-        dis_row = keep.tile([P, NODES], F32)
-
         def make_dis(first_chunk, last_chunk):
             slots = slice(PACK * first_chunk, PACK * last_chunk)
             if first_chunk > 0:
                 nc.vector.tensor_reduce(
-                    out=deg[:, slots], in_=deg_parts[:], axis=AXIS.X, op=ALU.add
+                    out=deg[:, ROW_SUMS:], in_=deg_parts[:], axis=AXIS.X, op=ALU.add
                 )
             nc.scalar.sqrt(out=root[:, slots], in_=deg[:, slots])
             nc.vector.reciprocal(out=dis[:, slots], in_=root[:, slots])
@@ -402,26 +410,28 @@ def tile_sage_re_pb_kernel(tc, h, adj, w, rw, b, out):
 
         with tc.manual_schedule():
             for g in (0, 1):
+                sum_row_on_scalar(2 * g)
+                sum_row_on_vector(2 * g + 1)
                 compare(g)
-                sum_row(2 * g)
-                sum_row(2 * g + 1)
                 sum_columns(g)
+            make_dis(0, 1)
             group_h_by_nodes(0)
+            spread_dis(0)
             group_h_by_features(0)
             count_columns(0)
             compare(2)
-            make_dis(0, 1)
+            for slot in range(EARLY, ROW_SUMS):
+                sum_row_on_vector(slot)
             sum_columns(2)
             count_columns(1)
             compare(3)
             sum_columns(3)
-            spread_dis(0)
             group_h_by_nodes(1)
             group_h_by_features(1)
-            quantise_h_by_nodes(0)
-            quantise_h_by_features(0)
             for slot in range(EARLY):
                 scale_row(slot, 0, 1)
+            quantise_h_by_nodes(0)
+            quantise_h_by_features(0)
             count_columns(2)
             compare(4)
             sum_columns(4)
@@ -435,11 +445,9 @@ def tile_sage_re_pb_kernel(tc, h, adj, w, rw, b, out):
                 turn_norm(g, 0, 1)
             group_h_by_features(2)
             group_h_by_nodes(3)
-            count_columns(4)
             compare(6)
             sum_columns(6)
             quantise_h_by_nodes(2)
-            count_columns(5)
             compare(7)
             sum_columns(7)
             make_dis(1, CHUNKS)
@@ -448,14 +456,16 @@ def tile_sage_re_pb_kernel(tc, h, adj, w, rw, b, out):
                 spread_dis(c)
             group_h_by_features(3)
             quantise_h_by_nodes(3)
+            count_columns(4)
             for c in (1, 2):
                 for slot in (0, 1):
                     scale_row(slot, c, 2 * c)
                 turn_norm(0, c, 2 * c)
-                count_columns(5 + c)
+                count_columns(4 + c)
                 group_weight(("rw", "w")[c - 1])
             scale_row(2, 1, CHUNKS)
             quantise_h_by_features(3)
+            count_columns(7)
             make_inv_nnz()
 
         mirrors = [(c, g) for g in range(GROUPS) for c in range(g // 2)]

@@ -21,6 +21,7 @@ ROW_TILES = NODES // P
 CHUNKS = NODES // K_PASS
 GROUP = 2 * P
 GROUPS = NODES // GROUP
+PAIRED = GROUPS - 1
 EARLY = PACK
 ROW_SUMS = EARLY + 2
 
@@ -320,10 +321,10 @@ def tile_sage_re_pb_kernel(tc, h, adj, w, rw, b, out):
             )
             norm_mx_of[g] = (codes, scales)
 
-        def aggregate(g):
+        def aggregate(g, halves=(0, 1)):
             codes, scales = norm_mx_of[g]
-            agg = work.tile([P, 2, FEAT], BF16, tag="agg")
-            for half in range(2):
+            for half in halves:
+                tile = 2 * g + half
                 cols = slice(P * half, P * (half + 1))
                 neighbours = psum_acc.tile([P, FEAT], F32, tag="neighbours", bufs=2)
                 for c in range(CHUNKS):
@@ -337,44 +338,54 @@ def tile_sage_re_pb_kernel(tc, h, adj, w, rw, b, out):
                         start=(c == 0),
                         stop=(c == CHUNKS - 1),
                     )
-                tile = 2 * g + half
+                agg = work.tile([P, FEAT], BF16, tag="agg", bufs=6)
                 nc.scalar.activation(
-                    out=agg[:, half, :],
+                    out=agg[:],
                     in_=neighbours[:],
                     func=ACT.Copy,
                     scale=inv_nnz[:, tile : tile + 1],
                 )
-            agg_of[g] = agg
+                agg_of[tile] = agg
 
-        def turn_agg(g):
+        def turn_agg(g, halves=(0, 1)):
             turned = psum_turn.tile([P, PACK, P], F32, tag="turned")
-            for half in range(2):
-                words = agg_of[g][:, half, :].bitcast(F32)
+            for k, half in enumerate(halves):
+                words = agg_of[2 * g + half][:].bitcast(F32)
                 for u in range(2):
                     nc.tensor.transpose(
-                        out=turned[:, 2 * half + u, :],
+                        out=turned[:, 2 * k + u, :],
                         in_=words[:, P * u : P * (u + 1)],
                         identity=ident[:],
                     )
+            tiles = len(halves)
             grouped = work.tile([P, GROUP * PACK], BF16, align_bytes=64, tag="agg_grouped")
             nc.scalar.copy(
-                out=grouped[:].bitcast(F32).rearrange("q (half i u) -> q half i u", half=2, u=2),
-                in_=turned[:].rearrange("q (half u) i -> q half i u", u=2),
+                out=grouped[:].bitcast(F32)[:, : GROUP * tiles].rearrange(
+                    "q (k i u) -> q k i u", k=tiles, u=2
+                ),
+                in_=turned[:, : 2 * tiles, :].rearrange("q (k u) i -> q k i u", u=2),
             )
-            agg_grouped_of[g] = grouped
+            agg_grouped_of[g, halves] = grouped
 
-        def quantise_agg(g):
+        def quantise_agg(g, halves=(0, 1)):
+            width = P * len(halves)
             codes = work.tile([P, GROUP], U32, align_bytes=64, tag="agg_codes")
             scales = work.tile([P, GROUP], U8, align_bytes=64, tag="agg_scales")
-            quantise(nc, agg_grouped_of[g][:], codes[:], scales[:])
-            agg_mx_of[g] = (codes, scales)
+            quantise(
+                nc,
+                agg_grouped_of[g, halves][:, : PACK * width],
+                codes[:, :width],
+                scales[:, :width],
+            )
+            for k, half in enumerate(halves):
+                cols = slice(P * k, P * (k + 1))
+                agg_mx_of[2 * g + half] = (codes[:, cols], scales[:, cols])
 
-        def combine(g):
-            codes, scales = agg_mx_of[g]
-            for half in range(2):
+        def combine(g, halves=(0, 1)):
+            for half in halves:
                 tile = 2 * g + half
+                codes, scales = agg_mx_of[tile]
                 nodes = slice(P * tile, P * (tile + 1))
-                cols = slice(P * half, P * (half + 1))
                 both = psum_acc.tile([P, FEAT], F32, tag="both", bufs=2)
                 mx_pass(
                     nc,
@@ -389,8 +400,8 @@ def tile_sage_re_pb_kernel(tc, h, adj, w, rw, b, out):
                 mx_pass(
                     nc,
                     both[:],
-                    codes[:, cols],
-                    scales[:, cols],
+                    codes,
+                    scales,
                     weight_codes["w"][:],
                     weight_scales["w"][:],
                     start=False,
@@ -404,6 +415,23 @@ def tile_sage_re_pb_kernel(tc, h, adj, w, rw, b, out):
             result = work.tile([P, FEAT], F32, tag="result")
             nc.scalar.activation(out=result[:], in_=biased[:], func=ACT.Relu)
             nc.sync.dma_start(out=out[P * tile : P * (tile + 1), :], in_=result[:])
+
+        def finish_on_vector(tile):
+            biased = work.tile([P, FEAT], F32, tag="biased")
+            result = work.tile([P, FEAT], F32, tag="result")
+            for k in range(2):
+                cols = slice(FEAT // 2 * k, FEAT // 2 * (k + 1))
+                nc.vector.tensor_tensor(
+                    out=biased[:, cols], in0=both_of[tile][:, cols], in1=bias[:, cols], op=ALU.add
+                )
+            for k in range(2):
+                cols = slice(FEAT // 2 * k, FEAT // 2 * (k + 1))
+                nc.vector.tensor_scalar_max(
+                    out=result[:, cols], in0=biased[:, cols], scalar1=0.0
+                )
+                nc.sync.dma_start(
+                    out=out[P * tile : P * (tile + 1), cols], in_=result[:, cols]
+                )
 
         def in_range(g):
             return 0 <= g < GROUPS
@@ -473,9 +501,9 @@ def tile_sage_re_pb_kernel(tc, h, adj, w, rw, b, out):
             first = max(n // 2, 1)
             if in_range(n) and n > 1:
                 scale_row(2 * n, first, CHUNKS)
-            if in_range(n - 2):
+            if in_range(n - 2) and n - 2 < PAIRED:
                 turn_agg(n - 2)
-            if in_range(n - 3):
+            if in_range(n - 3) and n - 3 < PAIRED:
                 finish(2 * (n - 3))
             if n == 1:
                 quantise_norm(0)
@@ -493,9 +521,24 @@ def tile_sage_re_pb_kernel(tc, h, adj, w, rw, b, out):
                 quantise_weight("w")
             if in_range(n - 1) and n > 1:
                 quantise_norm(n - 1)
-                aggregate(n - 1)
-            if in_range(n - 3):
+                if n - 1 < PAIRED:
+                    aggregate(n - 1)
+                else:
+                    for half in range(2):
+                        aggregate(n - 1, (half,))
+                        turn_agg(n - 1, (half,))
+            if in_range(n - 3) and n - 3 < PAIRED:
                 finish(2 * (n - 3) + 1)
             if in_range(n - 2):
-                quantise_agg(n - 2)
-                combine(n - 2)
+                if n - 2 < PAIRED:
+                    quantise_agg(n - 2)
+                    combine(n - 2)
+                else:
+                    for half in range(2):
+                        quantise_agg(n - 2, (half,))
+                        combine(n - 2, (half,))
+                        tile = 2 * (n - 2) + half
+                        if tile < ROW_TILES - 1:
+                            finish(tile)
+                        else:
+                            finish_on_vector(tile)

@@ -410,24 +410,22 @@ def tile_sage_re_pb_kernel(tc, h, adj, w, rw, b, out):
                 both_of[tile] = both
 
         def finish(tile):
-            biased = work.tile([P, FEAT], F32, tag="biased")
-            nc.vector.tensor_tensor(out=biased[:], in0=both_of[tile][:], in1=bias[:], op=ALU.add)
-            result = work.tile([P, FEAT], F32, tag="result")
-            nc.scalar.activation(out=result[:], in_=biased[:], func=ACT.Relu)
+            result = work.tile([P, FEAT], F32, tag="result", bufs=6)
+            nc.vector.tensor_tensor(out=result[:], in0=both_of[tile][:], in1=bias[:], op=ALU.add)
+            nc.scalar.activation(out=result[:], in_=result[:], func=ACT.Relu)
             nc.sync.dma_start(out=out[P * tile : P * (tile + 1), :], in_=result[:])
 
         def finish_on_vector(tile):
-            biased = work.tile([P, FEAT], F32, tag="biased")
-            result = work.tile([P, FEAT], F32, tag="result")
+            result = work.tile([P, FEAT], F32, tag="result", bufs=6)
             for k in range(2):
                 cols = slice(FEAT // 2 * k, FEAT // 2 * (k + 1))
                 nc.vector.tensor_tensor(
-                    out=biased[:, cols], in0=both_of[tile][:, cols], in1=bias[:, cols], op=ALU.add
+                    out=result[:, cols], in0=both_of[tile][:, cols], in1=bias[:, cols], op=ALU.add
                 )
             for k in range(2):
                 cols = slice(FEAT // 2 * k, FEAT // 2 * (k + 1))
                 nc.vector.tensor_scalar_max(
-                    out=result[:, cols], in0=biased[:, cols], scalar1=0.0
+                    out=result[:, cols], in0=result[:, cols], scalar1=0.0
                 )
                 nc.sync.dma_start(
                     out=out[P * tile : P * (tile + 1), cols], in_=result[:, cols]

@@ -25,6 +25,8 @@ PAIRED = GROUPS - 1
 EARLY = PACK
 ROW_SUMS = EARLY + 2
 
+SUM_WIDTH = 32
+
 RUN = 4
 
 FLOPS = 2 * NODES * NODES * FEAT + 2 * 2 * NODES * FEAT * FEAT
@@ -57,10 +59,10 @@ def tile_sage_re_pb_kernel(tc, h, adj, w, rw, b, out):
 
         ident = keep.tile([P, P], F32)
         make_identity(nc, ident[:])
-        ones = keep.tile([P, 1], BF16)
+        ones = keep.tile([P, SUM_WIDTH], BF16)
         nc.vector.memset(ones[:], 1.0)
         warm = keep.tile([P, 1], F32)
-        nc.scalar.sqrt(out=warm[:], in_=ones[:])
+        nc.scalar.sqrt(out=warm[:], in_=ones[:, :1])
 
         h_rows = keep.tile([P, ROW_TILES, FEAT], BF16)
         h_view = h.rearrange("(g q e) f -> q g e f", q=P, e=2)
@@ -140,8 +142,9 @@ def tile_sage_re_pb_kernel(tc, h, adj, w, rw, b, out):
             quantise(nc, hf_grouped_of[c][:], hf_codes[:, cols], hf_scales[:, cols])
 
         deg = keep.tile([P, ROW_TILES], F32)
-        deg_parts = psum_acc.tile([P, ROW_TILES - ROW_SUMS, ROW_TILES], F32, tag="both", bufs=2)
-        nnz_parts = psum_acc.tile([P, ROW_TILES, ROW_TILES], F32, tag="neighbours", bufs=2)
+        late_slots = ROW_TILES - ROW_SUMS
+        deg_parts = psum_acc.tile([P, ROW_TILES * late_slots + SUM_WIDTH - 1], F32, tag="both", bufs=2)
+        nnz_parts = psum_acc.tile([P, ROW_TILES * ROW_TILES + SUM_WIDTH - 1], F32, tag="neighbours", bufs=2)
         positive_of = {}
 
         def compare(g):
@@ -155,12 +158,18 @@ def tile_sage_re_pb_kernel(tc, h, adj, w, rw, b, out):
             )
             positive_of[g] = positive
 
+        def sum_at(parts, column):
+            return parts[:, column : column + SUM_WIDTH]
+
+        def parts_of_node(parts, nodes):
+            return parts[:, : ROW_TILES * nodes].rearrange("p (k n) -> p n k", n=nodes)
+
         def sum_columns(group):
             for slot in (2 * group, 2 * group + 1):
                 for s in range(ROW_SUMS, ROW_TILES):
                     g, e = divmod(s, 2)
                     nc.tensor.matmul(
-                        out=deg_parts[:, s - ROW_SUMS, slot : slot + 1],
+                        out=sum_at(deg_parts, late_slots * slot + s - ROW_SUMS),
                         lhsT=adj_rows[:, slot, GROUP * g + e : GROUP * (g + 1) : 2],
                         rhs=ones[:],
                         start=True,
@@ -172,7 +181,7 @@ def tile_sage_re_pb_kernel(tc, h, adj, w, rw, b, out):
                 for s in range(ROW_TILES):
                     first = NODES * e + P * s
                     nc.tensor.matmul(
-                        out=nnz_parts[:, s, 2 * g + e : 2 * g + e + 1],
+                        out=sum_at(nnz_parts, ROW_TILES * (2 * g + e) + s),
                         lhsT=positive_of[g][:, first : first + P],
                         rhs=ones[:],
                         start=True,
@@ -207,7 +216,7 @@ def tile_sage_re_pb_kernel(tc, h, adj, w, rw, b, out):
             slots = slice(PACK * first_chunk, PACK * last_chunk)
             if first_chunk > 0:
                 nc.vector.tensor_reduce(
-                    out=deg[:, ROW_SUMS:], in_=deg_parts[:], axis=AXIS.X, op=ALU.add
+                    out=deg[:, ROW_SUMS:], in_=parts_of_node(deg_parts, late_slots), axis=AXIS.X, op=ALU.add
                 )
             nc.scalar.sqrt(out=root[:, slots], in_=deg[:, slots])
             nc.vector.reciprocal(out=dis[:, slots], in_=root[:, slots])
@@ -232,7 +241,7 @@ def tile_sage_re_pb_kernel(tc, h, adj, w, rw, b, out):
         inv_nnz = keep.tile([P, ROW_TILES], F32)
 
         def make_inv_nnz():
-            nc.vector.tensor_reduce(out=nnz[:], in_=nnz_parts[:], axis=AXIS.X, op=ALU.add)
+            nc.vector.tensor_reduce(out=nnz[:], in_=parts_of_node(nnz_parts, ROW_TILES), axis=AXIS.X, op=ALU.add)
             nc.vector.tensor_scalar_max(out=nnz[:], in0=nnz[:], scalar1=1.0)
             nc.vector.reciprocal(out=inv_nnz[:], in_=nnz[:])
 

@@ -221,21 +221,28 @@ def tile_sage_re_pb_kernel(tc, h, adj, w, rw, b, out):
             nc.scalar.sqrt(out=root[:, slots], in_=deg[:, slots])
             nc.vector.reciprocal(out=dis[:, slots], in_=root[:, slots])
 
-        def spread_dis(c):
-            spread = psum_turn.tile([P, PACK, P], F32, tag="turned")
+        spread_of = {}
+
+        def spread_turn(c):
+            if c == 0:
+                spread = psum_turn.tile([P, K_PASS], F32, tag="turned", name="spread")
+            elif c < 3:
+                spread = psum_acc.tile([P, K_PASS], F32, tag="both", bufs=2, name="spread")
+            else:
+                spread = psum_acc.tile([P, K_PASS], F32, tag="neighbours", bufs=2, name="spread")
+            spread_of[c] = spread
             for k in range(PACK):
                 s = PACK * c + k
+                u, e = divmod(k, 2)
                 nc.tensor.transpose(
-                    out=spread[:, k, :],
+                    out=spread[:, GROUP * u + e : GROUP * (u + 1) : 2],
                     in_=dis[:, s : s + 1].to_broadcast([P, P]),
                     identity=ident[:],
                 )
-            nc.scalar.copy(
-                out=dis_row[:, K_PASS * c : K_PASS * (c + 1)].rearrange(
-                    "p (u n e) -> p u n e", u=2, e=2
-                ),
-                in_=spread[:].rearrange("p (u e) n -> p u n e", e=2),
-            )
+
+        def spread_copy(c):
+            spread = spread_of[c]
+            nc.scalar.copy(out=dis_row[:, K_PASS * c : K_PASS * (c + 1)], in_=spread[:])
 
         nnz = keep.tile([P, ROW_TILES], F32)
         inv_nnz = keep.tile([P, ROW_TILES], F32)
@@ -287,6 +294,17 @@ def tile_sage_re_pb_kernel(tc, h, adj, w, rw, b, out):
                 in0=adj_rows[:, slot, first:last],
                 scalar=dis[:, slot : slot + 1],
                 in1=dis_row[:, first:last],
+                op0=ALU.mult,
+                op1=ALU.mult,
+            )
+
+        def scale_row_early(slot, c):
+            row = adj_rows[:, slot, K_PASS * c : K_PASS * (c + 1)]
+            nc.vector.scalar_tensor_tensor(
+                out=row,
+                in0=row,
+                scalar=dis[:, slot : slot + 1],
+                in1=spread_of[c][:],
                 op0=ALU.mult,
                 op1=ALU.mult,
             )
@@ -451,7 +469,8 @@ def tile_sage_re_pb_kernel(tc, h, adj, w, rw, b, out):
                 sum_columns(g)
             make_dis(0, 1)
             group_h_by_nodes(0)
-            spread_dis(0)
+            spread_turn(0)
+            spread_copy(0)
             group_h_by_features(0)
             count_columns(0)
             compare(2)
@@ -488,44 +507,36 @@ def tile_sage_re_pb_kernel(tc, h, adj, w, rw, b, out):
             make_dis(1, CHUNKS)
             quantise_h_by_features(2)
             for c in range(1, CHUNKS):
-                spread_dis(c)
+                spread_turn(c)
+                spread_copy(c)
             group_h_by_features(3)
             quantise_h_by_nodes(3)
             count_columns(4)
             for c in (1, 2):
-                for slot in (0, 1):
-                    scale_row(slot, c, 2 * c)
+                for chunk in range(c, 2 * c):
+                    for slot in (0, 1):
+                        scale_row_early(slot, chunk)
                 turn_norm(0, c, 2 * c)
                 count_columns(4 + c)
-                group_weight(("rw", "w")[c - 1])
             scale_row(2, 1, CHUNKS)
             quantise_h_by_features(3)
             count_columns(7)
             make_inv_nnz()
+            for name in ("rw", "w"):
+                group_weight(name)
 
         mirrors = [(c, g) for g in range(GROUPS) for c in range(g // 2)]
         for n in range(1, GROUPS + 3):
             first = max(n // 2, 1)
             if in_range(n) and n > 1:
                 scale_row(2 * n, first, CHUNKS)
-            if in_range(n - 2) and n - 2 < PAIRED:
-                turn_agg(n - 2)
-            if in_range(n - 3) and n - 3 < PAIRED:
-                finish(2 * (n - 3))
             if n == 1:
                 quantise_norm(0)
                 aggregate(0)
             if in_range(n):
                 scale_row(2 * n + 1, first, CHUNKS)
-            ready = [(c, g) for c, g in mirrors if 2 * c + 1 < n][:2]
-            for engine_copy, (c, g) in zip((nc.scalar.copy, nc.vector.tensor_copy), ready):
-                mirror_norm(engine_copy, c, g)
-                mirrors.remove((c, g))
-            if in_range(n):
-                turn_norm(n, first, CHUNKS)
-            if n == 1:
-                quantise_weight("rw")
-                quantise_weight("w")
+            if in_range(n - 2) and n - 2 < PAIRED:
+                turn_agg(n - 2)
             if in_range(n - 1) and n > 1:
                 quantise_norm(n - 1)
                 if n - 1 < PAIRED:
@@ -534,6 +545,17 @@ def tile_sage_re_pb_kernel(tc, h, adj, w, rw, b, out):
                     for half in range(2):
                         aggregate(n - 1, (half,))
                         turn_agg(n - 1, (half,))
+            ready = [(c, g) for c, g in mirrors if 2 * c + 1 < n][:2]
+            for engine_copy, (c, g) in zip((nc.scalar.copy, nc.vector.tensor_copy), ready):
+                mirror_norm(engine_copy, c, g)
+                mirrors.remove((c, g))
+            if n == 1:
+                quantise_weight("rw")
+                quantise_weight("w")
+            if in_range(n):
+                turn_norm(n, first, CHUNKS)
+            if in_range(n - 3) and n - 3 < PAIRED:
+                finish(2 * (n - 3))
             if in_range(n - 3) and n - 3 < PAIRED:
                 finish(2 * (n - 3) + 1)
             if in_range(n - 2):

@@ -23,7 +23,7 @@ GROUP = 2 * P
 GROUPS = NODES // GROUP
 PAIRED = GROUPS - 1
 EARLY = PACK
-ROW_SUMS = EARLY + 2
+ROW_SUMS = EARLY + 0
 
 SUM_WIDTH = 32
 
@@ -62,7 +62,7 @@ def tile_sage_re_pb_kernel(tc, h, adj, w, rw, b, out):
         ones = keep.tile([P, SUM_WIDTH], BF16)
         nc.vector.memset(ones[:], 1.0)
         warm = keep.tile([P, 1], F32)
-        nc.scalar.sqrt(out=warm[:], in_=ones[:, :1])
+        nc.scalar.activation(out=warm[:], in_=ones[:, :1], func=ACT.Abs_reciprocal_sqrt)
 
         h_rows = keep.tile([P, ROW_TILES, FEAT], BF16)
         h_view = h.rearrange("(g q e) f -> q g e f", q=P, e=2)
@@ -82,8 +82,10 @@ def tile_sage_re_pb_kernel(tc, h, adj, w, rw, b, out):
                 nc.sync.dma_start(
                     out=adj_rows[:, 2 * g : 2 * (g + 1), :], in_=adj_view[:, g, :, :]
                 )
-            if c < CHUNKS - 1:
+            if c < 2:
                 load_h(c)
+            if c == 1:
+                load_h(2)
         weight_raw = {}
         for name, weight in (("rw", rw), ("w", w)):
             raw = keep.tile([P, PACK, FEAT], BF16, name="raw_" + name)
@@ -105,9 +107,9 @@ def tile_sage_re_pb_kernel(tc, h, adj, w, rw, b, out):
         def new_grouped(width):
             return stage.tile([P, width], BF16, align_bytes=64, tag="grouped", bufs=GROUPS + 1, name="grouped")
 
-        def group_h_by_nodes(c):
+        def group_h_by_nodes(c, engine_copy):
             grouped = new_grouped(FEAT * PACK)
-            nc.scalar.copy(
+            engine_copy(
                 out=grouped[:].rearrange("q (b f t) -> q b t f", f=RUN, t=PACK),
                 in_=h_rows[:, PACK * c : PACK * (c + 1), :].rearrange("q t (b f) -> q b t f", f=RUN),
             )
@@ -210,7 +212,6 @@ def tile_sage_re_pb_kernel(tc, h, adj, w, rw, b, out):
                 accum_out=deg[:, slot : slot + 1],
             )
 
-        root = keep.tile([P, ROW_TILES], F32)
         dis = keep.tile([P, ROW_TILES], F32)
         def make_dis(first_chunk, last_chunk):
             slots = slice(PACK * first_chunk, PACK * last_chunk)
@@ -218,8 +219,7 @@ def tile_sage_re_pb_kernel(tc, h, adj, w, rw, b, out):
                 nc.vector.tensor_reduce(
                     out=deg[:, ROW_SUMS:], in_=parts_of_node(deg_parts, late_slots), axis=AXIS.X, op=ALU.add
                 )
-            nc.scalar.sqrt(out=root[:, slots], in_=deg[:, slots])
-            nc.vector.reciprocal(out=dis[:, slots], in_=root[:, slots])
+            nc.scalar.activation(out=dis[:, slots], in_=deg[:, slots], func=ACT.Abs_reciprocal_sqrt)
 
         spread_of = {}
 
@@ -247,8 +247,10 @@ def tile_sage_re_pb_kernel(tc, h, adj, w, rw, b, out):
         nnz = keep.tile([P, ROW_TILES], F32)
         inv_nnz = keep.tile([P, ROW_TILES], F32)
 
-        def make_inv_nnz():
+        def count_nnz():
             nc.vector.tensor_reduce(out=nnz[:], in_=parts_of_node(nnz_parts, ROW_TILES), axis=AXIS.X, op=ALU.add)
+
+        def invert_nnz():
             nc.vector.tensor_scalar_max(out=nnz[:], in0=nnz[:], scalar1=1.0)
             nc.vector.reciprocal(out=inv_nnz[:], in_=nnz[:])
 
@@ -256,15 +258,16 @@ def tile_sage_re_pb_kernel(tc, h, adj, w, rw, b, out):
         weight_codes = {}
         weight_scales = {}
 
-        def group_weight(name):
-            grouped = new_grouped(FEAT * PACK)
-            for k in range(PACK):
+        def group_weight(name, engine_copy, k):
+            if k == 0:
+                weight_grouped[name] = new_grouped(FEAT * PACK)
+            grouped = weight_grouped[name]
+            if True:
                 cols = slice(P * k, P * (k + 1))
-                nc.scalar.copy(
+                engine_copy(
                     out=grouped[:].rearrange("q (o t) -> q o t", t=PACK)[:, cols, :],
                     in_=weight_raw[name][:, :, cols].rearrange("q t o -> q o t"),
                 )
-            weight_grouped[name] = grouped
 
         def quantise_weight(name):
             grouped = weight_grouped[name]
@@ -309,6 +312,8 @@ def tile_sage_re_pb_kernel(tc, h, adj, w, rw, b, out):
                 op1=ALU.mult,
             )
 
+        turned_of = {}
+
         def turn_norm(g, first_chunk, last_chunk):
             grouped_norm(g)
             for c in range(first_chunk, last_chunk):
@@ -321,6 +326,11 @@ def tile_sage_re_pb_kernel(tc, h, adj, w, rw, b, out):
                             in_=words[:, P * u : P * (u + 1)],
                             identity=ident[:],
                         )
+                turned_of[g, c] = turned
+
+        def copy_turned(g, first_chunk, last_chunk):
+            for c in range(first_chunk, last_chunk):
+                turned = turned_of[g, c]
                 span = GROUP * PACK // 2
                 nc.scalar.copy(
                     out=grouped_of[g][:].bitcast(F32)[:, span * c : span * (c + 1)].rearrange(
@@ -348,7 +358,9 @@ def tile_sage_re_pb_kernel(tc, h, adj, w, rw, b, out):
             )
             norm_mx_of[g] = (codes, scales)
 
-        def aggregate(g, halves=(0, 1)):
+        neighbours_of = {}
+
+        def sum_neighbours(g, halves=(0, 1)):
             codes, scales = norm_mx_of[g]
             for half in halves:
                 tile = 2 * g + half
@@ -365,10 +377,15 @@ def tile_sage_re_pb_kernel(tc, h, adj, w, rw, b, out):
                         start=(c == 0),
                         stop=(c == CHUNKS - 1),
                     )
+                neighbours_of[tile] = neighbours
+
+        def scale_agg(g, halves=(0, 1)):
+            for half in halves:
+                tile = 2 * g + half
                 agg = work.tile([P, FEAT], BF16, tag="agg", bufs=6)
                 nc.scalar.activation(
                     out=agg[:],
-                    in_=neighbours[:],
+                    in_=neighbours_of[tile][:],
                     func=ACT.Copy,
                     scale=inv_nnz[:, tile : tile + 1],
                 )
@@ -384,6 +401,10 @@ def tile_sage_re_pb_kernel(tc, h, adj, w, rw, b, out):
                         in_=words[:, P * u : P * (u + 1)],
                         identity=ident[:],
                     )
+            turned_of["agg", g, halves] = turned
+
+        def copy_turned_agg(g, halves=(0, 1)):
+            turned = turned_of["agg", g, halves]
             tiles = len(halves)
             grouped = work.tile([P, GROUP * PACK], BF16, align_bytes=64, tag="agg_grouped")
             nc.scalar.copy(
@@ -413,7 +434,9 @@ def tile_sage_re_pb_kernel(tc, h, adj, w, rw, b, out):
                 tile = 2 * g + half
                 codes, scales = agg_mx_of[tile]
                 nodes = slice(P * tile, P * (tile + 1))
-                both = psum_acc.tile([P, FEAT], F32, tag="both", bufs=2)
+                both = psum_acc.tile(
+                    [P, FEAT], F32, tag="both" if g < PAIRED else "neighbours", bufs=2, name="both"
+                )
                 mx_pass(
                     nc,
                     both[:],
@@ -436,10 +459,21 @@ def tile_sage_re_pb_kernel(tc, h, adj, w, rw, b, out):
                 )
                 both_of[tile] = both
 
-        def finish(tile):
+        result_of = {}
+
+        def add_bias(tile):
             result = work.tile([P, FEAT], F32, tag="result", bufs=6)
             nc.vector.tensor_tensor(out=result[:], in0=both_of[tile][:], in1=bias[:], op=ALU.add)
+            result_of[tile] = result
+
+        def rectify(tile):
+            result = result_of[tile]
             nc.scalar.activation(out=result[:], in_=result[:], func=ACT.Relu)
+            nc.sync.dma_start(out=out[P * tile : P * (tile + 1), :], in_=result[:])
+
+        def rectify_on_vector(tile):
+            result = result_of[tile]
+            nc.vector.tensor_scalar_max(out=result[:], in0=result[:], scalar1=0.0)
             nc.sync.dma_start(out=out[P * tile : P * (tile + 1), :], in_=result[:])
 
         def finish_on_vector(tile):
@@ -468,106 +502,145 @@ def tile_sage_re_pb_kernel(tc, h, adj, w, rw, b, out):
                 compare(g)
                 sum_columns(g)
             make_dis(0, 1)
-            group_h_by_nodes(0)
+            group_h_by_nodes(0, nc.vector.tensor_copy)
+            group_h_by_features(0)
             spread_turn(0)
             spread_copy(0)
-            group_h_by_features(0)
             count_columns(0)
             compare(2)
-            for slot in range(EARLY, ROW_SUMS):
-                sum_row_on_vector(slot)
             sum_columns(2)
+            quantise_h_by_nodes(0)
             count_columns(1)
             compare(3)
             sum_columns(3)
-            group_h_by_nodes(1)
+            group_h_by_nodes(1, nc.vector.tensor_copy)
             group_h_by_features(1)
             for slot in range(EARLY):
                 scale_row(slot, 0, 1)
-            quantise_h_by_nodes(0)
             quantise_h_by_features(0)
+            group_h_by_nodes(2, nc.scalar.copy)
             count_columns(2)
-            compare(4)
-            sum_columns(4)
-            count_columns(3)
-            compare(5)
-            sum_columns(5)
-            quantise_h_by_nodes(1)
-            quantise_h_by_features(1)
-            group_h_by_nodes(2)
             for g in (0, 1):
                 turn_norm(g, 0, 1)
+                copy_turned(g, 0, 1)
+            compare(4)
+            sum_columns(4)
+            quantise_h_by_nodes(1)
+            quantise_h_by_features(1)
+            count_columns(3)
             group_h_by_features(2)
-            group_h_by_nodes(3)
+            compare(5)
+            sum_columns(5)
+            count_columns(4)
+            quantise_h_by_nodes(2)
+            group_h_by_nodes(3, nc.scalar.copy)
+            quantise_h_by_features(2)
             compare(6)
             sum_columns(6)
-            quantise_h_by_nodes(2)
-            compare(7)
+            group_h_by_features(3)
+            quantise_h_by_nodes(3)
+            count_columns(5)
             sum_columns(7)
             make_dis(1, CHUNKS)
-            quantise_h_by_features(2)
+            compare(7)
+            quantise_h_by_features(3)
+            for piece in range(2):
+                group_weight("rw", nc.scalar.copy, piece)
             for c in range(1, CHUNKS):
                 spread_turn(c)
                 spread_copy(c)
-            group_h_by_features(3)
-            quantise_h_by_nodes(3)
-            count_columns(4)
+            count_columns(6)
             for c in (1, 2):
                 for chunk in range(c, 2 * c):
                     for slot in (0, 1):
                         scale_row_early(slot, chunk)
                 turn_norm(0, c, 2 * c)
-                count_columns(4 + c)
+                if c == 2:
+                    count_columns(7)
+                copy_turned(0, c, 2 * c)
             scale_row(2, 1, CHUNKS)
-            quantise_h_by_features(3)
-            count_columns(7)
-            make_inv_nnz()
-            for name in ("rw", "w"):
-                group_weight(name)
+            quantise_norm(0)
+            count_nnz()
+            scale_row(3, 1, CHUNKS)
+            invert_nnz()
+            sum_neighbours(0)
+            turn_norm(1, 1, CHUNKS)
+            for piece in range(2, PACK):
+                group_weight("rw", nc.scalar.copy, piece)
+            for piece in range(PACK):
+                group_weight("w", nc.scalar.copy, piece)
+            copy_turned(1, 1, CHUNKS)
+            scale_agg(0)
+            for slot in (4, 5):
+                scale_row(slot, 1, CHUNKS)
 
-        mirrors = [(c, g) for g in range(GROUPS) for c in range(g // 2)]
-        for n in range(1, GROUPS + 3):
-            first = max(n // 2, 1)
-            if in_range(n) and n > 1:
-                scale_row(2 * n, first, CHUNKS)
-            if n == 1:
-                quantise_norm(0)
-                aggregate(0)
-            if in_range(n):
-                scale_row(2 * n + 1, first, CHUNKS)
-            if in_range(n - 2) and n - 2 < PAIRED:
-                turn_agg(n - 2)
-            if in_range(n - 1) and n > 1:
-                quantise_norm(n - 1)
-                if n - 1 < PAIRED:
-                    aggregate(n - 1)
-                else:
-                    for half in range(2):
-                        aggregate(n - 1, (half,))
-                        turn_agg(n - 1, (half,))
-            ready = [(c, g) for c, g in mirrors if 2 * c + 1 < n][:2]
-            for engine_copy, (c, g) in zip((nc.scalar.copy, nc.vector.tensor_copy), ready):
-                mirror_norm(engine_copy, c, g)
-                mirrors.remove((c, g))
-            if n == 1:
-                quantise_weight("rw")
-                quantise_weight("w")
-            if in_range(n):
-                turn_norm(n, first, CHUNKS)
-            if in_range(n - 3) and n - 3 < PAIRED:
-                finish(2 * (n - 3))
-            if in_range(n - 3) and n - 3 < PAIRED:
-                finish(2 * (n - 3) + 1)
-            if in_range(n - 2):
-                if n - 2 < PAIRED:
-                    quantise_agg(n - 2)
-                    combine(n - 2)
-                else:
-                    for half in range(2):
-                        quantise_agg(n - 2, (half,))
-                        combine(n - 2, (half,))
-                        tile = 2 * (n - 2) + half
-                        if tile < ROW_TILES - 1:
-                            finish(tile)
-                        else:
-                            finish_on_vector(tile)
+            on_scalar = nc.scalar.copy
+            on_vector = nc.vector.tensor_copy
+            MIRRORS = {
+                0: ((on_scalar, 0, 2), (on_scalar, 0, 3),),
+                1: ((on_vector, 0, 4), (on_scalar, 0, 5),),
+                2: ((on_vector, 1, 4), (on_scalar, 1, 5),),
+                3: ((on_vector, 0, 6), (on_scalar, 1, 6),),
+                4: ((on_vector, 2, 6), (on_vector, 0, 7), (on_scalar, 1, 7),),
+                5: ((on_vector, 2, 7),),
+            }
+
+            def first_of(g):
+                return max(g // 2, 1)
+
+            for k in range(GROUPS - 2):
+                turn_agg(k)
+                copy_turned_agg(k)
+                quantise_norm(k + 1)
+                turn_norm(k + 2, first_of(k + 2), CHUNKS)
+                copy_turned(k + 2, first_of(k + 2), CHUNKS)
+                for copy, c, g in MIRRORS.get(k, ()):
+                    if copy == on_scalar:
+                        mirror_norm(copy, c, g)
+                for copy, c, g in MIRRORS.get(k, ()):
+                    if copy == on_vector:
+                        mirror_norm(copy, c, g)
+                if k - 1 >= 0:
+                    add_bias(2 * k - 2)
+                    add_bias(2 * k - 1)
+                if k == 0:
+                    quantise_weight("rw")
+                    quantise_weight("w")
+                if k + 3 < GROUPS:
+                    scale_row(2 * k + 6, first_of(k + 3), CHUNKS)
+                quantise_agg(k)
+                if k + 3 < GROUPS:
+                    scale_row(2 * k + 7, first_of(k + 3), CHUNKS)
+                sum_neighbours(k + 1)
+                scale_agg(k + 1)
+                if k - 1 >= 0:
+                    rectify(2 * k - 2)
+                    rectify(2 * k - 1)
+                combine(k)
+            quantise_norm(7)
+            add_bias(10)
+            add_bias(11)
+            sum_neighbours(7, (0,))
+            turn_agg(6)
+            sum_neighbours(7, (1,))
+            scale_agg(7, (0,))
+            copy_turned_agg(6)
+            turn_agg(7, (0,))
+            scale_agg(7, (1,))
+            copy_turned_agg(7, (0,))
+            quantise_agg(6)
+            rectify_on_vector(10)
+            rectify_on_vector(11)
+            combine(6)
+            quantise_agg(7, (0,))
+            turn_agg(7, (1,))
+            copy_turned_agg(7, (1,))
+            add_bias(12)
+            add_bias(13)
+            quantise_agg(7, (1,))
+            combine(7)
+            rectify(12)
+            rectify(13)
+            add_bias(14)
+            rectify(14)
+            finish_on_vector(15)

@@ -23,7 +23,7 @@ GROUP = 2 * P
 GROUPS = NODES // GROUP
 PAIRED = GROUPS - 1
 EARLY = PACK
-ROW_SUMS = EARLY + 0
+SECOND = 2 * EARLY
 
 SUM_WIDTH = 32
 
@@ -144,8 +144,12 @@ def tile_sage_re_pb_kernel(tc, h, adj, w, rw, b, out):
             quantise(nc, hf_grouped_of[c][:], hf_codes[:, cols], hf_scales[:, cols])
 
         deg = keep.tile([P, ROW_TILES], F32)
-        late_slots = ROW_TILES - ROW_SUMS
-        deg_parts = psum_acc.tile([P, ROW_TILES * late_slots + SUM_WIDTH - 1], F32, tag="both", bufs=2)
+        deg_parts = {}
+        for chunk, nodes, rows in ((1, SECOND - EARLY, SECOND), (2, ROW_TILES - SECOND, ROW_TILES)):
+            deg_parts[chunk] = psum_acc.tile(
+                [P, rows * nodes + SUM_WIDTH - 1], F32, tag="both", bufs=2, name="deg_parts"
+            )
+        right_part = keep.tile([P, PACK], F32)
         nnz_parts = psum_acc.tile([P, ROW_TILES * ROW_TILES + SUM_WIDTH - 1], F32, tag="neighbours", bufs=2)
         positive_of = {}
 
@@ -163,15 +167,16 @@ def tile_sage_re_pb_kernel(tc, h, adj, w, rw, b, out):
         def sum_at(parts, column):
             return parts[:, column : column + SUM_WIDTH]
 
-        def parts_of_node(parts, nodes):
-            return parts[:, : ROW_TILES * nodes].rearrange("p (k n) -> p n k", n=nodes)
+        def parts_of_node(parts, nodes, rows=ROW_TILES):
+            return parts[:, : rows * nodes].rearrange("p (k n) -> p n k", n=nodes)
 
         def sum_columns(group):
             for slot in (2 * group, 2 * group + 1):
-                for s in range(ROW_SUMS, ROW_TILES):
+                for s in range(EARLY if slot < SECOND else SECOND, ROW_TILES):
                     g, e = divmod(s, 2)
+                    chunk, first, nodes = (1, EARLY, SECOND - EARLY) if s < SECOND else (2, SECOND, ROW_TILES - SECOND)
                     nc.tensor.matmul(
-                        out=sum_at(deg_parts, late_slots * slot + s - ROW_SUMS),
+                        out=sum_at(deg_parts[chunk], nodes * slot + s - first),
                         lhsT=adj_rows[:, slot, GROUP * g + e : GROUP * (g + 1) : 2],
                         rhs=ones[:],
                         start=True,
@@ -191,7 +196,7 @@ def tile_sage_re_pb_kernel(tc, h, adj, w, rw, b, out):
                     )
 
         dis_row = keep.tile([P, NODES], F32)
-        spare = dis_row[:].bitcast(BF16)
+        spare = keep.tile([P, 2 * NODES], BF16)
 
         def sum_row_on_scalar(slot):
             nc.scalar.activation(
@@ -199,6 +204,27 @@ def tile_sage_re_pb_kernel(tc, h, adj, w, rw, b, out):
                 in_=adj_rows[:, slot, :],
                 func=ACT.Copy,
                 accum_out=deg[:, slot : slot + 1],
+            )
+
+        def sum_right_part(slot):
+            first = K_PASS * 2
+            nc.vector.tensor_scalar(
+                out=spare[:, NODES + first * (slot % 2) :][:, : NODES - first],
+                in0=adj_rows[:, slot, first:],
+                scalar1=1.0,
+                scalar2=None,
+                op0=ALU.mult,
+                op1=ALU.add,
+                accum_out=right_part[:, slot - EARLY : slot - EARLY + 1],
+            )
+
+        def sum_right_part_on_scalar(slot):
+            first = K_PASS * 2
+            nc.scalar.activation(
+                out=spare[:, first * (slot % 2) :][:, : NODES - first],
+                in_=adj_rows[:, slot, first:],
+                func=ACT.Copy,
+                accum_out=right_part[:, slot - EARLY : slot - EARLY + 1],
             )
 
         def sum_row_on_vector(slot):
@@ -213,18 +239,28 @@ def tile_sage_re_pb_kernel(tc, h, adj, w, rw, b, out):
             )
 
         dis = keep.tile([P, ROW_TILES], F32)
-        def make_dis(first_chunk, last_chunk):
+        def sum_deg(first_chunk, last_chunk):
             slots = slice(PACK * first_chunk, PACK * last_chunk)
             if first_chunk > 0:
                 nc.vector.tensor_reduce(
-                    out=deg[:, ROW_SUMS:], in_=parts_of_node(deg_parts, late_slots), axis=AXIS.X, op=ALU.add
+                    out=deg[:, slots],
+                    in_=parts_of_node(
+                        deg_parts[first_chunk], slots.stop - slots.start, SECOND if first_chunk == 1 else ROW_TILES
+                    ),
+                    axis=AXIS.X,
+                    op=ALU.add,
                 )
+
+        def make_dis(first_chunk, last_chunk):
+            slots = slice(PACK * first_chunk, PACK * last_chunk)
+            if first_chunk == 1:
+                nc.vector.tensor_add(out=deg[:, slots], in0=deg[:, slots], in1=right_part[:])
             nc.scalar.activation(out=dis[:, slots], in_=deg[:, slots], func=ACT.Abs_reciprocal_sqrt)
 
         spread_of = {}
 
         def spread_turn(c):
-            if c == 0:
+            if c < 2:
                 spread = psum_turn.tile([P, K_PASS], F32, tag="turned", name="spread")
             elif c < 3:
                 spread = psum_acc.tile([P, K_PASS], F32, tag="both", bufs=2, name="spread")
@@ -250,8 +286,10 @@ def tile_sage_re_pb_kernel(tc, h, adj, w, rw, b, out):
         def count_nnz():
             nc.vector.tensor_reduce(out=nnz[:], in_=parts_of_node(nnz_parts, ROW_TILES), axis=AXIS.X, op=ALU.add)
 
-        def invert_nnz():
+        def bound_nnz():
             nc.vector.tensor_scalar_max(out=nnz[:], in0=nnz[:], scalar1=1.0)
+
+        def invert_nnz():
             nc.vector.reciprocal(out=inv_nnz[:], in_=nnz[:])
 
         weight_grouped = {}
@@ -348,8 +386,8 @@ def tile_sage_re_pb_kernel(tc, h, adj, w, rw, b, out):
             )
 
         def quantise_norm(g):
-            codes = work.tile([P, CHUNKS, GROUP], U32, align_bytes=64, tag="norm_codes")
-            scales = work.tile([P, CHUNKS, GROUP], U8, align_bytes=64, tag="norm_scales")
+            codes = work.tile([P, CHUNKS, GROUP], U32, align_bytes=64, tag="norm_codes", bufs=2)
+            scales = work.tile([P, CHUNKS, GROUP], U8, align_bytes=64, tag="norm_scales", bufs=2)
             quantise(
                 nc,
                 grouped_of[g][:],
@@ -382,7 +420,7 @@ def tile_sage_re_pb_kernel(tc, h, adj, w, rw, b, out):
         def scale_agg(g, halves=(0, 1)):
             for half in halves:
                 tile = 2 * g + half
-                agg = work.tile([P, FEAT], BF16, tag="agg", bufs=6)
+                agg = work.tile([P, FEAT], BF16, tag="agg", bufs=4)
                 nc.scalar.activation(
                     out=agg[:],
                     in_=neighbours_of[tile][:],
@@ -406,7 +444,7 @@ def tile_sage_re_pb_kernel(tc, h, adj, w, rw, b, out):
         def copy_turned_agg(g, halves=(0, 1)):
             turned = turned_of["agg", g, halves]
             tiles = len(halves)
-            grouped = work.tile([P, GROUP * PACK], BF16, align_bytes=64, tag="agg_grouped")
+            grouped = work.tile([P, GROUP * PACK], BF16, align_bytes=64, tag="agg_grouped", bufs=2)
             nc.scalar.copy(
                 out=grouped[:].bitcast(F32)[:, : GROUP * tiles].rearrange(
                     "q (k i u) -> q k i u", k=tiles, u=2
@@ -506,84 +544,88 @@ def tile_sage_re_pb_kernel(tc, h, adj, w, rw, b, out):
             group_h_by_features(0)
             spread_turn(0)
             spread_copy(0)
-            count_columns(0)
-            compare(2)
+            for slot in (4, 5):
+                sum_right_part_on_scalar(slot)
             sum_columns(2)
+            compare(2)
+            count_columns(0)
             quantise_h_by_nodes(0)
-            count_columns(1)
-            compare(3)
+            for slot in (6, 7):
+                sum_right_part(slot)
             sum_columns(3)
-            group_h_by_nodes(1, nc.vector.tensor_copy)
+            group_h_by_nodes(1, nc.scalar.copy)
+            sum_deg(1, 2)
+            compare(3)
+            make_dis(1, 2)
             group_h_by_features(1)
+            spread_turn(1)
+            spread_copy(1)
+            count_columns(1)
             for slot in range(EARLY):
                 scale_row(slot, 0, 1)
+            count_columns(2)
+            sum_columns(4)
             quantise_h_by_features(0)
             group_h_by_nodes(2, nc.scalar.copy)
-            count_columns(2)
-            for g in (0, 1):
-                turn_norm(g, 0, 1)
-                copy_turned(g, 0, 1)
+            group_h_by_features(2)
             compare(4)
-            sum_columns(4)
+            for slot in range(EARLY):
+                scale_row(slot, 1, 2)
+            sum_columns(5)
+            for c in (0, 1):
+                for g in (0, 1):
+                    turn_norm(g, c, c + 1)
+                    copy_turned(g, c, c + 1)
+            count_columns(3)
             quantise_h_by_nodes(1)
             quantise_h_by_features(1)
-            count_columns(3)
-            group_h_by_features(2)
             compare(5)
-            sum_columns(5)
+            sum_columns(6)
             count_columns(4)
             quantise_h_by_nodes(2)
             group_h_by_nodes(3, nc.scalar.copy)
-            quantise_h_by_features(2)
             compare(6)
-            sum_columns(6)
-            group_h_by_features(3)
-            quantise_h_by_nodes(3)
-            count_columns(5)
+            quantise_h_by_features(2)
             sum_columns(7)
-            make_dis(1, CHUNKS)
+            sum_deg(2, CHUNKS)
+            make_dis(2, CHUNKS)
+            group_h_by_features(3)
             compare(7)
-            quantise_h_by_features(3)
-            for piece in range(2):
-                group_weight("rw", nc.scalar.copy, piece)
-            for c in range(1, CHUNKS):
+            for c in range(2, CHUNKS):
                 spread_turn(c)
                 spread_copy(c)
-            count_columns(6)
-            for c in (1, 2):
-                for chunk in range(c, 2 * c):
-                    for slot in (0, 1):
-                        scale_row_early(slot, chunk)
-                turn_norm(0, c, 2 * c)
-                if c == 2:
-                    count_columns(7)
-                copy_turned(0, c, 2 * c)
-            scale_row(2, 1, CHUNKS)
+            count_columns(5)
+            for piece in range(3):
+                group_weight("rw", nc.scalar.copy, piece)
+            quantise_h_by_nodes(3)
+            for chunk in (2, 3):
+                for slot in (0, 1):
+                    scale_row_early(slot, chunk)
+                turn_norm(0, chunk, chunk + 1)
+                count_columns(4 + chunk)
+                copy_turned(0, chunk, chunk + 1)
+            scale_row(2, 2, CHUNKS)
+            scale_row(3, 2, CHUNKS)
             quantise_norm(0)
             count_nnz()
-            scale_row(3, 1, CHUNKS)
-            invert_nnz()
+            quantise_h_by_features(3)
+            bound_nnz()
             sum_neighbours(0)
-            turn_norm(1, 1, CHUNKS)
-            for piece in range(2, PACK):
-                group_weight("rw", nc.scalar.copy, piece)
+            turn_norm(1, 2, CHUNKS)
+            group_weight("rw", nc.scalar.copy, 3)
             for piece in range(PACK):
                 group_weight("w", nc.scalar.copy, piece)
-            copy_turned(1, 1, CHUNKS)
+            for g in (2, 3):
+                mirror_norm(nc.scalar.copy, 0, g)
+            copy_turned(1, 2, CHUNKS)
+            scale_row(4, 1, CHUNKS)
+            invert_nnz()
             scale_agg(0)
-            for slot in (4, 5):
-                scale_row(slot, 1, CHUNKS)
+            scale_row(5, 1, CHUNKS)
+            for name in ("rw", "w"):
+                quantise_weight(name)
 
-            on_scalar = nc.scalar.copy
-            on_vector = nc.vector.tensor_copy
-            MIRRORS = {
-                0: ((on_scalar, 0, 2), (on_scalar, 0, 3),),
-                1: ((on_vector, 0, 4), (on_scalar, 0, 5),),
-                2: ((on_vector, 1, 4), (on_scalar, 1, 5),),
-                3: ((on_vector, 0, 6), (on_scalar, 1, 6),),
-                4: ((on_vector, 2, 6), (on_vector, 0, 7), (on_scalar, 1, 7),),
-                5: ((on_vector, 2, 7),),
-            }
+            mirrors = [(c, g) for g in range(4, GROUPS) for c in range(g // 2)]
 
             def first_of(g):
                 return max(g // 2, 1)
@@ -594,18 +636,12 @@ def tile_sage_re_pb_kernel(tc, h, adj, w, rw, b, out):
                 quantise_norm(k + 1)
                 turn_norm(k + 2, first_of(k + 2), CHUNKS)
                 copy_turned(k + 2, first_of(k + 2), CHUNKS)
-                for copy, c, g in MIRRORS.get(k, ()):
-                    if copy == on_scalar:
-                        mirror_norm(copy, c, g)
-                for copy, c, g in MIRRORS.get(k, ()):
-                    if copy == on_vector:
-                        mirror_norm(copy, c, g)
+                ready, mirrors = mirrors[: 1 + min(k, 1)], mirrors[1 + min(k, 1) :]
+                for engine_copy, (c, g) in zip((nc.vector.tensor_copy, nc.scalar.copy), ready):
+                    mirror_norm(engine_copy, c, g)
                 if k - 1 >= 0:
                     add_bias(2 * k - 2)
                     add_bias(2 * k - 1)
-                if k == 0:
-                    quantise_weight("rw")
-                    quantise_weight("w")
                 if k + 3 < GROUPS:
                     scale_row(2 * k + 6, first_of(k + 3), CHUNKS)
                 quantise_agg(k)

@@ -75,17 +75,21 @@ def tile_sage_re_pb_kernel(tc, h, adj, w, rw, b, out):
                 in_=h_view[:, 2 * c : 2 * (c + 1), :, :],
             )
 
-        for c in range(CHUNKS):
-            if c == CHUNKS - 1:
-                load_h(c)
-            for g in (2 * c, 2 * c + 1):
-                nc.sync.dma_start(
-                    out=adj_rows[:, 2 * g : 2 * (g + 1), :], in_=adj_view[:, g, :, :]
-                )
-            if c < 2:
-                load_h(c)
-            if c == 1:
-                load_h(2)
+        def load_adj(g):
+            nc.sync.dma_start(out=adj_rows[:, 2 * g : 2 * (g + 1), :], in_=adj_view[:, g, :, :])
+
+        load_h(0)
+        load_adj(0)
+        load_adj(1)
+        load_adj(2)
+        load_adj(3)
+        load_h(1)
+        load_h(2)
+        load_adj(4)
+        load_adj(5)
+        load_h(3)
+        load_adj(6)
+        load_adj(7)
         weight_raw = {}
         for name, weight in (("rw", rw), ("w", w)):
             raw = keep.tile([P, PACK, FEAT], BF16, name="raw_" + name)
@@ -109,10 +113,16 @@ def tile_sage_re_pb_kernel(tc, h, adj, w, rw, b, out):
 
         def group_h_by_nodes(c, engine_copy):
             grouped = new_grouped(FEAT * PACK)
-            engine_copy(
-                out=grouped[:].rearrange("q (b f t) -> q b t f", f=RUN, t=PACK),
-                in_=h_rows[:, PACK * c : PACK * (c + 1), :].rearrange("q t (b f) -> q b t f", f=RUN),
-            )
+            for k in range(PACK):
+                u, e = divmod(k, 2)
+                engine_copy(
+                    out=grouped[:, PACK * P * k : PACK * P * (k + 1)].rearrange(
+                        "q (b m t) -> q b t m", m=RUN, t=PACK
+                    ),
+                    in_=h_rows[:, PACK * c : PACK * (c + 1), 2 * P * u + e : 2 * P * (u + 1) : 2].rearrange(
+                        "q t (b m) -> q b t m", m=RUN
+                    ),
+                )
             hn_grouped_of[c] = grouped
 
         def group_h_by_features(c):
@@ -422,12 +432,54 @@ def tile_sage_re_pb_kernel(tc, h, adj, w, rw, b, out):
                 tile = 2 * g + half
                 agg = work.tile([P, FEAT], BF16, tag="agg", bufs=4)
                 nc.scalar.activation(
-                    out=agg[:],
-                    in_=neighbours_of[tile][:],
+                    out=agg[:].rearrange("p (u m e) -> p u m e", u=2, e=2),
+                    in_=neighbours_of[tile][:].rearrange("p (u e m) -> p u m e", u=2, e=2),
                     func=ACT.Copy,
                     scale=inv_nnz[:, tile : tile + 1],
                 )
                 agg_of[tile] = agg
+
+        inv_row = keep.tile([P, GROUP], F32)
+
+        def spread_inv_nnz():
+            spread = psum_turn.tile([P, 2, P], F32, tag="turned", name="spread")
+            for half in range(2):
+                tile = 2 * PAIRED + half
+                nc.tensor.transpose(
+                    out=spread[:, half, :],
+                    in_=inv_nnz[:, tile : tile + 1].to_broadcast([P, P]),
+                    identity=ident[:],
+                )
+            nc.scalar.copy(out=inv_row[:], in_=spread[:].rearrange("p half i -> p (half i)"))
+
+        def sum_neighbours_turned(half):
+            codes, scales = norm_mx_of[PAIRED]
+            cols = slice(P * half, P * (half + 1))
+            sums = psum_acc.tile([P, PACK, P], F32, tag="neighbours", bufs=2, name="sums")
+            neighbours_of[2 * PAIRED + half] = sums
+            for t in range(PACK):
+                window = slice(P * t, P * (t + 1))
+                for c in range(CHUNKS):
+                    mx_pass(
+                        nc,
+                        sums[:, t, :],
+                        hn_codes[:, c, window],
+                        hn_scales[:, c, window],
+                        codes[:, c, cols],
+                        scales[:, c, cols],
+                        start=(c == 0),
+                        stop=(c == CHUNKS - 1),
+                    )
+
+        def scale_turned(half):
+            grouped = work.tile([P, GROUP * PACK], BF16, align_bytes=64, tag="agg_grouped", bufs=2)
+            nc.vector.tensor_tensor(
+                out=grouped[:, : P * PACK].rearrange("p (i t) -> p i t", t=PACK),
+                in0=neighbours_of[2 * PAIRED + half][:].rearrange("p t i -> p i t"),
+                in1=inv_row[:, P * half : P * (half + 1)].unsqueeze(2).to_broadcast([P, P, PACK]),
+                op=ALU.mult,
+            )
+            agg_grouped_of[PAIRED, (half,)] = grouped
 
         def turn_agg(g, halves=(0, 1)):
             turned = psum_turn.tile([P, PACK, P], F32, tag="turned")
@@ -534,22 +586,23 @@ def tile_sage_re_pb_kernel(tc, h, adj, w, rw, b, out):
             return 0 <= g < GROUPS
 
         with tc.manual_schedule():
+            group_h_by_nodes(0, nc.vector.tensor_copy)
+            group_h_by_features(0)
+            quantise_h_by_nodes(0)
+            quantise_h_by_features(0)
             for g in (0, 1):
                 sum_row_on_scalar(2 * g)
                 sum_row_on_vector(2 * g + 1)
                 compare(g)
                 sum_columns(g)
             make_dis(0, 1)
-            group_h_by_nodes(0, nc.vector.tensor_copy)
-            group_h_by_features(0)
             spread_turn(0)
             spread_copy(0)
-            for slot in (4, 5):
-                sum_right_part_on_scalar(slot)
+            sum_right_part_on_scalar(4)
+            sum_right_part(5)
             sum_columns(2)
             compare(2)
             count_columns(0)
-            quantise_h_by_nodes(0)
             for slot in (6, 7):
                 sum_right_part(slot)
             sum_columns(3)
@@ -565,7 +618,6 @@ def tile_sage_re_pb_kernel(tc, h, adj, w, rw, b, out):
                 scale_row(slot, 0, 1)
             count_columns(2)
             sum_columns(4)
-            quantise_h_by_features(0)
             group_h_by_nodes(2, nc.scalar.copy)
             group_h_by_features(2)
             compare(4)
@@ -621,6 +673,7 @@ def tile_sage_re_pb_kernel(tc, h, adj, w, rw, b, out):
             scale_row(4, 1, CHUNKS)
             invert_nnz()
             scale_agg(0)
+            spread_inv_nnz()
             scale_row(5, 1, CHUNKS)
             for name in ("rw", "w"):
                 quantise_weight(name)
@@ -637,7 +690,8 @@ def tile_sage_re_pb_kernel(tc, h, adj, w, rw, b, out):
                 turn_norm(k + 2, first_of(k + 2), CHUNKS)
                 copy_turned(k + 2, first_of(k + 2), CHUNKS)
                 ready, mirrors = mirrors[: 1 + min(k, 1)], mirrors[1 + min(k, 1) :]
-                for engine_copy, (c, g) in zip((nc.vector.tensor_copy, nc.scalar.copy), ready):
+                engines = (nc.vector.tensor_copy, nc.scalar.copy) if k > 0 else (nc.scalar.copy,)
+                for engine_copy, (c, g) in zip(engines, ready):
                     mirror_norm(engine_copy, c, g)
                 if k - 1 >= 0:
                     add_bias(2 * k - 2)
@@ -653,27 +707,23 @@ def tile_sage_re_pb_kernel(tc, h, adj, w, rw, b, out):
                     rectify(2 * k - 2)
                     rectify(2 * k - 1)
                 combine(k)
-            quantise_norm(7)
+            quantise_norm(PAIRED)
             add_bias(10)
             add_bias(11)
-            sum_neighbours(7, (0,))
             turn_agg(6)
-            sum_neighbours(7, (1,))
-            scale_agg(7, (0,))
             copy_turned_agg(6)
-            turn_agg(7, (0,))
-            scale_agg(7, (1,))
-            copy_turned_agg(7, (0,))
+            sum_neighbours_turned(0)
+            sum_neighbours_turned(1)
+            rectify(10)
+            rectify(11)
             quantise_agg(6)
-            rectify_on_vector(10)
-            rectify_on_vector(11)
+            scale_turned(0)
             combine(6)
             quantise_agg(7, (0,))
-            turn_agg(7, (1,))
-            copy_turned_agg(7, (1,))
+            scale_turned(1)
             add_bias(12)
-            add_bias(13)
             quantise_agg(7, (1,))
+            add_bias(13)
             combine(7)
             rectify(12)
             rectify(13)

@@ -22,8 +22,8 @@ CHUNKS = NODES // K_PASS
 GROUP = 2 * P
 GROUPS = NODES // GROUP
 PAIRED = GROUPS - 1
-EARLY = PACK
-SECOND = 2 * EARLY
+EARLY = 2 * PACK
+EARLY_NODES = EARLY * P
 
 SUM_WIDTH = 32
 
@@ -64,9 +64,30 @@ def tile_sage_re_pb_kernel(tc, h, adj, w, rw, b, out):
         warm = keep.tile([P, 1], F32)
         nc.scalar.activation(out=warm[:], in_=ones[:, :1], func=ACT.Abs_reciprocal_sqrt)
 
+        select = keep.tile([P, 4, P], F32)
+        nc.gpsimd.memset(select[:], 0.0)
+        for half in range(2):
+            for e in range(2):
+                nc.gpsimd.tensor_copy(
+                    out=select[:, 2 * half + e, e::2],
+                    in_=ident[:, P // 2 * half : P // 2 * (half + 1)],
+                )
+
         h_rows = keep.tile([P, ROW_TILES, FEAT], BF16)
         h_view = h.rearrange("(g q e) f -> q g e f", q=P, e=2)
-        adj_rows = keep.tile([P, ROW_TILES, NODES], BF16)
+        adj_top = keep.tile([P, EARLY, NODES], BF16)
+        adj_low = keep.tile([P, ROW_TILES - EARLY, NODES - EARLY_NODES], BF16)
+
+        def adj_part(first_slot, end_slot, first, end):
+            if first_slot < EARLY:
+                return adj_top[:, first_slot:end_slot, first:end]
+            return adj_low[
+                :, first_slot - EARLY : end_slot - EARLY, first - EARLY_NODES : end - EARLY_NODES
+            ]
+
+        def adj_row(slot, first, end):
+            return adj_part(slot, slot + 1, first, end)[:, 0, :]
+
         adj_view = adj.rearrange("(g q e) n -> q g e n", q=P, e=2)
 
         def load_h(c):
@@ -76,14 +97,17 @@ def tile_sage_re_pb_kernel(tc, h, adj, w, rw, b, out):
             )
 
         def load_adj(g):
-            nc.sync.dma_start(out=adj_rows[:, 2 * g : 2 * (g + 1), :], in_=adj_view[:, g, :, :])
+            first = 0 if 2 * g < EARLY else EARLY_NODES
+            nc.sync.dma_start(
+                out=adj_part(2 * g, 2 * (g + 1), first, NODES), in_=adj_view[:, g, :, first:]
+            )
 
         load_h(0)
         load_adj(0)
+        load_h(1)
         load_adj(1)
         load_adj(2)
         load_adj(3)
-        load_h(1)
         load_h(2)
         load_adj(4)
         load_adj(5)
@@ -105,6 +129,7 @@ def tile_sage_re_pb_kernel(tc, h, adj, w, rw, b, out):
         hn_scales = keep.tile([P, CHUNKS, FEAT], U8, align_bytes=64)
         hf_codes = keep.tile([P, NODES], U32, align_bytes=64)
         hf_scales = keep.tile([P, NODES], U8, align_bytes=64)
+        turned_of = {}
         hn_grouped_of = {}
         hf_grouped_of = {}
 
@@ -154,118 +179,116 @@ def tile_sage_re_pb_kernel(tc, h, adj, w, rw, b, out):
             quantise(nc, hf_grouped_of[c][:], hf_codes[:, cols], hf_scales[:, cols])
 
         deg = keep.tile([P, ROW_TILES], F32)
-        deg_parts = {}
-        for chunk, nodes, rows in ((1, SECOND - EARLY, SECOND), (2, ROW_TILES - SECOND, ROW_TILES)):
-            deg_parts[chunk] = psum_acc.tile(
-                [P, rows * nodes + SUM_WIDTH - 1], F32, tag="both", bufs=2, name="deg_parts"
-            )
-        right_part = keep.tile([P, PACK], F32)
-        nnz_parts = psum_acc.tile([P, ROW_TILES * ROW_TILES + SUM_WIDTH - 1], F32, tag="neighbours", bufs=2)
+        late_nodes = ROW_TILES - EARLY
+        early_parts = psum_acc.tile([P, EARLY * EARLY + SUM_WIDTH - 1], F32, tag="both", bufs=2)
+        late_parts = psum_acc.tile([P, ROW_TILES * late_nodes + SUM_WIDTH - 1], F32, tag="both", bufs=2)
+        right_part = keep.tile([P, EARLY], F32)
+        nnz_early_end = EARLY * EARLY + SUM_WIDTH - 1
+        nnz_parts = psum_acc.tile(
+            [P, nnz_early_end + ROW_TILES * late_nodes + SUM_WIDTH - 1], F32, tag="neighbours", bufs=2
+        )
+        row_counts = keep.tile([P, EARLY], F32)
         positive_of = {}
 
         def compare(g):
-            positive = new_grouped(2 * NODES)
+            slots = (2 * g, 2 * (g + 1))
+            first = 0 if 2 * g < EARLY else EARLY_NODES
+            end = EARLY_NODES if 2 * g < EARLY else NODES
+            positive = new_grouped(2 * NODES)[:].rearrange("q (e n) -> q e n", e=2)
+            positive_of[g] = positive
             nc.vector.tensor_scalar(
-                out=positive[:].rearrange("q (e n) -> q e n", e=2),
-                in0=adj_rows[:, 2 * g : 2 * (g + 1), :],
+                out=positive[:, :, first:end],
+                in0=adj_part(*slots, first, end),
                 scalar1=0.0,
                 scalar2=None,
                 op0=ALU.is_gt,
             )
-            positive_of[g] = positive
+            if end < NODES:
+                for e in range(2):
+                    slot = 2 * g + e
+                    nc.vector.tensor_scalar(
+                        out=positive[:, e, end:],
+                        in0=adj_row(slot, end, NODES),
+                        scalar1=0.0,
+                        scalar2=None,
+                        op0=ALU.is_gt,
+                        op1=ALU.add,
+                        accum_out=row_counts[:, slot : slot + 1],
+                    )
 
         def sum_at(parts, column):
             return parts[:, column : column + SUM_WIDTH]
 
-        def parts_of_node(parts, nodes, rows=ROW_TILES):
+        def parts_of_node(parts, nodes, rows):
             return parts[:, : rows * nodes].rearrange("p (k n) -> p n k", n=nodes)
 
         def sum_columns(group):
             for slot in (2 * group, 2 * group + 1):
-                for s in range(EARLY if slot < SECOND else SECOND, ROW_TILES):
+                for s in range(0 if slot < EARLY else EARLY, ROW_TILES):
                     g, e = divmod(s, 2)
-                    chunk, first, nodes = (1, EARLY, SECOND - EARLY) if s < SECOND else (2, SECOND, ROW_TILES - SECOND)
+                    if s < EARLY:
+                        out = sum_at(early_parts, EARLY * slot + s)
+                    else:
+                        out = sum_at(late_parts, late_nodes * slot + s - EARLY)
                     nc.tensor.matmul(
-                        out=sum_at(deg_parts[chunk], nodes * slot + s - first),
-                        lhsT=adj_rows[:, slot, GROUP * g + e : GROUP * (g + 1) : 2],
+                        out=out,
+                        lhsT=adj_row(slot, GROUP * g, GROUP * (g + 1))[:, e::2],
                         rhs=ones[:],
                         start=True,
                         stop=True,
                     )
 
         def count_columns(g):
-            for e in range(2):
-                for s in range(ROW_TILES):
-                    first = NODES * e + P * s
-                    nc.tensor.matmul(
-                        out=sum_at(nnz_parts, ROW_TILES * (2 * g + e) + s),
-                        lhsT=positive_of[g][:, first : first + P],
-                        rhs=ones[:],
-                        start=True,
-                        stop=True,
-                    )
+            for slot in (2 * g, 2 * g + 1):
+                row = positive_of[g][:, slot % 2, :]
+                for s in range(0 if slot < EARLY else EARLY, ROW_TILES):
+                    if s < EARLY:
+                        u, e = divmod(s, 2)
+                        out = sum_at(nnz_parts, EARLY * slot + s)
+                        block = row[:, GROUP * u + e : GROUP * (u + 1) : 2]
+                    else:
+                        out = sum_at(nnz_parts, nnz_early_end + late_nodes * slot + s - EARLY)
+                        block = row[:, P * s : P * (s + 1)]
+                    nc.tensor.matmul(out=out, lhsT=block, rhs=ones[:], start=True, stop=True)
 
         dis_row = keep.tile([P, NODES], F32)
-        spare = keep.tile([P, 2 * NODES], BF16)
+        spare = dis_row[:].bitcast(BF16).rearrange("p (k n) -> p k n", k=4)
 
-        def sum_row_on_scalar(slot):
+        def sum_right_on_scalar(slot):
             nc.scalar.activation(
-                out=spare[:, :NODES],
-                in_=adj_rows[:, slot, :],
+                out=spare[:, slot % 2, :],
+                in_=adj_row(slot, EARLY_NODES, NODES),
                 func=ACT.Copy,
-                accum_out=deg[:, slot : slot + 1],
+                accum_out=right_part[:, slot : slot + 1],
             )
 
-        def sum_right_part(slot):
-            first = K_PASS * 2
+        def sum_right_on_vector(slot):
             nc.vector.tensor_scalar(
-                out=spare[:, NODES + first * (slot % 2) :][:, : NODES - first],
-                in0=adj_rows[:, slot, first:],
+                out=spare[:, 2 + slot % 2, :],
+                in0=adj_row(slot, EARLY_NODES, NODES),
                 scalar1=1.0,
                 scalar2=None,
                 op0=ALU.mult,
                 op1=ALU.add,
-                accum_out=right_part[:, slot - EARLY : slot - EARLY + 1],
-            )
-
-        def sum_right_part_on_scalar(slot):
-            first = K_PASS * 2
-            nc.scalar.activation(
-                out=spare[:, first * (slot % 2) :][:, : NODES - first],
-                in_=adj_rows[:, slot, first:],
-                func=ACT.Copy,
-                accum_out=right_part[:, slot - EARLY : slot - EARLY + 1],
-            )
-
-        def sum_row_on_vector(slot):
-            nc.vector.tensor_scalar(
-                out=spare[:, NODES:],
-                in0=adj_rows[:, slot, :],
-                scalar1=1.0,
-                scalar2=None,
-                op0=ALU.mult,
-                op1=ALU.add,
-                accum_out=deg[:, slot : slot + 1],
+                accum_out=right_part[:, slot : slot + 1],
             )
 
         dis = keep.tile([P, ROW_TILES], F32)
-        def sum_deg(first_chunk, last_chunk):
-            slots = slice(PACK * first_chunk, PACK * last_chunk)
-            if first_chunk > 0:
-                nc.vector.tensor_reduce(
-                    out=deg[:, slots],
-                    in_=parts_of_node(
-                        deg_parts[first_chunk], slots.stop - slots.start, SECOND if first_chunk == 1 else ROW_TILES
-                    ),
-                    axis=AXIS.X,
-                    op=ALU.add,
-                )
 
-        def make_dis(first_chunk, last_chunk):
-            slots = slice(PACK * first_chunk, PACK * last_chunk)
-            if first_chunk == 1:
-                nc.vector.tensor_add(out=deg[:, slots], in0=deg[:, slots], in1=right_part[:])
-            nc.scalar.activation(out=dis[:, slots], in_=deg[:, slots], func=ACT.Abs_reciprocal_sqrt)
+        def sum_early_deg():
+            nc.vector.tensor_reduce(
+                out=deg[:, :EARLY], in_=parts_of_node(early_parts, EARLY, EARLY), axis=AXIS.X, op=ALU.add
+            )
+
+        def make_early_dis():
+            nc.vector.tensor_add(out=deg[:, :EARLY], in0=deg[:, :EARLY], in1=right_part[:])
+            nc.scalar.activation(out=dis[:, :EARLY], in_=deg[:, :EARLY], func=ACT.Abs_reciprocal_sqrt)
+
+        def make_late_dis():
+            nc.vector.tensor_reduce(
+                out=deg[:, EARLY:], in_=parts_of_node(late_parts, late_nodes, ROW_TILES), axis=AXIS.X, op=ALU.add
+            )
+            nc.scalar.activation(out=dis[:, EARLY:], in_=deg[:, EARLY:], func=ACT.Abs_reciprocal_sqrt)
 
         spread_of = {}
 
@@ -290,14 +313,40 @@ def tile_sage_re_pb_kernel(tc, h, adj, w, rw, b, out):
             spread = spread_of[c]
             nc.scalar.copy(out=dis_row[:, K_PASS * c : K_PASS * (c + 1)], in_=spread[:])
 
+        nnz_early = keep.tile([P, EARLY], F32)
         nnz = keep.tile([P, ROW_TILES], F32)
         inv_nnz = keep.tile([P, ROW_TILES], F32)
 
         def count_nnz():
-            nc.vector.tensor_reduce(out=nnz[:], in_=parts_of_node(nnz_parts, ROW_TILES), axis=AXIS.X, op=ALU.add)
+            nc.vector.tensor_reduce(
+                out=nnz_early[:], in_=parts_of_node(nnz_parts, EARLY, EARLY), axis=AXIS.X, op=ALU.add
+            )
+            nc.vector.tensor_reduce(
+                out=nnz[:, EARLY:],
+                in_=parts_of_node(nnz_parts[:, nnz_early_end:], late_nodes, ROW_TILES),
+                axis=AXIS.X,
+                op=ALU.add,
+            )
+            nc.vector.tensor_add(out=nnz_early[:], in0=nnz_early[:], in1=row_counts[:])
+            moved = psum_turn.tile([P, 2, EARLY // 2], F32, tag="turned", name="moved")
+            for half in range(2):
+                for e in range(2):
+                    nc.tensor.matmul(
+                        out=moved[:, half, :],
+                        lhsT=select[:, 2 * half + e, :],
+                        rhs=nnz_early[:, e::2],
+                        start=(e == 0),
+                        stop=(e == 1),
+                    )
+            turned_of["nnz"] = moved
 
         def bound_nnz():
-            nc.vector.tensor_scalar_max(out=nnz[:], in0=nnz[:], scalar1=1.0)
+            nc.vector.tensor_scalar_max(out=nnz[:, EARLY:], in0=nnz[:, EARLY:], scalar1=1.0)
+            nc.vector.tensor_scalar_max(
+                out=nnz[:, :EARLY].rearrange("p (g half) -> p half g", half=2),
+                in0=turned_of["nnz"][:],
+                scalar1=1.0,
+            )
 
         def invert_nnz():
             nc.vector.reciprocal(out=inv_nnz[:], in_=nnz[:])
@@ -341,8 +390,8 @@ def tile_sage_re_pb_kernel(tc, h, adj, w, rw, b, out):
             first = K_PASS * first_chunk
             last = K_PASS * last_chunk
             nc.vector.scalar_tensor_tensor(
-                out=adj_rows[:, slot, first:last],
-                in0=adj_rows[:, slot, first:last],
+                out=adj_row(slot, first, last),
+                in0=adj_row(slot, first, last),
                 scalar=dis[:, slot : slot + 1],
                 in1=dis_row[:, first:last],
                 op0=ALU.mult,
@@ -350,7 +399,7 @@ def tile_sage_re_pb_kernel(tc, h, adj, w, rw, b, out):
             )
 
         def scale_row_early(slot, c):
-            row = adj_rows[:, slot, K_PASS * c : K_PASS * (c + 1)]
+            row = adj_row(slot, K_PASS * c, K_PASS * (c + 1))
             nc.vector.scalar_tensor_tensor(
                 out=row,
                 in0=row,
@@ -360,14 +409,13 @@ def tile_sage_re_pb_kernel(tc, h, adj, w, rw, b, out):
                 op1=ALU.mult,
             )
 
-        turned_of = {}
 
         def turn_norm(g, first_chunk, last_chunk):
             grouped_norm(g)
             for c in range(first_chunk, last_chunk):
                 turned = psum_turn.tile([P, PACK, P], F32, tag="turned")
                 for e in range(2):
-                    words = adj_rows[:, 2 * g + e, K_PASS * c : K_PASS * (c + 1)].bitcast(F32)
+                    words = adj_row(2 * g + e, K_PASS * c, K_PASS * (c + 1)).bitcast(F32)
                     for u in range(2):
                         nc.tensor.transpose(
                             out=turned[:, 2 * e + u, :],
@@ -390,14 +438,14 @@ def tile_sage_re_pb_kernel(tc, h, adj, w, rw, b, out):
         def mirror_norm(engine_copy, c, g):
             engine_copy(
                 out=grouped_norm(g)[:, c, :, :].rearrange("q (b i) t -> q b t i", i=RUN),
-                in_=adj_rows[:, PACK * c : PACK * (c + 1), GROUP * g : GROUP * (g + 1)].rearrange(
+                in_=adj_part(PACK * c, PACK * (c + 1), GROUP * g, GROUP * (g + 1)).rearrange(
                     "q t (b i) -> q b t i", i=RUN
                 ),
             )
 
         def quantise_norm(g):
-            codes = work.tile([P, CHUNKS, GROUP], U32, align_bytes=64, tag="norm_codes", bufs=2)
-            scales = work.tile([P, CHUNKS, GROUP], U8, align_bytes=64, tag="norm_scales", bufs=2)
+            codes = work.tile([P, CHUNKS, GROUP], U32, align_bytes=64, tag="norm_codes")
+            scales = work.tile([P, CHUNKS, GROUP], U8, align_bytes=64, tag="norm_scales")
             quantise(
                 nc,
                 grouped_of[g][:],
@@ -430,7 +478,7 @@ def tile_sage_re_pb_kernel(tc, h, adj, w, rw, b, out):
         def scale_agg(g, halves=(0, 1)):
             for half in halves:
                 tile = 2 * g + half
-                agg = work.tile([P, FEAT], BF16, tag="agg", bufs=4)
+                agg = work.tile([P, FEAT], BF16, tag="agg", bufs=6)
                 nc.scalar.activation(
                     out=agg[:].rearrange("p (u m e) -> p u m e", u=2, e=2),
                     in_=neighbours_of[tile][:].rearrange("p (u e m) -> p u m e", u=2, e=2),
@@ -472,7 +520,7 @@ def tile_sage_re_pb_kernel(tc, h, adj, w, rw, b, out):
                     )
 
         def scale_turned(half):
-            grouped = work.tile([P, GROUP * PACK], BF16, align_bytes=64, tag="agg_grouped", bufs=2)
+            grouped = work.tile([P, GROUP * PACK], BF16, align_bytes=64, tag="agg_grouped")
             nc.vector.tensor_tensor(
                 out=grouped[:, : P * PACK].rearrange("p (i t) -> p i t", t=PACK),
                 in0=neighbours_of[2 * PAIRED + half][:].rearrange("p t i -> p i t"),
@@ -496,7 +544,7 @@ def tile_sage_re_pb_kernel(tc, h, adj, w, rw, b, out):
         def copy_turned_agg(g, halves=(0, 1)):
             turned = turned_of["agg", g, halves]
             tiles = len(halves)
-            grouped = work.tile([P, GROUP * PACK], BF16, align_bytes=64, tag="agg_grouped", bufs=2)
+            grouped = work.tile([P, GROUP * PACK], BF16, align_bytes=64, tag="agg_grouped")
             nc.scalar.copy(
                 out=grouped[:].bitcast(F32)[:, : GROUP * tiles].rearrange(
                     "q (k i u) -> q k i u", k=tiles, u=2
@@ -590,57 +638,56 @@ def tile_sage_re_pb_kernel(tc, h, adj, w, rw, b, out):
             group_h_by_features(0)
             quantise_h_by_nodes(0)
             quantise_h_by_features(0)
-            for g in (0, 1):
-                sum_row_on_scalar(2 * g)
-                sum_row_on_vector(2 * g + 1)
-                compare(g)
-                sum_columns(g)
-            make_dis(0, 1)
-            spread_turn(0)
-            spread_copy(0)
-            sum_right_part_on_scalar(4)
-            sum_right_part(5)
-            sum_columns(2)
-            compare(2)
+            for slot in (0, 1):
+                sum_right_on_scalar(slot)
+            compare(0)
+            sum_columns(0)
             count_columns(0)
-            for slot in (6, 7):
-                sum_right_part(slot)
-            sum_columns(3)
-            group_h_by_nodes(1, nc.scalar.copy)
-            sum_deg(1, 2)
-            compare(3)
-            make_dis(1, 2)
+            group_h_by_nodes(1, nc.vector.tensor_copy)
             group_h_by_features(1)
-            spread_turn(1)
-            spread_copy(1)
+            quantise_h_by_nodes(1)
+            for slot in (2, 3):
+                sum_right_on_scalar(slot)
+            compare(1)
+            sum_columns(1)
+            quantise_h_by_features(1)
             count_columns(1)
-            for slot in range(EARLY):
-                scale_row(slot, 0, 1)
+            for slot in (4, 5):
+                sum_right_on_scalar(slot)
+            compare(2)
+            sum_columns(2)
             count_columns(2)
-            sum_columns(4)
+            sum_right_on_scalar(6)
+            sum_right_on_vector(7)
+            sum_columns(3)
+            sum_early_deg()
+            make_early_dis()
+            compare(3)
+            for c in (0, 1):
+                spread_turn(c)
+                spread_copy(c)
+            count_columns(3)
             group_h_by_nodes(2, nc.scalar.copy)
             group_h_by_features(2)
+            for c in (0, 1):
+                for slot in range(PACK):
+                    scale_row(slot, c, c + 1)
+            sum_columns(4)
             compare(4)
-            for slot in range(EARLY):
-                scale_row(slot, 1, 2)
-            sum_columns(5)
             for c in (0, 1):
                 for g in (0, 1):
                     turn_norm(g, c, c + 1)
                     copy_turned(g, c, c + 1)
-            count_columns(3)
-            quantise_h_by_nodes(1)
-            quantise_h_by_features(1)
+            quantise_h_by_nodes(2)
+            sum_columns(5)
             compare(5)
+            quantise_h_by_features(2)
             sum_columns(6)
             count_columns(4)
-            quantise_h_by_nodes(2)
             group_h_by_nodes(3, nc.scalar.copy)
             compare(6)
-            quantise_h_by_features(2)
             sum_columns(7)
-            sum_deg(2, CHUNKS)
-            make_dis(2, CHUNKS)
+            make_late_dis()
             group_h_by_features(3)
             compare(7)
             for c in range(2, CHUNKS):

@@ -24,6 +24,7 @@ GROUPS = NODES // GROUP
 PAIRED = GROUPS - 1
 EARLY = 2 * PACK
 EARLY_NODES = EARLY * P
+EARLY_GROUPS = EARLY // 2
 
 SUM_WIDTH = 32
 
@@ -63,15 +64,6 @@ def tile_sage_re_pb_kernel(tc, h, adj, w, rw, b, out):
         nc.vector.memset(ones[:], 1.0)
         warm = keep.tile([P, 1], F32)
         nc.scalar.activation(out=warm[:], in_=ones[:, :1], func=ACT.Abs_reciprocal_sqrt)
-
-        select = keep.tile([P, 4, P], F32)
-        nc.gpsimd.memset(select[:], 0.0)
-        for half in range(2):
-            for e in range(2):
-                nc.gpsimd.tensor_copy(
-                    out=select[:, 2 * half + e, e::2],
-                    in_=ident[:, P // 2 * half : P // 2 * (half + 1)],
-                )
 
         h_rows = keep.tile([P, ROW_TILES, FEAT], BF16)
         h_view = h.rearrange("(g q e) f -> q g e f", q=P, e=2)
@@ -130,17 +122,34 @@ def tile_sage_re_pb_kernel(tc, h, adj, w, rw, b, out):
         hf_codes = keep.tile([P, NODES], U32, align_bytes=64)
         hf_scales = keep.tile([P, NODES], U8, align_bytes=64)
         turned_of = {}
+
+        def copy_turned_words(g, grouped, place, turned):
+            span = GROUP * PACK // 2
+            words = grouped[:].bitcast(F32)[:, span * place : span * (place + 1)]
+            if g < EARLY_GROUPS:
+                nc.scalar.copy(
+                    out=words.rearrange("q (e p u) -> q e p u", e=2, u=2),
+                    in_=turned[:].rearrange("q (e u) p -> q e p u", u=2),
+                )
+            else:
+                nc.scalar.copy(
+                    out=words.rearrange("q (p e u) -> q p e u", e=2, u=2),
+                    in_=turned[:].rearrange("q (e u) p -> q p e u", u=2),
+                )
+
         hn_grouped_of = {}
         hf_grouped_of = {}
 
         def new_grouped(width):
             return stage.tile([P, width], BF16, align_bytes=64, tag="grouped", bufs=GROUPS + 1, name="grouped")
 
-        def group_h_by_nodes(c, engine_copy):
-            grouped = new_grouped(FEAT * PACK)
-            for k in range(PACK):
+        def group_h_by_nodes(c, *engines, pieces=range(PACK)):
+            if 0 in pieces:
+                hn_grouped_of[c] = new_grouped(FEAT * PACK)
+            grouped = hn_grouped_of[c]
+            for k in pieces:
                 u, e = divmod(k, 2)
-                engine_copy(
+                engines[k % len(engines)](
                     out=grouped[:, PACK * P * k : PACK * P * (k + 1)].rearrange(
                         "q (b m t) -> q b t m", m=RUN, t=PACK
                     ),
@@ -148,13 +157,9 @@ def tile_sage_re_pb_kernel(tc, h, adj, w, rw, b, out):
                         "q t (b m) -> q b t m", m=RUN
                     ),
                 )
-            hn_grouped_of[c] = grouped
 
         def group_h_by_features(c):
             grouped = new_grouped(K_PASS * PACK)
-            grouped_words = grouped[:].bitcast(F32).rearrange(
-                "q (g p e u) -> q g p e u", g=2, e=2, u=2
-            )
             for g in range(2):
                 turned = psum_turn.tile([P, PACK, P], F32, tag="turned")
                 for e in range(2):
@@ -165,10 +170,7 @@ def tile_sage_re_pb_kernel(tc, h, adj, w, rw, b, out):
                             in_=row_words[:, P * u : P * (u + 1)],
                             identity=ident[:],
                         )
-                nc.scalar.copy(
-                    out=grouped_words[:, g, :, :, :],
-                    in_=turned[:].rearrange("q (e u) p -> q p e u", u=2),
-                )
+                copy_turned_words(2 * c + g, grouped, g, turned)
             hf_grouped_of[c] = grouped
 
         def quantise_h_by_nodes(c):
@@ -203,18 +205,21 @@ def tile_sage_re_pb_kernel(tc, h, adj, w, rw, b, out):
                 scalar2=None,
                 op0=ALU.is_gt,
             )
-            if end < NODES:
-                for e in range(2):
-                    slot = 2 * g + e
-                    nc.vector.tensor_scalar(
-                        out=positive[:, e, end:],
-                        in0=adj_row(slot, end, NODES),
-                        scalar1=0.0,
-                        scalar2=None,
-                        op0=ALU.is_gt,
-                        op1=ALU.add,
-                        accum_out=row_counts[:, slot : slot + 1],
-                    )
+
+        def compare_right(g):
+            positive = positive_of[g]
+            end = EARLY_NODES
+            for e in range(2):
+                slot = 2 * g + e
+                nc.vector.tensor_scalar(
+                    out=positive[:, e, end:],
+                    in0=adj_row(slot, end, NODES),
+                    scalar1=0.0,
+                    scalar2=None,
+                    op0=ALU.is_gt,
+                    op1=ALU.add,
+                    accum_out=row_counts[:, slot : slot + 1],
+                )
 
         def sum_at(parts, column):
             return parts[:, column : column + SUM_WIDTH]
@@ -313,13 +318,12 @@ def tile_sage_re_pb_kernel(tc, h, adj, w, rw, b, out):
             spread = spread_of[c]
             nc.scalar.copy(out=dis_row[:, K_PASS * c : K_PASS * (c + 1)], in_=spread[:])
 
-        nnz_early = keep.tile([P, EARLY], F32)
         nnz = keep.tile([P, ROW_TILES], F32)
         inv_nnz = keep.tile([P, ROW_TILES], F32)
 
         def count_nnz():
             nc.vector.tensor_reduce(
-                out=nnz_early[:], in_=parts_of_node(nnz_parts, EARLY, EARLY), axis=AXIS.X, op=ALU.add
+                out=nnz[:, :EARLY], in_=parts_of_node(nnz_parts, EARLY, EARLY), axis=AXIS.X, op=ALU.add
             )
             nc.vector.tensor_reduce(
                 out=nnz[:, EARLY:],
@@ -327,26 +331,12 @@ def tile_sage_re_pb_kernel(tc, h, adj, w, rw, b, out):
                 axis=AXIS.X,
                 op=ALU.add,
             )
-            nc.vector.tensor_add(out=nnz_early[:], in0=nnz_early[:], in1=row_counts[:])
-            moved = psum_turn.tile([P, 2, EARLY // 2], F32, tag="turned", name="moved")
-            for half in range(2):
-                for e in range(2):
-                    nc.tensor.matmul(
-                        out=moved[:, half, :],
-                        lhsT=select[:, 2 * half + e, :],
-                        rhs=nnz_early[:, e::2],
-                        start=(e == 0),
-                        stop=(e == 1),
-                    )
-            turned_of["nnz"] = moved
+
+        def add_row_counts():
+            nc.vector.tensor_add(out=nnz[:, :EARLY], in0=nnz[:, :EARLY], in1=row_counts[:])
 
         def bound_nnz():
-            nc.vector.tensor_scalar_max(out=nnz[:, EARLY:], in0=nnz[:, EARLY:], scalar1=1.0)
-            nc.vector.tensor_scalar_max(
-                out=nnz[:, :EARLY].rearrange("p (g half) -> p half g", half=2),
-                in0=turned_of["nnz"][:],
-                scalar1=1.0,
-            )
+            nc.vector.tensor_scalar_max(out=nnz[:], in0=nnz[:], scalar1=1.0)
 
         def invert_nnz():
             nc.vector.reciprocal(out=inv_nnz[:], in_=nnz[:])
@@ -426,22 +416,20 @@ def tile_sage_re_pb_kernel(tc, h, adj, w, rw, b, out):
 
         def copy_turned(g, first_chunk, last_chunk):
             for c in range(first_chunk, last_chunk):
-                turned = turned_of[g, c]
-                span = GROUP * PACK // 2
-                nc.scalar.copy(
-                    out=grouped_of[g][:].bitcast(F32)[:, span * c : span * (c + 1)].rearrange(
-                        "q (p e u) -> q p e u", e=2, u=2
-                    ),
-                    in_=turned[:].rearrange("q (e u) p -> q p e u", u=2),
-                )
+                copy_turned_words(g, grouped_of[g], c, turned_of[g, c])
 
         def mirror_norm(engine_copy, c, g):
-            engine_copy(
-                out=grouped_norm(g)[:, c, :, :].rearrange("q (b i) t -> q b t i", i=RUN),
-                in_=adj_part(PACK * c, PACK * (c + 1), GROUP * g, GROUP * (g + 1)).rearrange(
-                    "q t (b i) -> q b t i", i=RUN
-                ),
-            )
+            rows = adj_part(PACK * c, PACK * (c + 1), GROUP * g, GROUP * (g + 1))
+            mirrored = grouped_norm(g)[:, c, :, :]
+            if g < EARLY_GROUPS:
+                parts = [(mirrored[:, P * e : P * (e + 1), :], rows[:, :, e::2]) for e in range(2)]
+            else:
+                parts = [(mirrored, rows)]
+            for out_part, in_part in parts:
+                engine_copy(
+                    out=out_part.rearrange("q (b i) t -> q b t i", i=RUN),
+                    in_=in_part.rearrange("q t (b i) -> q b t i", i=RUN),
+                )
 
         def quantise_norm(g):
             codes = work.tile([P, CHUNKS, GROUP], U32, align_bytes=64, tag="norm_codes")
@@ -597,6 +585,11 @@ def tile_sage_re_pb_kernel(tc, h, adj, w, rw, b, out):
                 )
                 both_of[tile] = both
 
+        def out_rows(tile):
+            if tile < EARLY:
+                return out.rearrange("(g p e) o -> g e p o", p=P, e=2)[tile // 2, tile % 2, :, :]
+            return out[P * tile : P * (tile + 1), :]
+
         result_of = {}
 
         def add_bias(tile):
@@ -607,12 +600,12 @@ def tile_sage_re_pb_kernel(tc, h, adj, w, rw, b, out):
         def rectify(tile):
             result = result_of[tile]
             nc.scalar.activation(out=result[:], in_=result[:], func=ACT.Relu)
-            nc.sync.dma_start(out=out[P * tile : P * (tile + 1), :], in_=result[:])
+            nc.sync.dma_start(out=out_rows(tile), in_=result[:])
 
         def rectify_on_vector(tile):
             result = result_of[tile]
             nc.vector.tensor_scalar_max(out=result[:], in0=result[:], scalar1=0.0)
-            nc.sync.dma_start(out=out[P * tile : P * (tile + 1), :], in_=result[:])
+            nc.sync.dma_start(out=out_rows(tile), in_=result[:])
 
         def finish_on_vector(tile):
             result = work.tile([P, FEAT], F32, tag="result", bufs=6)
@@ -627,105 +620,113 @@ def tile_sage_re_pb_kernel(tc, h, adj, w, rw, b, out):
                     out=result[:, cols], in0=result[:, cols], scalar1=0.0
                 )
                 nc.sync.dma_start(
-                    out=out[P * tile : P * (tile + 1), cols], in_=result[:, cols]
+                    out=out_rows(tile)[:, cols], in_=result[:, cols]
                 )
 
         def in_range(g):
             return 0 <= g < GROUPS
 
         with tc.manual_schedule():
-            group_h_by_nodes(0, nc.vector.tensor_copy)
+            group_h_by_nodes(0, nc.scalar.copy, nc.vector.tensor_copy, nc.vector.tensor_copy, nc.vector.tensor_copy)
             group_h_by_features(0)
             quantise_h_by_nodes(0)
             quantise_h_by_features(0)
             for slot in (0, 1):
                 sum_right_on_scalar(slot)
             compare(0)
+            compare_right(0)
             sum_columns(0)
             count_columns(0)
-            group_h_by_nodes(1, nc.vector.tensor_copy)
+            group_h_by_nodes(1, nc.scalar.copy, nc.vector.tensor_copy, nc.vector.tensor_copy, nc.vector.tensor_copy)
             group_h_by_features(1)
             quantise_h_by_nodes(1)
             for slot in (2, 3):
                 sum_right_on_scalar(slot)
             compare(1)
+            compare_right(1)
             sum_columns(1)
             quantise_h_by_features(1)
             count_columns(1)
             for slot in (4, 5):
                 sum_right_on_scalar(slot)
             compare(2)
+            compare_right(2)
             sum_columns(2)
             count_columns(2)
             sum_right_on_scalar(6)
             sum_right_on_vector(7)
             sum_columns(3)
+            compare(3)
             sum_early_deg()
             make_early_dis()
-            compare(3)
+            compare_right(3)
             for c in (0, 1):
                 spread_turn(c)
-                spread_copy(c)
+            group_h_by_nodes(2, nc.scalar.copy, pieces=(0,))
+            spread_copy(1)
             count_columns(3)
-            group_h_by_nodes(2, nc.scalar.copy)
+            group_h_by_nodes(2, nc.scalar.copy, pieces=(1, 2, 3))
             group_h_by_features(2)
-            for c in (0, 1):
-                for slot in range(PACK):
-                    scale_row(slot, c, c + 1)
+            for slot in range(PACK):
+                scale_row_early(slot, 0)
+            for slot in range(PACK):
+                scale_row(slot, 1, 2)
             sum_columns(4)
-            compare(4)
-            for c in (0, 1):
-                for g in (0, 1):
-                    turn_norm(g, c, c + 1)
-                    copy_turned(g, c, c + 1)
-            quantise_h_by_nodes(2)
             sum_columns(5)
-            compare(5)
-            quantise_h_by_features(2)
+            for g in (0, 1):
+                turn_norm(g, 0, 1)
             sum_columns(6)
-            count_columns(4)
-            group_h_by_nodes(3, nc.scalar.copy)
-            compare(6)
+            copy_turned(0, 0, 1)
+            turn_norm(0, 1, 2)
             sum_columns(7)
             make_late_dis()
-            group_h_by_features(3)
-            compare(7)
+            copy_turned(1, 0, 1)
+            copy_turned(0, 1, 2)
+            turn_norm(1, 1, 2)
+            copy_turned(1, 1, 2)
+            compare(4)
+            compare(5)
+            quantise_h_by_nodes(2)
             for c in range(2, CHUNKS):
                 spread_turn(c)
                 spread_copy(c)
+            count_columns(4)
+            compare(6)
             count_columns(5)
-            for piece in range(3):
-                group_weight("rw", nc.scalar.copy, piece)
-            quantise_h_by_nodes(3)
+            compare(7)
+            quantise_h_by_features(2)
+            group_h_by_nodes(3, nc.scalar.copy)
             for chunk in (2, 3):
                 for slot in (0, 1):
                     scale_row_early(slot, chunk)
                 turn_norm(0, chunk, chunk + 1)
                 count_columns(4 + chunk)
                 copy_turned(0, chunk, chunk + 1)
+            group_h_by_features(3)
             scale_row(2, 2, CHUNKS)
-            scale_row(3, 2, CHUNKS)
-            quantise_norm(0)
+            quantise_h_by_nodes(3)
             count_nnz()
-            quantise_h_by_features(3)
+            quantise_norm(0)
+            add_row_counts()
+            scale_row(3, 2, CHUNKS)
             bound_nnz()
             sum_neighbours(0)
             turn_norm(1, 2, CHUNKS)
-            group_weight("rw", nc.scalar.copy, 3)
             for piece in range(PACK):
-                group_weight("w", nc.scalar.copy, piece)
-            for g in (2, 3):
-                mirror_norm(nc.scalar.copy, 0, g)
+                group_weight("rw", nc.scalar.copy, piece)
+            mirror_norm(nc.scalar.copy, 0, 2)
             copy_turned(1, 2, CHUNKS)
             scale_row(4, 1, CHUNKS)
             invert_nnz()
+            quantise_h_by_features(3)
             scale_agg(0)
+            for piece in range(PACK):
+                group_weight("w", nc.scalar.copy, piece)
             spread_inv_nnz()
             scale_row(5, 1, CHUNKS)
-            for name in ("rw", "w"):
-                quantise_weight(name)
+            quantise_weight("rw")
 
-            mirrors = [(c, g) for g in range(4, GROUPS) for c in range(g // 2)]
+            mirrors = [(c, g) for g in range(3, GROUPS) for c in range(g // 2)]
 
             def first_of(g):
                 return max(g // 2, 1)
@@ -736,15 +737,16 @@ def tile_sage_re_pb_kernel(tc, h, adj, w, rw, b, out):
                 quantise_norm(k + 1)
                 turn_norm(k + 2, first_of(k + 2), CHUNKS)
                 copy_turned(k + 2, first_of(k + 2), CHUNKS)
-                ready, mirrors = mirrors[: 1 + min(k, 1)], mirrors[1 + min(k, 1) :]
-                engines = (nc.vector.tensor_copy, nc.scalar.copy) if k > 0 else (nc.scalar.copy,)
-                for engine_copy, (c, g) in zip(engines, ready):
+                ready, mirrors = mirrors[:2], mirrors[2:]
+                for engine_copy, (c, g) in zip((nc.vector.tensor_copy, nc.scalar.copy), ready):
                     mirror_norm(engine_copy, c, g)
                 if k - 1 >= 0:
                     add_bias(2 * k - 2)
                     add_bias(2 * k - 1)
                 if k + 3 < GROUPS:
                     scale_row(2 * k + 6, first_of(k + 3), CHUNKS)
+                if k == 0:
+                    quantise_weight("w")
                 quantise_agg(k)
                 if k + 3 < GROUPS:
                     scale_row(2 * k + 7, first_of(k + 3), CHUNKS)

@@ -147,14 +147,16 @@ def tile_sage_re_pb_kernel(tc, h, adj, w, rw, b, out):
             if 0 in pieces:
                 hn_grouped_of[c] = new_grouped(FEAT * PACK)
             grouped = hn_grouped_of[c]
+            by_feature = grouped[:].rearrange(
+                "q (u e b m t) -> q u b t m e", u=2, e=2, m=RUN // 2, t=PACK
+            )
+            blocks = P // RUN
             for k in pieces:
-                u, e = divmod(k, 2)
+                u, part = divmod(k, 2)
                 engines[k % len(engines)](
-                    out=grouped[:, PACK * P * k : PACK * P * (k + 1)].rearrange(
-                        "q (b m t) -> q b t m", m=RUN, t=PACK
-                    ),
-                    in_=h_rows[:, PACK * c : PACK * (c + 1), 2 * P * u + e : 2 * P * (u + 1) : 2].rearrange(
-                        "q t (b m) -> q b t m", m=RUN
+                    out=by_feature[:, u, blocks * part : blocks * (part + 1), :, :, :],
+                    in_=h_rows[:, PACK * c : PACK * (c + 1), P * k : P * (k + 1)].rearrange(
+                        "q t (b m e) -> q b t m e", m=RUN // 2, e=2
                     ),
                 )
 
@@ -352,8 +354,10 @@ def tile_sage_re_pb_kernel(tc, h, adj, w, rw, b, out):
             if True:
                 cols = slice(P * k, P * (k + 1))
                 engine_copy(
-                    out=grouped[:].rearrange("q (o t) -> q o t", t=PACK)[:, cols, :],
-                    in_=weight_raw[name][:, :, cols].rearrange("q t o -> q o t"),
+                    out=grouped[:, PACK * P * k : PACK * P * (k + 1)].rearrange(
+                        "q (b o t) -> q b t o", o=RUN, t=PACK
+                    ),
+                    in_=weight_raw[name][:, :, cols].rearrange("q t (b o) -> q b t o", o=RUN),
                 )
 
         def quantise_weight(name):
@@ -422,13 +426,14 @@ def tile_sage_re_pb_kernel(tc, h, adj, w, rw, b, out):
             rows = adj_part(PACK * c, PACK * (c + 1), GROUP * g, GROUP * (g + 1))
             mirrored = grouped_norm(g)[:, c, :, :]
             if g < EARLY_GROUPS:
-                parts = [(mirrored[:, P * e : P * (e + 1), :], rows[:, :, e::2]) for e in range(2)]
-            else:
-                parts = [(mirrored, rows)]
-            for out_part, in_part in parts:
                 engine_copy(
-                    out=out_part.rearrange("q (b i) t -> q b t i", i=RUN),
-                    in_=in_part.rearrange("q t (b i) -> q b t i", i=RUN),
+                    out=mirrored.rearrange("q (e b m) t -> q b t m e", e=2, m=RUN // 2),
+                    in_=rows.rearrange("q t (b m e) -> q b t m e", m=RUN // 2, e=2),
+                )
+            else:
+                engine_copy(
+                    out=mirrored.rearrange("q (b i) t -> q b t i", i=RUN),
+                    in_=rows.rearrange("q t (b i) -> q b t i", i=RUN),
                 )
 
         def quantise_norm(g):
@@ -777,5 +782,5 @@ def tile_sage_re_pb_kernel(tc, h, adj, w, rw, b, out):
             rectify(12)
             rectify(13)
             add_bias(14)
-            rectify(14)
+            rectify_on_vector(14)
             finish_on_vector(15)

from contextlib import ExitStack

import concourse.mybir as mybir
from concourse.masks import make_identity

F32 = mybir.dt.float32
BF16 = mybir.dt.bfloat16
U32 = mybir.dt.uint32
U8 = mybir.dt.uint8
FP8X4 = mybir.dt.float8_e4m3fn_x4
ALU = mybir.AluOpType
ACT = mybir.ActivationFunctionType
AXIS = mybir.AxisListType

P = 128
PACK = 4
K_PASS = P * PACK
NODES = 2048
FEAT = 512
ROW_TILES = NODES // P
CHUNKS = NODES // K_PASS
GROUP = 2 * P
GROUPS = NODES // GROUP
PAIRED = GROUPS - 1
EARLY = 2 * PACK
EARLY_NODES = EARLY * P
EARLY_GROUPS = EARLY // 2

SUM_WIDTH = 32

RUN = 4

FLOPS = 2 * NODES * NODES * FEAT + 2 * 2 * NODES * FEAT * FEAT


def quantise(nc, grouped, codes, scales):
    nc.vector.quantize_mx(out=codes.bitcast(FP8X4), scales=scales, in_=grouped)


def mx_pass(nc, acc, stat_codes, stat_scales, mov_codes, mov_scales, start, stop):
    nc.tensor.matmul_mx(
        out=acc,
        lhsT=stat_codes.bitcast(FP8X4),
        lhsT_scale=stat_scales,
        rhs=mov_codes.bitcast(FP8X4),
        rhs_scale=mov_scales,
        start=start,
        stop=stop,
    )


def tile_sage_re_pb_kernel(tc, h, adj, w, rw, b, out):
    nc = tc.nc
    with ExitStack() as stack:
        keep = stack.enter_context(tc.tile_pool(name="keep", bufs=1))
        stage = stack.enter_context(tc.tile_pool(name="stage", bufs=2))
        work = stack.enter_context(tc.tile_pool(name="work", bufs=3))
        psum_turn = stack.enter_context(tc.psum_pool(name="psum_turn", bufs=4))
        psum_acc = stack.enter_context(tc.psum_pool(name="psum_acc", bufs=2))

        ident = keep.tile([P, P], F32)
        make_identity(nc, ident[:])
        ones = keep.tile([P, SUM_WIDTH], BF16)
        nc.vector.memset(ones[:], 1.0)
        warm = keep.tile([P, 1], F32)
        nc.scalar.activation(out=warm[:], in_=ones[:, :1], func=ACT.Abs_reciprocal_sqrt)

        h_rows = keep.tile([P, ROW_TILES, FEAT], BF16)
        h_view = h.rearrange("(g q e) f -> q g e f", q=P, e=2)
        adj_top = keep.tile([P, EARLY, NODES], BF16)
        adj_low = keep.tile([P, ROW_TILES - EARLY, NODES - EARLY_NODES], BF16)

        def adj_part(first_slot, end_slot, first, end):
            if first_slot < EARLY:
                return adj_top[:, first_slot:end_slot, first:end]
            return adj_low[
                :, first_slot - EARLY : end_slot - EARLY, first - EARLY_NODES : end - EARLY_NODES
            ]

        def adj_row(slot, first, end):
            return adj_part(slot, slot + 1, first, end)[:, 0, :]

        adj_view = adj.rearrange("(g q e) n -> q g e n", q=P, e=2)

        def load_h(c):
            nc.sync.dma_start(
                out=h_rows[:, PACK * c : PACK * (c + 1), :].rearrange("q (u e) f -> q u e f", e=2),
                in_=h_view[:, 2 * c : 2 * (c + 1), :, :],
            )

        def load_adj(g):
            first = 0 if 2 * g < EARLY else EARLY_NODES
            nc.sync.dma_start(
                out=adj_part(2 * g, 2 * (g + 1), first, NODES), in_=adj_view[:, g, :, first:]
            )

        load_h(0)
        load_adj(0)
        load_h(1)
        load_adj(1)
        load_adj(2)
        load_adj(3)
        load_h(2)
        load_adj(4)
        load_adj(5)
        load_h(3)
        load_adj(6)
        load_adj(7)
        weight_raw = {}
        for name, weight in (("rw", rw), ("w", w)):
            raw = keep.tile([P, PACK, FEAT], BF16, name="raw_" + name)
            nc.sync.dma_start(
                out=raw[:].rearrange("q (u e) o -> q u e o", e=2),
                in_=weight.rearrange("(u q e) o -> q u e o", q=P, e=2),
            )
            weight_raw[name] = raw
        bias = keep.tile([P, FEAT], BF16)
        nc.sync.dma_start(out=bias[:], in_=b.partition_broadcast(P))

        hn_codes = keep.tile([P, CHUNKS, FEAT], U32, align_bytes=64)
        hn_scales = keep.tile([P, CHUNKS, FEAT], U8, align_bytes=64)
        hf_codes = keep.tile([P, NODES], U32, align_bytes=64)
        hf_scales = keep.tile([P, NODES], U8, align_bytes=64)
        turned_of = {}

        def copy_turned_words(g, grouped, place, turned):
            span = GROUP * PACK // 2
            words = grouped[:].bitcast(F32)[:, span * place : span * (place + 1)]
            if g < EARLY_GROUPS:
                nc.scalar.copy(
                    out=words.rearrange("q (e p u) -> q e p u", e=2, u=2),
                    in_=turned[:].rearrange("q (e u) p -> q e p u", u=2),
                )
            else:
                nc.scalar.copy(
                    out=words.rearrange("q (p e u) -> q p e u", e=2, u=2),
                    in_=turned[:].rearrange("q (e u) p -> q p e u", u=2),
                )

        hn_grouped_of = {}
        hf_grouped_of = {}

        def new_grouped(width):
            return stage.tile([P, width], BF16, align_bytes=64, tag="grouped", bufs=GROUPS + 1, name="grouped")

        def group_h_by_nodes(c, *engines, pieces=range(PACK)):
            if 0 in pieces:
                hn_grouped_of[c] = new_grouped(FEAT * PACK)
            grouped = hn_grouped_of[c]
            by_feature = grouped[:].rearrange(
                "q (u e b m t) -> q u b t m e", u=2, e=2, m=RUN // 2, t=PACK
            )
            blocks = P // RUN
            for k in pieces:
                u, part = divmod(k, 2)
                engines[k % len(engines)](
                    out=by_feature[:, u, blocks * part : blocks * (part + 1), :, :, :],
                    in_=h_rows[:, PACK * c : PACK * (c + 1), P * k : P * (k + 1)].rearrange(
                        "q t (b m e) -> q b t m e", m=RUN // 2, e=2
                    ),
                )

        def group_h_by_features(c):
            grouped = new_grouped(K_PASS * PACK)
            for g in range(2):
                turned = psum_turn.tile([P, PACK, P], F32, tag="turned")
                for e in range(2):
                    row_words = h_rows[:, PACK * c + 2 * g + e, :].bitcast(F32)
                    for u in range(2):
                        nc.tensor.transpose(
                            out=turned[:, 2 * e + u, :],
                            in_=row_words[:, P * u : P * (u + 1)],
                            identity=ident[:],
                        )
                copy_turned_words(2 * c + g, grouped, g, turned)
            hf_grouped_of[c] = grouped

        def quantise_h_by_nodes(c):
            quantise(nc, hn_grouped_of[c][:], hn_codes[:, c, :], hn_scales[:, c, :])

        def quantise_h_by_features(c):
            cols = slice(K_PASS * c, K_PASS * (c + 1))
            quantise(nc, hf_grouped_of[c][:], hf_codes[:, cols], hf_scales[:, cols])

        deg = keep.tile([P, ROW_TILES], F32)
        late_nodes = ROW_TILES - EARLY
        early_parts = psum_acc.tile([P, EARLY * EARLY + SUM_WIDTH - 1], F32, tag="both", bufs=2)
        late_parts = psum_acc.tile([P, ROW_TILES * late_nodes + SUM_WIDTH - 1], F32, tag="both", bufs=2)
        right_part = keep.tile([P, EARLY], F32)
        nnz_early_end = EARLY * EARLY + SUM_WIDTH - 1
        nnz_parts = psum_acc.tile(
            [P, nnz_early_end + ROW_TILES * late_nodes + SUM_WIDTH - 1], F32, tag="neighbours", bufs=2
        )
        row_counts = keep.tile([P, EARLY], F32)
        positive_of = {}

        def compare(g):
            slots = (2 * g, 2 * (g + 1))
            first = 0 if 2 * g < EARLY else EARLY_NODES
            end = EARLY_NODES if 2 * g < EARLY else NODES
            positive = new_grouped(2 * NODES)[:].rearrange("q (e n) -> q e n", e=2)
            positive_of[g] = positive
            nc.vector.tensor_scalar(
                out=positive[:, :, first:end],
                in0=adj_part(*slots, first, end),
                scalar1=0.0,
                scalar2=None,
                op0=ALU.is_gt,
            )

        def compare_right(g):
            positive = positive_of[g]
            end = EARLY_NODES
            for e in range(2):
                slot = 2 * g + e
                nc.vector.tensor_scalar(
                    out=positive[:, e, end:],
                    in0=adj_row(slot, end, NODES),
                    scalar1=0.0,
                    scalar2=None,
                    op0=ALU.is_gt,
                    op1=ALU.add,
                    accum_out=row_counts[:, slot : slot + 1],
                )

        def sum_at(parts, column):
            return parts[:, column : column + SUM_WIDTH]

        def parts_of_node(parts, nodes, rows):
            return parts[:, : rows * nodes].rearrange("p (k n) -> p n k", n=nodes)

        def sum_columns(group):
            for slot in (2 * group, 2 * group + 1):
                for s in range(0 if slot < EARLY else EARLY, ROW_TILES):
                    g, e = divmod(s, 2)
                    if s < EARLY:
                        out = sum_at(early_parts, EARLY * slot + s)
                    else:
                        out = sum_at(late_parts, late_nodes * slot + s - EARLY)
                    nc.tensor.matmul(
                        out=out,
                        lhsT=adj_row(slot, GROUP * g, GROUP * (g + 1))[:, e::2],
                        rhs=ones[:],
                        start=True,
                        stop=True,
                    )

        def count_columns(g):
            for slot in (2 * g, 2 * g + 1):
                row = positive_of[g][:, slot % 2, :]
                for s in range(0 if slot < EARLY else EARLY, ROW_TILES):
                    if s < EARLY:
                        u, e = divmod(s, 2)
                        out = sum_at(nnz_parts, EARLY * slot + s)
                        block = row[:, GROUP * u + e : GROUP * (u + 1) : 2]
                    else:
                        out = sum_at(nnz_parts, nnz_early_end + late_nodes * slot + s - EARLY)
                        block = row[:, P * s : P * (s + 1)]
                    nc.tensor.matmul(out=out, lhsT=block, rhs=ones[:], start=True, stop=True)

        dis_row = keep.tile([P, NODES], F32)
        spare = dis_row[:].bitcast(BF16).rearrange("p (k n) -> p k n", k=4)

        def sum_right_on_scalar(slot):
            nc.scalar.activation(
                out=spare[:, slot % 2, :],
                in_=adj_row(slot, EARLY_NODES, NODES),
                func=ACT.Copy,
                accum_out=right_part[:, slot : slot + 1],
            )

        def sum_right_on_vector(slot):
            nc.vector.tensor_scalar(
                out=spare[:, 2 + slot % 2, :],
                in0=adj_row(slot, EARLY_NODES, NODES),
                scalar1=1.0,
                scalar2=None,
                op0=ALU.mult,
                op1=ALU.add,
                accum_out=right_part[:, slot : slot + 1],
            )

        dis = keep.tile([P, ROW_TILES], F32)

        def sum_early_deg():
            nc.vector.tensor_reduce(
                out=deg[:, :EARLY], in_=parts_of_node(early_parts, EARLY, EARLY), axis=AXIS.X, op=ALU.add
            )

        def make_early_dis():
            nc.vector.tensor_add(out=deg[:, :EARLY], in0=deg[:, :EARLY], in1=right_part[:])
            nc.scalar.activation(out=dis[:, :EARLY], in_=deg[:, :EARLY], func=ACT.Abs_reciprocal_sqrt)

        def make_late_dis():
            nc.vector.tensor_reduce(
                out=deg[:, EARLY:], in_=parts_of_node(late_parts, late_nodes, ROW_TILES), axis=AXIS.X, op=ALU.add
            )
            nc.scalar.activation(out=dis[:, EARLY:], in_=deg[:, EARLY:], func=ACT.Abs_reciprocal_sqrt)

        spread_of = {}

        def spread_turn(c):
            if c < 2:
                spread = psum_turn.tile([P, K_PASS], F32, tag="turned", name="spread")
            elif c < 3:
                spread = psum_acc.tile([P, K_PASS], F32, tag="both", bufs=2, name="spread")
            else:
                spread = psum_acc.tile([P, K_PASS], F32, tag="neighbours", bufs=2, name="spread")
            spread_of[c] = spread
            for k in range(PACK):
                s = PACK * c + k
                u, e = divmod(k, 2)
                nc.tensor.transpose(
                    out=spread[:, GROUP * u + e : GROUP * (u + 1) : 2],
                    in_=dis[:, s : s + 1].to_broadcast([P, P]),
                    identity=ident[:],
                )

        def spread_copy(c):
            spread = spread_of[c]
            nc.scalar.copy(out=dis_row[:, K_PASS * c : K_PASS * (c + 1)], in_=spread[:])

        nnz = keep.tile([P, ROW_TILES], F32)
        inv_nnz = keep.tile([P, ROW_TILES], F32)

        def count_nnz():
            nc.vector.tensor_reduce(
                out=nnz[:, :EARLY], in_=parts_of_node(nnz_parts, EARLY, EARLY), axis=AXIS.X, op=ALU.add
            )
            nc.vector.tensor_reduce(
                out=nnz[:, EARLY:],
                in_=parts_of_node(nnz_parts[:, nnz_early_end:], late_nodes, ROW_TILES),
                axis=AXIS.X,
                op=ALU.add,
            )

        def add_row_counts():
            nc.vector.tensor_add(out=nnz[:, :EARLY], in0=nnz[:, :EARLY], in1=row_counts[:])

        def bound_nnz():
            nc.vector.tensor_scalar_max(out=nnz[:], in0=nnz[:], scalar1=1.0)

        def invert_nnz():
            nc.vector.reciprocal(out=inv_nnz[:], in_=nnz[:])

        weight_grouped = {}
        weight_codes = {}
        weight_scales = {}

        def group_weight(name, engine_copy, k):
            if k == 0:
                weight_grouped[name] = new_grouped(FEAT * PACK)
            grouped = weight_grouped[name]
            if True:
                cols = slice(P * k, P * (k + 1))
                engine_copy(
                    out=grouped[:, PACK * P * k : PACK * P * (k + 1)].rearrange(
                        "q (b o t) -> q b t o", o=RUN, t=PACK
                    ),
                    in_=weight_raw[name][:, :, cols].rearrange("q t (b o) -> q b t o", o=RUN),
                )

        def quantise_weight(name):
            grouped = weight_grouped[name]
            codes = keep.tile([P, FEAT], U32, align_bytes=64, name="codes_" + name)
            scales = keep.tile([P, FEAT], U8, align_bytes=64, name="scales_" + name)
            quantise(nc, grouped[:], codes[:], scales[:])
            weight_codes[name] = codes
            weight_scales[name] = scales

        grouped_of = {}
        norm_mx_of = {}
        agg_of = {}
        agg_grouped_of = {}
        agg_mx_of = {}
        both_of = {}

        def grouped_norm(g):
            if g not in grouped_of:
                grouped_of[g] = new_grouped(CHUNKS * GROUP * PACK)
            return grouped_of[g][:].rearrange("q (c i t) -> q c i t", c=CHUNKS, t=PACK)

        def scale_row(slot, first_chunk, last_chunk):
            first = K_PASS * first_chunk
            last = K_PASS * last_chunk
            nc.vector.scalar_tensor_tensor(
                out=adj_row(slot, first, last),
                in0=adj_row(slot, first, last),
                scalar=dis[:, slot : slot + 1],
                in1=dis_row[:, first:last],
                op0=ALU.mult,
                op1=ALU.mult,
            )

        def scale_row_early(slot, c):
            row = adj_row(slot, K_PASS * c, K_PASS * (c + 1))
            nc.vector.scalar_tensor_tensor(
                out=row,
                in0=row,
                scalar=dis[:, slot : slot + 1],
                in1=spread_of[c][:],
                op0=ALU.mult,
                op1=ALU.mult,
            )


        def turn_norm(g, first_chunk, last_chunk):
            grouped_norm(g)
            for c in range(first_chunk, last_chunk):
                turned = psum_turn.tile([P, PACK, P], F32, tag="turned")
                for e in range(2):
                    words = adj_row(2 * g + e, K_PASS * c, K_PASS * (c + 1)).bitcast(F32)
                    for u in range(2):
                        nc.tensor.transpose(
                            out=turned[:, 2 * e + u, :],
                            in_=words[:, P * u : P * (u + 1)],
                            identity=ident[:],
                        )
                turned_of[g, c] = turned

        def copy_turned(g, first_chunk, last_chunk):
            for c in range(first_chunk, last_chunk):
                copy_turned_words(g, grouped_of[g], c, turned_of[g, c])

        def mirror_norm(engine_copy, c, g):
            rows = adj_part(PACK * c, PACK * (c + 1), GROUP * g, GROUP * (g + 1))
            mirrored = grouped_norm(g)[:, c, :, :]
            if g < EARLY_GROUPS:
                engine_copy(
                    out=mirrored.rearrange("q (e b m) t -> q b t m e", e=2, m=RUN // 2),
                    in_=rows.rearrange("q t (b m e) -> q b t m e", m=RUN // 2, e=2),
                )
            else:
                engine_copy(
                    out=mirrored.rearrange("q (b i) t -> q b t i", i=RUN),
                    in_=rows.rearrange("q t (b i) -> q b t i", i=RUN),
                )

        def quantise_norm(g):
            codes = work.tile([P, CHUNKS, GROUP], U32, align_bytes=64, tag="norm_codes")
            scales = work.tile([P, CHUNKS, GROUP], U8, align_bytes=64, tag="norm_scales")
            quantise(
                nc,
                grouped_of[g][:],
                codes[:].rearrange("q c i -> q (c i)"),
                scales[:].rearrange("q c i -> q (c i)"),
            )
            norm_mx_of[g] = (codes, scales)

        neighbours_of = {}

        def sum_neighbours(g, halves=(0, 1)):
            codes, scales = norm_mx_of[g]
            for half in halves:
                tile = 2 * g + half
                cols = slice(P * half, P * (half + 1))
                neighbours = psum_acc.tile([P, FEAT], F32, tag="neighbours", bufs=2)
                for c in range(CHUNKS):
                    mx_pass(
                        nc,
                        neighbours[:],
                        codes[:, c, cols],
                        scales[:, c, cols],
                        hn_codes[:, c, :],
                        hn_scales[:, c, :],
                        start=(c == 0),
                        stop=(c == CHUNKS - 1),
                    )
                neighbours_of[tile] = neighbours

        def scale_agg(g, halves=(0, 1)):
            for half in halves:
                tile = 2 * g + half
                agg = work.tile([P, FEAT], BF16, tag="agg", bufs=6)
                nc.scalar.activation(
                    out=agg[:].rearrange("p (u m e) -> p u m e", u=2, e=2),
                    in_=neighbours_of[tile][:].rearrange("p (u e m) -> p u m e", u=2, e=2),
                    func=ACT.Copy,
                    scale=inv_nnz[:, tile : tile + 1],
                )
                agg_of[tile] = agg

        inv_row = keep.tile([P, GROUP], F32)

        def spread_inv_nnz():
            spread = psum_turn.tile([P, 2, P], F32, tag="turned", name="spread")
            for half in range(2):
                tile = 2 * PAIRED + half
                nc.tensor.transpose(
                    out=spread[:, half, :],
                    in_=inv_nnz[:, tile : tile + 1].to_broadcast([P, P]),
                    identity=ident[:],
                )
            nc.scalar.copy(out=inv_row[:], in_=spread[:].rearrange("p half i -> p (half i)"))

        def sum_neighbours_turned(half):
            codes, scales = norm_mx_of[PAIRED]
            cols = slice(P * half, P * (half + 1))
            sums = psum_acc.tile([P, PACK, P], F32, tag="neighbours", bufs=2, name="sums")
            neighbours_of[2 * PAIRED + half] = sums
            for t in range(PACK):
                window = slice(P * t, P * (t + 1))
                for c in range(CHUNKS):
                    mx_pass(
                        nc,
                        sums[:, t, :],
                        hn_codes[:, c, window],
                        hn_scales[:, c, window],
                        codes[:, c, cols],
                        scales[:, c, cols],
                        start=(c == 0),
                        stop=(c == CHUNKS - 1),
                    )

        def scale_turned(half):
            grouped = work.tile([P, GROUP * PACK], BF16, align_bytes=64, tag="agg_grouped")
            nc.vector.tensor_tensor(
                out=grouped[:, : P * PACK].rearrange("p (i t) -> p i t", t=PACK),
                in0=neighbours_of[2 * PAIRED + half][:].rearrange("p t i -> p i t"),
                in1=inv_row[:, P * half : P * (half + 1)].unsqueeze(2).to_broadcast([P, P, PACK]),
                op=ALU.mult,
            )
            agg_grouped_of[PAIRED, (half,)] = grouped

        def turn_agg(g, halves=(0, 1)):
            turned = psum_turn.tile([P, PACK, P], F32, tag="turned")
            for k, half in enumerate(halves):
                words = agg_of[2 * g + half][:].bitcast(F32)
                for u in range(2):
                    nc.tensor.transpose(
                        out=turned[:, 2 * k + u, :],
                        in_=words[:, P * u : P * (u + 1)],
                        identity=ident[:],
                    )
            turned_of["agg", g, halves] = turned

        def copy_turned_agg(g, halves=(0, 1)):
            turned = turned_of["agg", g, halves]
            tiles = len(halves)
            grouped = work.tile([P, GROUP * PACK], BF16, align_bytes=64, tag="agg_grouped")
            nc.scalar.copy(
                out=grouped[:].bitcast(F32)[:, : GROUP * tiles].rearrange(
                    "q (k i u) -> q k i u", k=tiles, u=2
                ),
                in_=turned[:, : 2 * tiles, :].rearrange("q (k u) i -> q k i u", u=2),
            )
            agg_grouped_of[g, halves] = grouped

        def quantise_agg(g, halves=(0, 1)):
            width = P * len(halves)
            codes = work.tile([P, GROUP], U32, align_bytes=64, tag="agg_codes")
            scales = work.tile([P, GROUP], U8, align_bytes=64, tag="agg_scales")
            quantise(
                nc,
                agg_grouped_of[g, halves][:, : PACK * width],
                codes[:, :width],
                scales[:, :width],
            )
            for k, half in enumerate(halves):
                cols = slice(P * k, P * (k + 1))
                agg_mx_of[2 * g + half] = (codes[:, cols], scales[:, cols])

        def combine(g, halves=(0, 1)):
            for half in halves:
                tile = 2 * g + half
                codes, scales = agg_mx_of[tile]
                nodes = slice(P * tile, P * (tile + 1))
                both = psum_acc.tile(
                    [P, FEAT], F32, tag="both" if g < PAIRED else "neighbours", bufs=2, name="both"
                )
                mx_pass(
                    nc,
                    both[:],
                    hf_codes[:, nodes],
                    hf_scales[:, nodes],
                    weight_codes["rw"][:],
                    weight_scales["rw"][:],
                    start=True,
                    stop=False,
                )
                mx_pass(
                    nc,
                    both[:],
                    codes,
                    scales,
                    weight_codes["w"][:],
                    weight_scales["w"][:],
                    start=False,
                    stop=True,
                )
                both_of[tile] = both

        def out_rows(tile):
            if tile < EARLY:
                return out.rearrange("(g p e) o -> g e p o", p=P, e=2)[tile // 2, tile % 2, :, :]
            return out[P * tile : P * (tile + 1), :]

        result_of = {}

        def add_bias(tile):
            result = work.tile([P, FEAT], F32, tag="result", bufs=6)
            nc.vector.tensor_tensor(out=result[:], in0=both_of[tile][:], in1=bias[:], op=ALU.add)
            result_of[tile] = result

        def rectify(tile):
            result = result_of[tile]
            nc.scalar.activation(out=result[:], in_=result[:], func=ACT.Relu)
            nc.sync.dma_start(out=out_rows(tile), in_=result[:])

        def rectify_on_vector(tile):
            result = result_of[tile]
            nc.vector.tensor_scalar_max(out=result[:], in0=result[:], scalar1=0.0)
            nc.sync.dma_start(out=out_rows(tile), in_=result[:])

        def finish_on_vector(tile):
            result = work.tile([P, FEAT], F32, tag="result", bufs=6)
            for k in range(2):
                cols = slice(FEAT // 2 * k, FEAT // 2 * (k + 1))
                nc.vector.tensor_tensor(
                    out=result[:, cols], in0=both_of[tile][:, cols], in1=bias[:, cols], op=ALU.add
                )
            for k in range(2):
                cols = slice(FEAT // 2 * k, FEAT // 2 * (k + 1))
                nc.vector.tensor_scalar_max(
                    out=result[:, cols], in0=result[:, cols], scalar1=0.0
                )
                nc.sync.dma_start(
                    out=out_rows(tile)[:, cols], in_=result[:, cols]
                )

        def in_range(g):
            return 0 <= g < GROUPS

        with tc.manual_schedule():
            group_h_by_nodes(0, nc.scalar.copy, nc.vector.tensor_copy, nc.vector.tensor_copy, nc.vector.tensor_copy)
            group_h_by_features(0)
            quantise_h_by_nodes(0)
            quantise_h_by_features(0)
            for slot in (0, 1):
                sum_right_on_scalar(slot)
            compare(0)
            compare_right(0)
            sum_columns(0)
            count_columns(0)
            group_h_by_nodes(1, nc.scalar.copy, nc.vector.tensor_copy, nc.vector.tensor_copy, nc.vector.tensor_copy)
            group_h_by_features(1)
            quantise_h_by_nodes(1)
            for slot in (2, 3):
                sum_right_on_scalar(slot)
            compare(1)
            compare_right(1)
            sum_columns(1)
            quantise_h_by_features(1)
            count_columns(1)
            for slot in (4, 5):
                sum_right_on_scalar(slot)
            compare(2)
            compare_right(2)
            sum_columns(2)
            count_columns(2)
            sum_right_on_scalar(6)
            sum_right_on_vector(7)
            sum_columns(3)
            compare(3)
            sum_early_deg()
            make_early_dis()
            compare_right(3)
            for c in (0, 1):
                spread_turn(c)
            group_h_by_nodes(2, nc.scalar.copy, pieces=(0,))
            spread_copy(1)
            count_columns(3)
            group_h_by_nodes(2, nc.scalar.copy, pieces=(1, 2, 3))
            group_h_by_features(2)
            for slot in range(PACK):
                scale_row_early(slot, 0)
            for slot in range(PACK):
                scale_row(slot, 1, 2)
            sum_columns(4)
            sum_columns(5)
            for g in (0, 1):
                turn_norm(g, 0, 1)
            sum_columns(6)
            copy_turned(0, 0, 1)
            turn_norm(0, 1, 2)
            sum_columns(7)
            make_late_dis()
            copy_turned(1, 0, 1)
            copy_turned(0, 1, 2)
            turn_norm(1, 1, 2)
            copy_turned(1, 1, 2)
            compare(4)
            compare(5)
            quantise_h_by_nodes(2)
            for c in range(2, CHUNKS):
                spread_turn(c)
                spread_copy(c)
            count_columns(4)
            compare(6)
            count_columns(5)
            compare(7)
            quantise_h_by_features(2)
            group_h_by_nodes(3, nc.scalar.copy)
            for chunk in (2, 3):
                for slot in (0, 1):
                    scale_row_early(slot, chunk)
                turn_norm(0, chunk, chunk + 1)
                count_columns(4 + chunk)
                copy_turned(0, chunk, chunk + 1)
            group_h_by_features(3)
            scale_row(2, 2, CHUNKS)
            quantise_h_by_nodes(3)
            count_nnz()
            quantise_norm(0)
            add_row_counts()
            scale_row(3, 2, CHUNKS)
            bound_nnz()
            sum_neighbours(0)
            turn_norm(1, 2, CHUNKS)
            for piece in range(PACK):
                group_weight("rw", nc.scalar.copy, piece)
            mirror_norm(nc.scalar.copy, 0, 2)
            copy_turned(1, 2, CHUNKS)
            scale_row(4, 1, CHUNKS)
            invert_nnz()
            quantise_h_by_features(3)
            scale_agg(0)
            for piece in range(PACK):
                group_weight("w", nc.scalar.copy, piece)
            spread_inv_nnz()
            scale_row(5, 1, CHUNKS)
            quantise_weight("rw")

            mirrors = [(c, g) for g in range(3, GROUPS) for c in range(g // 2)]

            def first_of(g):
                return max(g // 2, 1)

            for k in range(GROUPS - 2):
                turn_agg(k)
                copy_turned_agg(k)
                quantise_norm(k + 1)
                turn_norm(k + 2, first_of(k + 2), CHUNKS)
                copy_turned(k + 2, first_of(k + 2), CHUNKS)
                ready, mirrors = mirrors[:2], mirrors[2:]
                for engine_copy, (c, g) in zip((nc.vector.tensor_copy, nc.scalar.copy), ready):
                    mirror_norm(engine_copy, c, g)
                if k - 1 >= 0:
                    add_bias(2 * k - 2)
                    add_bias(2 * k - 1)
                if k + 3 < GROUPS:
                    scale_row(2 * k + 6, first_of(k + 3), CHUNKS)
                if k == 0:
                    quantise_weight("w")
                quantise_agg(k)
                if k + 3 < GROUPS:
                    scale_row(2 * k + 7, first_of(k + 3), CHUNKS)
                sum_neighbours(k + 1)
                scale_agg(k + 1)
                if k - 1 >= 0:
                    rectify(2 * k - 2)
                    rectify(2 * k - 1)
                combine(k)
            quantise_norm(PAIRED)
            add_bias(10)
            add_bias(11)
            turn_agg(6)
            copy_turned_agg(6)
            sum_neighbours_turned(0)
            sum_neighbours_turned(1)
            rectify(10)
            rectify(11)
            quantise_agg(6)
            scale_turned(0)
            combine(6)
            quantise_agg(7, (0,))
            scale_turned(1)
            add_bias(12)
            quantise_agg(7, (1,))
            add_bias(13)
            combine(7)
            rectify(12)
            rectify(13)
            add_bias(14)
            rectify_on_vector(14)
            finish_on_vector(15)
